import numpy as np
import ml_dtypes


def mxq(x, axis, fmt="e4m3"):
    dtype, down = {"e4m3": (ml_dtypes.float8_e4m3fn, 7), "e5m2": (ml_dtypes.float8_e5m2, 14)}[fmt]
    v = np.moveaxis(np.asarray(x, np.float32).astype(ml_dtypes.bfloat16).astype(np.float64), axis, -1)
    blocks = v.reshape(v.shape[:-1] + (-1, 32))
    amax = np.abs(blocks).max(-1, keepdims=True)
    byte = np.maximum(np.where(amax > 0, np.frexp(amax)[1] - 1 + 127, 0) - down, 1)
    scale = np.exp2(byte - 127.0)
    codes = (blocks / scale).astype(np.float32).astype(dtype).astype(np.float64)
    return np.moveaxis((codes * scale).reshape(v.shape), -1, axis)


WIDE = False


def mx_kscale(k):
    if not WIDE:
        return np.ones(k)
    levels = np.array([18, -18])
    if k % 512:
        return np.exp2(np.random.permutation(np.resize(levels, k // 32))).repeat(32)
    a = np.empty((k // 512, 16))
    for p in range(k // 512):
        a[p, :8] = np.random.permutation(np.resize(levels, 8))
        for g in range(8):
            far = levels[np.abs(levels - a[p, g]) >= 10]
            a[p, g + 8] = far[np.random.randint(len(far))]
    return np.exp2(a.ravel()).repeat(32)


BF16 = ml_dtypes.bfloat16


def bf(x):
    return np.asarray(x, np.float32).astype(BF16)


def f64(x):
    return np.asarray(x).astype(np.float64)


B, S, D, C = 1024, 4, 512, 1024
MIN_SCALE = 1e-3
TEMPERATURE = 1.5


def sigmoid(v):
    return 1.0 / (1.0 + np.exp(-v))


def setup_inputs():
    u = mx_kscale(C)
    v = mx_kscale(D)
    s = mx_kscale(B)
    features0 = bf(np.random.standard_normal((B, D)) * 0.3)
    W_diag0 = bf(np.random.standard_normal((D, D)) * 2.0 / np.sqrt(D))
    b_diag = bf(-4.0 + 0.2 * np.random.standard_normal(D))
    W_cls0 = bf(np.random.standard_normal((C, D)) * 3.0 / np.sqrt(D))
    b_cls = bf(np.random.standard_normal(C) * 0.3)
    noise0 = bf(np.random.standard_normal((B, S, D)) * 10.0)
    lr_samples = bf(np.random.standard_normal((B, S, D)) * 0.3)
    g = bf(np.random.standard_normal((B, S, C)) * np.exp2(np.random.randint(-6, 1, (B, S, 1))) / s[:, None, None] * u)
    z = f64(features0) @ f64(W_diag0).T + f64(b_diag)
    return {
        "features": bf(f64(features0) * s[:, None]),
        "W_diag": bf(f64(W_diag0) / v[:, None]),
        "b_diag": b_diag,
        "W_cls": bf(f64(W_cls0) / u[:, None]),
        "b_cls": b_cls,
        "noise_diag": bf(f64(noise0) * v),
        "lr_samples": lr_samples,
        "z": np.asarray(z, np.float32),
        "grad_out": g,
    }


def reference(features, W_diag, b_diag, W_cls, b_cls, noise_diag, lr_samples, z, grad_out):
    dlogits = (f64(grad_out) / TEMPERATURE).reshape(-1, C)
    dpre = mxq(dlogits, 1, "e5m2") @ mxq(f64(W_cls), 0, "e4m3")
    dpre = dpre.reshape(-1, S, D)
    dstd = np.sum(dpre * f64(noise_diag), axis=1)
    dz = dstd * sigmoid(f64(z))
    direct = np.sum(dpre, axis=1)
    dfeatures = (mxq(dz, 1, "e5m2") @ mxq(f64(W_diag), 0, "e4m3")) + direct
    dW_diag = mxq(dz, 0, "e5m2").T @ mxq(f64(features), 0, "e4m3")
    return dfeatures, dW_diag

@@ -1,0 +1,470 @@
+from contextlib import ExitStack
+
+import concourse.mybir as mybir
+from concourse.masks import make_identity
+
+F32 = mybir.dt.float32
+BF16 = mybir.dt.bfloat16
+U32 = mybir.dt.uint32
+U8 = mybir.dt.uint8
+E4M3 = mybir.dt.float8_e4m3fn_x4
+E5M2 = mybir.dt.float8_e5m2_x4
+MULT = mybir.AluOpType.mult
+ADD = mybir.AluOpType.add
+
+P = 128
+B, S, D, C = 1024, 4, 512, 1024
+TEMPERATURE = 1.5
+TILES = B // P
+FLOPS = 2 * (B * S * C * D + B * D * D + D * D * B)
+BYTES = 2 * (B * S * C + B * S * D + B * D + D * D + C * D) + 4 * (B * D) + 4 * (B * D + D * D)
+
+
+def tile_hetxlhead_pa_v_kernel(
+    tc, features, w_diag, b_diag, w_cls, b_cls, noise_diag, lr_samples, z, grad_out, out_0, out_1
+):
+    nc = tc.nc
+    g_view = grad_out.rearrange("(g p j) s c -> g j p s c", p=P, j=4)
+    n_view = noise_diag.rearrange("(g p j) s d -> g p j s d", p=P, j=4)
+    z_view = z.rearrange("(g p j) d -> g p j d", p=P, j=4)
+    o_view = out_0.rearrange("(g p j) d -> g j p d", p=P, j=4)
+
+    with ExitStack() as ctx:
+        pool = ctx.enter_context(tc.tile_pool(name="sbuf", bufs=1))
+        psum = ctx.enter_context(tc.psum_pool(name="psum", bufs=1))
+
+        def sb(tag, shape, dtype, bufs):
+            return pool.tile(shape, dtype, name=tag, tag=tag, bufs=bufs, align_bytes=64)
+
+        def ps(tag, shape, bufs):
+            return psum.tile(shape, F32, name=tag, tag=tag, bufs=bufs)
+
+        ident = sb("ident", [P, P], F32, 1)
+        make_identity(nc, ident[:])
+
+        SPLIT = (6, 7)
+        last = {}
+        raw, noise, zt, gs, trb, grp, cod, dpb = {}, {}, {}, {}, {}, {}, {}, {}
+        prod, part, dstd, sig, dz, dzt_b, dzt, dzc, outb = {}, {}, {}, {}, {}, {}, {}, {}, {}
+
+        def quantised(tag, cols, bufs):
+            return sb(tag + "_c", [P, cols], U32, bufs), sb(tag + "_s", [P, cols], U8, bufs)
+
+        def load_g(J, a=0, b=S):
+            if J % 2 == 0 and a == 0:
+                raw[J // 2] = sb("raw", [P, 2 * S * C], BF16, 3)
+            at = S * C * (J % 2)
+            nc.sync.dma_start(
+                out=raw[J // 2][:, at + C * a : at + C * b].rearrange("p (s c) -> p s c", c=C),
+                in_=g_view[J // 4, J % 4][:, a:b, :],
+            )
+
+        def load_n(J, count):
+            if J % 2 == 0:
+                noise[J // 2] = sb("noise", [P, 2, S, D], BF16, 3)
+            at = J % 2
+            nc.sync.dma_start(
+                out=noise[J // 2][:, at : at + count], in_=n_view[J // 4][:, J % 4 : J % 4 + count]
+            )
+
+        def load_z(J):
+            zt[J // 2] = sb("z", [P, 2, D], F32, 3)
+            nc.sync.dma_start(out=zt[J // 2][:], in_=z_view[J // 4][:, J % 4 : J % 4 + 2])
+
+        def load_w(src):
+            t = sb("wraw", [P, 4, D], BF16, 3)
+            nc.sync.dma_start(out=t[:], in_=src.rearrange("(p j) w -> p j w", j=4))
+            return t
+
+        def rows(J, a, b):
+            at = S * C * (J % 2)
+            return raw[J // 2][:, at + C * a : at + C * b]
+
+        def prescale(J, hf, a=0, b=2):
+            if a == 0:
+                gs[J, hf] = sb("gs", [P, 2, 512, 2], BF16, 4)
+            nc.vector.tensor_scalar(
+                out=gs[J, hf][:, :, 256 * a : 256 * b, :],
+                in0=rows(J, 2 * hf + a, 2 * hf + b).rearrange("p (q u e) -> p u q e", u=2, e=2),
+                scalar1=1.0 / TEMPERATURE,
+                scalar2=None,
+                op0=MULT,
+            )
+
+        def scalar_prescale(J, hf):
+            gs[J, hf] = sb("gs", [P, 2, 512, 2], BF16, 4)
+            nc.scalar.activation(
+                gs[J, hf][:], rows(J, 2 * hf, 2 * hf + 2).rearrange("p (q u e) -> p u q e", u=2, e=2),
+                mybir.ActivationFunctionType.Copy, scale=1.0 / TEMPERATURE,
+            )
+
+        def turn(J, s):
+            trb[J, s] = ps("tr", [P, 2, 2, P], 4)
+            words = gs[J, s // 2][:].rearrange("p u q e -> p (u q e)").bitcast(F32)
+            for h in range(2):
+                for u in range(2):
+                    a = u * 512 + (s % 2) * 256 + h * 128
+                    nc.tensor.transpose(trb[J, s][:, h, u, :], words[:, a : a + 128], ident[:])
+
+        def empty_turn(J, s):
+            hf = s // 2
+            if s % 2 == 0:
+                grp[J, hf] = sb("grp", [P, 2, 2, P, 2], F32, 3)
+            nc.scalar.copy(out=grp[J, hf][:, s % 2], in_=trb[J, s][:].rearrange("p h u r -> p h r u"))
+
+        def quant_g(J, hf, a=0, b=2):
+            if a == 0:
+                cod[J, hf] = quantised("g", 512, 8)
+            cols = slice(256 * a, 256 * b)
+            nc.vector.quantize_mx(
+                out=cod[J, hf][0][:, cols].bitcast(E5M2),
+                scales=cod[J, hf][1][:, cols],
+                in_=grp[J, hf][:, a:b].rearrange("p s h r u -> p (s h r u)").bitcast(BF16),
+            )
+
+        def g_pass(out, J, s, h, start, stop):
+            codes, scales = cod[J, s // 2]
+            cols = slice(((s % 2) * 2 + h) * P, ((s % 2) * 2 + h + 1) * P)
+            nc.tensor.matmul_mx(
+                out=out, lhsT=codes[:, cols].bitcast(E5M2), lhsT_scale=scales[:, cols],
+                rhs=wc[h][0][:].bitcast(E4M3), rhs_scale=wc[h][1][:], start=start, stop=stop,
+            )
+
+        def dpre(J, s):
+            dpb[J, s] = ps("dp", [P, D], 3)
+            for h in range(2):
+                g_pass(dpb[J, s][:], J, s, h, h == 0, h == 1)
+
+        def direct(J, s):
+            if s == 3 and J in SPLIT:
+                return
+            if s == 0:
+                outb[J] = ps("out", [P, D], 1) if J < TILES - 2 else ps("tr", [P, D], 4)
+            for h in range(2):
+                g_pass(outb[J][:], J, s, h, s == 0 and h == 0, False)
+
+        def times_noise(J, s):
+            hf = s // 2
+            if s % 2 == 0:
+                prod[J, hf] = sb("prod", [P, 2, D], F32, 4)
+            nc.vector.tensor_tensor(
+                out=prod[J, hf][:, s % 2, :], in0=dpb[J, s][:], in1=noise[J // 2][:, J % 2, s, :], op=MULT
+            )
+
+        def add_pair(J, hf):
+            part[J, hf] = sb("part", [P, D], F32, 3)
+            nc.vector.tensor_tensor(
+                out=part[J, hf][:], in0=prod[J, hf][:, 0, :], in1=prod[J, hf][:, 1, :], op=ADD
+            )
+
+        def add_all(J, eng):
+            dstd[J] = sb("dstd", [P, D], F32, 2)
+            eng.tensor_tensor(out=dstd[J][:], in0=part[J, 0][:], in1=part[J, 1][:], op=ADD)
+
+        def sigmoid(J):
+            sig[J] = sb("sig", [P, D], F32, 3)
+            nc.scalar.activation(sig[J][:], zt[J // 2][:, J % 2, :], mybir.ActivationFunctionType.Sigmoid)
+
+        def make_dz(J, cols, eng):
+            if J % 4 == 0 and cols.start == 0:
+                dz[J // 4] = sb("dz", [P, 4, D], BF16, 2)
+            eng.tensor_tensor(
+                out=dz[J // 4][:, J % 4, cols], in0=dstd[J][:, cols], in1=sig[J][:, cols], op=MULT
+            )
+
+        def turn_dz(J):
+            dzt_b[J] = ps("dp", [P, 2, P], 3)
+            words = dz[J // 4][:, J % 4, :].bitcast(F32)
+            for u in range(2):
+                nc.tensor.transpose(dzt_b[J][:, u, :], words[:, u : 256 : 2], ident[:])
+
+        def empty_dz(J):
+            dzt[J] = sb("dzt", [P, P, 2], F32, 2)
+            nc.scalar.copy(out=dzt[J][:], in_=dzt_b[J][:].rearrange("p u r -> p r u"))
+
+        def quant_dz(J):
+            dzc[J] = quantised("dzt", P, 2)
+            nc.vector.quantize_mx(
+                out=dzc[J][0][:].bitcast(E5M2), scales=dzc[J][1][:],
+                in_=dzt[J][:].rearrange("p r u -> p (r u)").bitcast(BF16),
+            )
+
+        def dz_pass(J):
+            nc.tensor.matmul_mx(
+                out=outb[J][:], lhsT=dzc[J][0][:].bitcast(E5M2), lhsT_scale=dzc[J][1][:],
+                rhs=wd[0][:].bitcast(E4M3), rhs_scale=wd[1][:], start=False, stop=True,
+            )
+
+        def keep_last(J):
+            if J in SPLIT:
+                last[J] = sb("last", [P, D], F32, 2)
+                nc.scalar.copy(out=last[J][:], in_=dpb[J, 3][:])
+
+        def store_out(J):
+            res = sb("res", [P, D], F32, 3)
+            if J in SPLIT:
+                nc.vector.tensor_tensor(out=res[:], in0=outb[J][:], in1=last[J][:], op=ADD)
+            else:
+                nc.scalar.copy(out=res[:], in_=outb[J][:])
+            nc.sync.dma_start(out=o_view[J // 4, J % 4], in_=res[:])
+
+        def interleave(eng_copy, dst, src, cols):
+            eng_copy(out=dst[:, cols, :], in_=src[:, :, cols].rearrange("p j w -> p w j"))
+
+        def quant_w(pair, t, fmt, cols=slice(0, D)):
+            nc.vector.quantize_mx(
+                out=pair[0][:, cols].bitcast(fmt), scales=pair[1][:, cols],
+                in_=t[:, cols, :].rearrange("p w j -> p (w j)"),
+            )
+
+        def grouped_w():
+            return sb("wg", [P, D, 4], BF16, 2)
+
+        def weight_pass(m, g):
+            cols = slice(m * P, (m + 1) * P)
+            nc.tensor.matmul_mx(
+                out=acc[m][:], lhsT=dzq[g][0][:, cols].bitcast(E5M2), lhsT_scale=dzq[g][1][:, cols],
+                rhs=ft[g][0][:].bitcast(E4M3), rhs_scale=ft[g][1][:], start=g == 0, stop=g == 1,
+            )
+
+        full = slice(0, D)
+        left, right = slice(0, D // 2), slice(D // 2, D)
+        ctx.enter_context(tc.manual_schedule())
+
+        dummy = sb("dummy", [P, 1], F32, 1)
+        nc.vector.memset(dummy[:], 0.0)
+        nc.scalar.activation(dummy[:], dummy[:], mybir.ActivationFunctionType.Sigmoid)
+
+        wc_raw = [load_w(w_cls[0:512, :]), load_w(w_cls[512:1024, :])]
+        load_g(0, 0, 1)
+        load_g(0, 1, 2)
+        load_g(0, 2, 4)
+        load_n(0, 1)
+        load_g(1, 0, 2)
+        load_g(1, 2, 4)
+        load_g(2)
+        load_n(1, 1)
+        load_z(0)
+        load_g(3)
+        wd_raw = load_w(w_diag)
+        load_n(2, 2)
+        load_g(4)
+        load_z(2)
+        load_g(5)
+
+        wc = [quantised("wc0", D, 1), quantised("wc1", D, 1)]
+        wd = quantised("wd", D, 1)
+        ft = [quantised("ft0", D, 1), quantised("ft1", D, 1)]
+        dzq = [quantised("dz0", D, 1), quantised("dz1", D, 1)]
+
+        wg = [grouped_w(), grouped_w()]
+        for h in range(2):
+            interleave(nc.vector.tensor_copy, wg[h], wc_raw[h], left)
+            interleave(nc.scalar.copy, wg[h], wc_raw[h], right)
+        prescale(0, 0, 0, 1)
+        turn(0, 0)
+        empty_turn(0, 0)
+        quant_w(wc[0], wg[0], E4M3)
+        prescale(0, 0, 1, 2)
+        turn(0, 1)
+        quant_w(wc[1], wg[1], E4M3)
+        quant_g(0, 0, 0, 1)
+        empty_turn(0, 1)
+        prescale(0, 1)
+        dpre(0, 0)
+        turn(0, 2)
+        turn(0, 3)
+        quant_g(0, 0, 1, 2)
+        empty_turn(0, 2)
+        empty_turn(0, 3)
+        dpre(0, 1)
+        times_noise(0, 0)
+        prescale(1, 0)
+        turn(1, 0)
+        turn(1, 1)
+        times_noise(0, 1)
+        quant_g(0, 1)
+        empty_turn(1, 0)
+        empty_turn(1, 1)
+        dpre(0, 2)
+        dpre(0, 3)
+        prescale(1, 1)
+        add_pair(0, 0)
+        turn(1, 2)
+        turn(1, 3)
+        times_noise(0, 2)
+        times_noise(0, 3)
+        empty_turn(1, 2)
+        empty_turn(1, 3)
+        sigmoid(0)
+        quant_g(1, 0)
+        direct(0, 0)
+        direct(0, 1)
+        prescale(2, 0)
+        dpre(1, 0)
+        turn(2, 0)
+        turn(2, 1)
+        prescale(2, 1)
+        empty_turn(2, 0)
+        empty_turn(2, 1)
+        quant_g(1, 1)
+        add_pair(0, 1)
+        add_all(0, nc.vector)
+
+        ft_raw = [load_w(features[0:512, :])]
+        load_n(4, 2)
+        load_g(6)
+        load_z(4)
+        ft_raw.append(load_w(features[512:1024, :]))
+        load_g(7)
+        load_n(6, 2)
+        load_z(6)
+
+        L = TILES - 1
+        acc = []
+        EARLY = ()
+        SIDE = {3: "f0", 4: "f1", 5: "dz"}
+        make_dz(0, full, nc.gpsimd)
+        dpre(1, 1)
+        times_noise(1, 0)
+        times_noise(1, 1)
+        dpre(1, 2)
+        times_noise(1, 2)
+        dpre(1, 3)
+        times_noise(1, 3)
+        direct(0, 2)
+        direct(0, 3)
+        turn(2, 2)
+        turn(2, 3)
+        turn_dz(0)
+        empty_turn(2, 2)
+        empty_turn(2, 3)
+        side = grouped_w()
+        interleave(nc.scalar.copy, side, wd_raw, right)
+        empty_dz(0)
+        prescale(3, 0)
+        quant_g(2, 0)
+        prescale(3, 1)
+        sigmoid(1)
+        add_pair(1, 0)
+        quant_g(2, 1)
+        for s in range(S):
+            turn(3, s)
+        add_pair(1, 1)
+        interleave(nc.vector.tensor_copy, side, wd_raw, left)
+        quant_dz(0)
+        quant_w(wd, side, E4M3)
+        add_all(1, nc.vector)
+
+        for J in range(2, TILES):
+            nxt = J < L
+            if nxt:
+                empty_turn(J + 1, 0)
+                empty_turn(J + 1, 1)
+            dpre(J, 0)
+            times_noise(J, 0)
+            make_dz(J - 1, full, nc.gpsimd)
+            dpre(J, 1)
+            times_noise(J, 1)
+            if J < L:
+                dz_pass(J - 2)
+                store_out(J - 2)
+            if nxt:
+                empty_turn(J + 1, 2)
+                empty_turn(J + 1, 3)
+            sigmoid(J)
+            if J in EARLY:
+                scalar_prescale(J + 3, 1)
+            dpre(J, 2)
+            times_noise(J, 2)
+            if J == L:
+                direct(J - 1, 0)
+                direct(J - 1, 1)
+            dpre(J, 3)
+            if J == L:
+                quant_dz(J - 2)
+                dz_pass(J - 2)
+                store_out(J - 2)
+                add_pair(J, 0)
+            times_noise(J, 3)
+            keep_last(J)
+            for s in range(2 if J == L else 0, S):
+                direct(J - 1, s)
+            if J + 2 < TILES:
+                prescale(J + 2, 0)
+                if J - 1 not in EARLY:
+                    prescale(J + 2, 1)
+            if J - 1 in SIDE:
+                quant_w(pair, side, E5M2 if SIDE[J - 1] == "dz" else E4M3)
+            if nxt:
+                quant_g(J + 1, 0)
+                add_pair(J, 0)
+                quant_g(J + 1, 1)
+            turn_dz(J - 1)
+            if J + 2 < TILES:
+                for s in range(S):
+                    turn(J + 2, s)
+            if J == L:
+                break
+            if J in SIDE:
+                src = {"f0": ft_raw[0], "f1": ft_raw[1], "dz": dz[0]}[SIDE[J]]
+                pair = {"f0": ft[0], "f1": ft[1], "dz": dzq[0]}[SIDE[J]]
+                side = grouped_w()
+                interleave(nc.scalar.copy, side, src, left)
+                empty_dz(J - 1)
+                interleave(nc.scalar.copy, side, src, right)
+                add_pair(J, 1)
+                quant_dz(J - 1)
+            else:
+                empty_dz(J - 1)
+                add_pair(J, 1)
+                if J < L - 1:
+                    quant_dz(J - 1)
+            add_all(J, nc.vector)
+            if J == L - 1:
+                acc = [ps("tr", [P, D], 4), ps("tr", [P, D], 4)]
+                weight_pass(0, 0)
+                weight_pass(1, 0)
+
+        part[L, 1] = sb("part", [P, D], F32, 3)
+        nc.vector.tensor_tensor(out=part[L, 1][:], in0=part[L, 0][:], in1=prod[L, 1][:, 0, :], op=ADD)
+        empty_dz(L - 1)
+        for s in range(S):
+            direct(L, s)
+        dstd[L] = sb("dstd", [P, D], F32, 2)
+        for cols in (left, right):
+            nc.vector.tensor_tensor(
+                out=dstd[L][:, cols], in0=part[L, 1][:, cols], in1=prod[L, 1][:, 1, cols], op=ADD
+            )
+        for cols in (left, right):
+            make_dz(L, cols, nc.vector)
+        acc += [ps("dp", [P, D], 3), ps("dp", [P, D], 3)]
+        turn_dz(L)
+        weight_pass(2, 0)
+        weight_pass(3, 0)
+        t = grouped_w()
+        quarter = [slice(m * P, (m + 1) * P) for m in range(4)]
+        interleave(nc.vector.tensor_copy, t, dz[1], quarter[0])
+        interleave(nc.scalar.copy, t, dz[1], quarter[1])
+        quant_dz(L - 1)
+        dz_pass(L - 1)
+        interleave(nc.vector.tensor_copy, t, dz[1], quarter[2])
+        quant_w(dzq[1], t, E5M2, quarter[0])
+        interleave(nc.vector.tensor_copy, t, dz[1], quarter[3])
+        quant_w(dzq[1], t, E5M2, quarter[1])
+        empty_dz(L)
+        quant_w(dzq[1], t, E5M2, quarter[2])
+        quant_w(dzq[1], t, E5M2, quarter[3])
+        quant_dz(L)
+        for m in range(4):
+            weight_pass(m, 1)
+        dz_pass(L)
+        store_out(L - 1)
+        for m in range(4):
+            r = sb("res1", [P, D], F32, 4)
+            if m == 0:
+                nc.vector.tensor_copy(out=r[:], in_=acc[m][:])
+            else:
+                nc.scalar.copy(out=r[:], in_=acc[m][:])
+            nc.sync.dma_start(out=out_1[m * P : (m + 1) * P, :], in_=r[:])
+        store_out(L)

@@ -16,6 +16,9 @@ P = 128
 B, S, D, C = 1024, 4, 512, 1024
 TEMPERATURE = 1.5
 TILES = B // P
+LAST = TILES - 1
+KEPT = 1
+SPLIT = (7,)
 FLOPS = 2 * (B * S * C * D + B * D * D + D * D * B)
 BYTES = 2 * (B * S * C + B * S * D + B * D + D * D + C * D) + 4 * (B * D) + 4 * (B * D + D * D)
 
@@ -25,7 +28,7 @@ def tile_hetxlhead_pa_v_kernel(
 ):
     nc = tc.nc
     g_view = grad_out.rearrange("(g p j) s c -> g j p s c", p=P, j=4)
-    n_view = noise_diag.rearrange("(g p j) s d -> g p j s d", p=P, j=4)
+    n_view = noise_diag.rearrange("(g p j) s d -> g j p s d", p=P, j=4)
     z_view = z.rearrange("(g p j) d -> g p j d", p=P, j=4)
     o_view = out_0.rearrange("(g p j) d -> g j p d", p=P, j=4)
 
@@ -36,144 +39,145 @@ def tile_hetxlhead_pa_v_kernel(
         def sb(tag, shape, dtype, bufs):
             return pool.tile(shape, dtype, name=tag, tag=tag, bufs=bufs, align_bytes=64)
 
-        def ps(tag, shape, bufs):
-            return psum.tile(shape, F32, name=tag, tag=tag, bufs=bufs)
+        def ps(tag, shape):
+            return psum.tile(shape, F32, name=tag, tag=tag, bufs={"tr": 2, "dp": 4, "out": 2}[tag])
 
         ident = sb("ident", [P, P], F32, 1)
         make_identity(nc, ident[:])
 
-        SPLIT = (6, 7)
-        last = {}
+        kept = {}
         raw, noise, zt, gs, trb, grp, cod, dpb = {}, {}, {}, {}, {}, {}, {}, {}
-        prod, part, dstd, sig, dz, dzt_b, dzt, dzc, outb = {}, {}, {}, {}, {}, {}, {}, {}, {}
+        prod, part, dstd, sig, dz, dzt_b, dzt, dzc, outb, res = {}, {}, {}, {}, {}, {}, {}, {}, {}, {}
 
         def quantised(tag, cols, bufs):
             return sb(tag + "_c", [P, cols], U32, bufs), sb(tag + "_s", [P, cols], U8, bufs)
 
         def load_g(J, a=0, b=S):
-            if J % 2 == 0 and a == 0:
-                raw[J // 2] = sb("raw", [P, 2 * S * C], BF16, 3)
-            at = S * C * (J % 2)
-            nc.sync.dma_start(
-                out=raw[J // 2][:, at + C * a : at + C * b].rearrange("p (s c) -> p s c", c=C),
-                in_=g_view[J // 4, J % 4][:, a:b, :],
-            )
+            if b - a == S:
+                t = sb("raw", [P, S * C], BF16, 3)
+            else:
+                t = sb("raw_part", [P, (b - a) * C], BF16, 5)
+            nc.sync.dma_start(out=t[:].rearrange("p (s c) -> p s c", c=C), in_=g_view[J // 4, J % 4][:, a:b, :])
+            for s in range(a, b):
+                raw[J, s] = (t, s - a)
 
-        def load_n(J, count):
-            if J % 2 == 0:
-                noise[J // 2] = sb("noise", [P, 2, S, D], BF16, 3)
-            at = J % 2
-            nc.sync.dma_start(
-                out=noise[J // 2][:, at : at + count], in_=n_view[J // 4][:, J % 4 : J % 4 + count]
-            )
+        def load_n(J, a=0, b=S):
+            if b - a == S:
+                t = sb("noise", [P, S, D], BF16, 4)
+            else:
+                t = sb("noise%d_%d" % (J, a), [P, b - a, D], BF16, 1)
+            nc.sync.dma_start(out=t[:], in_=n_view[J // 4, J % 4][:, a:b, :])
+            for s in range(a, b):
+                noise[J, s] = t[:, s - a, :]
 
-        def load_z(J):
-            zt[J // 2] = sb("z", [P, 2, D], F32, 3)
-            nc.sync.dma_start(out=zt[J // 2][:], in_=z_view[J // 4][:, J % 4 : J % 4 + 2])
+        def load_z(J, count):
+            t = sb("z", [P, count, D], F32, 3)
+            nc.sync.dma_start(out=t[:], in_=z_view[J // 4][:, J % 4 : J % 4 + count])
+            for k in range(count):
+                zt[J + k] = t[:, k, :]
 
         def load_w(src):
             t = sb("wraw", [P, 4, D], BF16, 3)
             nc.sync.dma_start(out=t[:], in_=src.rearrange("(p j) w -> p j w", j=4))
             return t
 
-        def rows(J, a, b):
-            at = S * C * (J % 2)
-            return raw[J // 2][:, at + C * a : at + C * b]
+        def scale_views(J, a, b):
+            t = sb("gs", [P, 2, 256 * (b - a), 2], BF16, 4)
+            for s in range(a, b):
+                gs[J, s] = (t, s - a, b - a)
+            src, at = raw[J, a]
+            return t[:], src[:, C * at : C * (at + b - a)].rearrange("p (q u e) -> p u q e", u=2, e=2)
 
-        def prescale(J, hf, a=0, b=2):
-            if a == 0:
-                gs[J, hf] = sb("gs", [P, 2, 512, 2], BF16, 4)
-            nc.vector.tensor_scalar(
-                out=gs[J, hf][:, :, 256 * a : 256 * b, :],
-                in0=rows(J, 2 * hf + a, 2 * hf + b).rearrange("p (q u e) -> p u q e", u=2, e=2),
-                scalar1=1.0 / TEMPERATURE,
-                scalar2=None,
-                op0=MULT,
-            )
+        def prescale(J, a, b):
+            dst, src = scale_views(J, a, b)
+            nc.vector.tensor_scalar(out=dst, in0=src, scalar1=1.0 / TEMPERATURE, scalar2=None, op0=MULT)
 
-        def scalar_prescale(J, hf):
-            gs[J, hf] = sb("gs", [P, 2, 512, 2], BF16, 4)
-            nc.scalar.activation(
-                gs[J, hf][:], rows(J, 2 * hf, 2 * hf + 2).rearrange("p (q u e) -> p u q e", u=2, e=2),
-                mybir.ActivationFunctionType.Copy, scale=1.0 / TEMPERATURE,
-            )
+        def scalar_prescale(J, a, b):
+            dst, src = scale_views(J, a, b)
+            nc.scalar.activation(dst, src, mybir.ActivationFunctionType.Copy, scale=1.0 / TEMPERATURE)
 
         def turn(J, s):
-            trb[J, s] = ps("tr", [P, 2, 2, P], 4)
-            words = gs[J, s // 2][:].rearrange("p u q e -> p (u q e)").bitcast(F32)
+            trb[J, s] = ps("tr", [P, 2, 2, P])
+            t, at, count = gs[J, s]
+            words = t[:].rearrange("p u q e -> p (u q e)").bitcast(F32)
             for h in range(2):
                 for u in range(2):
-                    a = u * 512 + (s % 2) * 256 + h * 128
-                    nc.tensor.transpose(trb[J, s][:, h, u, :], words[:, a : a + 128], ident[:])
+                    a = u * 256 * count + at * 256 + h * P
+                    nc.tensor.transpose(trb[J, s][:, h, u, :], words[:, a : a + P], ident[:])
 
-        def empty_turn(J, s):
-            hf = s // 2
-            if s % 2 == 0:
-                grp[J, hf] = sb("grp", [P, 2, 2, P, 2], F32, 3)
-            nc.scalar.copy(out=grp[J, hf][:, s % 2], in_=trb[J, s][:].rearrange("p h u r -> p h r u"))
+        def empty_turn(J, s, count=2):
+            at = s % count
+            if at == 0:
+                t = sb("grp", [P, count, 2, P, 2], F32, 3)
+                for k in range(count):
+                    grp[J, s + k] = t
+            nc.scalar.copy(out=grp[J, s][:, at], in_=trb[J, s][:].rearrange("p h u r -> p h r u"))
 
-        def quant_g(J, hf, a=0, b=2):
-            if a == 0:
-                cod[J, hf] = quantised("g", 512, 8)
-            cols = slice(256 * a, 256 * b)
+        def quant_g(J, a, b):
+            codes, scales = quantised("g", 256 * (b - a), 7)
             nc.vector.quantize_mx(
-                out=cod[J, hf][0][:, cols].bitcast(E5M2),
-                scales=cod[J, hf][1][:, cols],
-                in_=grp[J, hf][:, a:b].rearrange("p s h r u -> p (s h r u)").bitcast(BF16),
+                out=codes[:].bitcast(E5M2), scales=scales[:],
+                in_=grp[J, a][:].rearrange("p s h r u -> p (s h r u)").bitcast(BF16),
             )
+            for s in range(a, b):
+                cod[J, s] = (codes, scales, s - a)
 
         def g_pass(out, J, s, h, start, stop):
-            codes, scales = cod[J, s // 2]
-            cols = slice(((s % 2) * 2 + h) * P, ((s % 2) * 2 + h + 1) * P)
+            codes, scales, at = cod[J, s]
+            cols = slice((at * 2 + h) * P, (at * 2 + h + 1) * P)
             nc.tensor.matmul_mx(
                 out=out, lhsT=codes[:, cols].bitcast(E5M2), lhsT_scale=scales[:, cols],
                 rhs=wc[h][0][:].bitcast(E4M3), rhs_scale=wc[h][1][:], start=start, stop=stop,
             )
 
         def dpre(J, s):
-            dpb[J, s] = ps("dp", [P, D], 3)
+            dpb[J, s] = ps("dp", [P, D])
             for h in range(2):
                 g_pass(dpb[J, s][:], J, s, h, h == 0, h == 1)
 
-        def direct(J, s):
-            if s == 3 and J in SPLIT:
-                return
+        def direct(J, a=0, b=S, tag="out"):
+            if a == 0:
+                outb[J] = ps(tag, [P, D])
+            for s in range(a, b):
+                if s == KEPT and J in SPLIT:
+                    continue
+                for h in range(2):
+                    g_pass(outb[J][:], J, s, h, s == 0 and h == 0, False)
+
+        def keep_dpre(J):
+            if J in SPLIT:
+                kept[J] = sb("kept", [P, D], F32, 4)
+                nc.scalar.copy(out=kept[J][:], in_=dpb[J, KEPT][:])
+
+        def times_noise(J, s, cols=slice(0, D)):
             if s == 0:
-                outb[J] = ps("out", [P, D], 1) if J < TILES - 2 else ps("tr", [P, D], 4)
-            for h in range(2):
-                g_pass(outb[J][:], J, s, h, s == 0 and h == 0, False)
-
-        def times_noise(J, s):
-            hf = s // 2
-            if s % 2 == 0:
-                prod[J, hf] = sb("prod", [P, 2, D], F32, 4)
+                prod[J] = sb("prod", [P, 2, 2, D], F32, 2)
             nc.vector.tensor_tensor(
-                out=prod[J, hf][:, s % 2, :], in0=dpb[J, s][:], in1=noise[J // 2][:, J % 2, s, :], op=MULT
+                out=prod[J][:, s % 2, s // 2, cols], in0=dpb[J, s][:, cols], in1=noise[J, s][:, cols], op=MULT
             )
 
-        def add_pair(J, hf):
-            part[J, hf] = sb("part", [P, D], F32, 3)
-            nc.vector.tensor_tensor(
-                out=part[J, hf][:], in0=prod[J, hf][:, 0, :], in1=prod[J, hf][:, 1, :], op=ADD
-            )
+        def add_pairs(J):
+            part[J] = sb("part", [P, 2, D], F32, 2)
+            nc.vector.tensor_tensor(out=part[J][:], in0=prod[J][:, 0], in1=prod[J][:, 1], op=ADD)
 
-        def add_all(J, eng):
-            dstd[J] = sb("dstd", [P, D], F32, 2)
-            eng.tensor_tensor(out=dstd[J][:], in0=part[J, 0][:], in1=part[J, 1][:], op=ADD)
+        def add_all(J, eng, cols=slice(0, D)):
+            if cols.start == 0:
+                dstd[J] = sb("dstd", [P, D], F32, 2)
+            eng.tensor_tensor(out=dstd[J][:, cols], in0=part[J][:, 0, cols], in1=part[J][:, 1, cols], op=ADD)
 
         def sigmoid(J):
             sig[J] = sb("sig", [P, D], F32, 3)
-            nc.scalar.activation(sig[J][:], zt[J // 2][:, J % 2, :], mybir.ActivationFunctionType.Sigmoid)
+            nc.scalar.activation(sig[J][:], zt[J], mybir.ActivationFunctionType.Sigmoid)
 
-        def make_dz(J, cols, eng):
+        def make_dz(J, eng, cols=slice(0, D)):
             if J % 4 == 0 and cols.start == 0:
                 dz[J // 4] = sb("dz", [P, 4, D], BF16, 2)
             eng.tensor_tensor(
                 out=dz[J // 4][:, J % 4, cols], in0=dstd[J][:, cols], in1=sig[J][:, cols], op=MULT
             )
 
-        def turn_dz(J):
-            dzt_b[J] = ps("dp", [P, 2, P], 3)
+        def turn_dz(J, tag="dp"):
+            dzt_b[J] = ps(tag, [P, 2, P])
             words = dz[J // 4][:, J % 4, :].bitcast(F32)
             for u in range(2):
                 nc.tensor.transpose(dzt_b[J][:, u, :], words[:, u : 256 : 2], ident[:])
@@ -195,21 +199,21 @@ def tile_hetxlhead_pa_v_kernel(
                 rhs=wd[0][:].bitcast(E4M3), rhs_scale=wd[1][:], start=False, stop=True,
             )
 
-        def keep_last(J):
+        def empty_out(J):
+            res[J] = sb("res", [P, D], F32, 4)
             if J in SPLIT:
-                last[J] = sb("last", [P, D], F32, 2)
-                nc.scalar.copy(out=last[J][:], in_=dpb[J, 3][:])
+                nc.vector.tensor_tensor(out=res[J][:], in0=outb[J][:], in1=kept[J][:], op=ADD)
+            else:
+                nc.scalar.copy(out=res[J][:], in_=outb[J][:])
 
         def store_out(J):
-            res = sb("res", [P, D], F32, 3)
-            if J in SPLIT:
-                nc.vector.tensor_tensor(out=res[:], in0=outb[J][:], in1=last[J][:], op=ADD)
-            else:
-                nc.scalar.copy(out=res[:], in_=outb[J][:])
-            nc.sync.dma_start(out=o_view[J // 4, J % 4], in_=res[:])
+            nc.sync.dma_start(out=o_view[J // 4, J % 4], in_=res[J][:])
 
-        def interleave(eng_copy, dst, src, cols):
-            eng_copy(out=dst[:, cols, :], in_=src[:, :, cols].rearrange("p j w -> p w j"))
+        def interleave(copy, dst, src, cols):
+            copy(
+                out=dst[:, cols, :].rearrange("p (c i) j -> p c j i", i=4),
+                in_=src[:, :, cols].rearrange("p j (c i) -> p c j i", i=4),
+            )
 
         def quant_w(pair, t, fmt, cols=slice(0, D)):
             nc.vector.quantize_mx(
@@ -220,6 +224,11 @@ def tile_hetxlhead_pa_v_kernel(
         def grouped_w():
             return sb("wg", [P, D, 4], BF16, 2)
 
+        def warm_up(count):
+            bank = ps("dp", [P, D])
+            for k in range(count):
+                nc.tensor.matmul(bank[:], lhsT=wc_raw[0][:, 1, 0:P], rhs=wc_raw[0][:, 0, :], start=True, stop=True)
+
         def weight_pass(m, g):
             cols = slice(m * P, (m + 1) * P)
             nc.tensor.matmul_mx(
@@ -227,244 +236,233 @@ def tile_hetxlhead_pa_v_kernel(
                 rhs=ft[g][0][:].bitcast(E4M3), rhs_scale=ft[g][1][:], start=g == 0, stop=g == 1,
             )
 
-        full = slice(0, D)
+        wc = [quantised("wc0", D, 1), quantised("wc1", D, 1)]
+        wd = quantised("wd", D, 1)
+        ft = [quantised("ft0", D, 1), quantised("ft1", D, 1)]
+        dzq = [quantised("dz0", D, 1), quantised("dz1", D, 1)]
         left, right = slice(0, D // 2), slice(D // 2, D)
+        quarter = [slice(m * P, (m + 1) * P) for m in range(4)]
+        acc = []
         ctx.enter_context(tc.manual_schedule())
 
         dummy = sb("dummy", [P, 1], F32, 1)
         nc.vector.memset(dummy[:], 0.0)
         nc.scalar.activation(dummy[:], dummy[:], mybir.ActivationFunctionType.Sigmoid)
 
-        wc_raw = [load_w(w_cls[0:512, :]), load_w(w_cls[512:1024, :])]
+        wc_raw = [load_w(w_cls[0:512, :])]
         load_g(0, 0, 1)
+        wc_raw.append(load_w(w_cls[512:1024, :]))
         load_g(0, 1, 2)
         load_g(0, 2, 4)
-        load_n(0, 1)
+        load_n(0, 0, 2)
         load_g(1, 0, 2)
+        load_n(0, 2, 4)
         load_g(1, 2, 4)
-        load_g(2)
-        load_n(1, 1)
-        load_z(0)
-        load_g(3)
+        load_g(2, 0, 2)
+        load_n(1)
+        load_z(0, 1)
+        load_g(2, 2, 4)
+        load_g(3, 0, 2)
         wd_raw = load_w(w_diag)
-        load_n(2, 2)
+        load_n(2)
+        load_z(1, 1)
+        load_g(3, 2, 4)
         load_g(4)
-        load_z(2)
+        load_z(2, 2)
+        load_n(3)
+        ft_raw = [load_w(features[0:512, :])]
         load_g(5)
+        load_n(4)
+        load_z(4, 2)
+        load_g(6)
+        ft_raw.append(load_w(features[512:1024, :]))
+        load_n(5)
+        load_g(7)
+        load_n(6)
+        load_z(6, 2)
+        load_n(7)
 
-        wc = [quantised("wc0", D, 1), quantised("wc1", D, 1)]
-        wd = quantised("wd", D, 1)
-        ft = [quantised("ft0", D, 1), quantised("ft1", D, 1)]
-        dzq = [quantised("dz0", D, 1), quantised("dz1", D, 1)]
-
+        on_vector, on_scalar = slice(0, 320), slice(320, D)
         wg = [grouped_w(), grouped_w()]
-        for h in range(2):
-            interleave(nc.vector.tensor_copy, wg[h], wc_raw[h], left)
-            interleave(nc.scalar.copy, wg[h], wc_raw[h], right)
-        prescale(0, 0, 0, 1)
+        warm_up(3)
+        interleave(nc.vector.tensor_copy, wg[0], wc_raw[0], on_vector)
+        interleave(nc.scalar.copy, wg[0], wc_raw[0], on_scalar)
+        prescale(0, 0, 1)
         turn(0, 0)
-        empty_turn(0, 0)
+        warm_up(2)
         quant_w(wc[0], wg[0], E4M3)
-        prescale(0, 0, 1, 2)
+        interleave(nc.vector.tensor_copy, wg[1], wc_raw[1], on_vector)
+        interleave(nc.scalar.copy, wg[1], wc_raw[1], on_scalar)
+        empty_turn(0, 0, 1)
+        prescale(0, 1, 2)
         turn(0, 1)
+        warm_up(1)
         quant_w(wc[1], wg[1], E4M3)
-        quant_g(0, 0, 0, 1)
-        empty_turn(0, 1)
-        prescale(0, 1)
+        quant_g(0, 0, 1)
+        empty_turn(0, 1, 1)
+        prescale(0, 2, 4)
         dpre(0, 0)
         turn(0, 2)
         turn(0, 3)
-        quant_g(0, 0, 1, 2)
+        quant_g(0, 1, 2)
+        direct(0, 0, 1)
         empty_turn(0, 2)
         empty_turn(0, 3)
         dpre(0, 1)
         times_noise(0, 0)
-        prescale(1, 0)
+        prescale(1, 0, 2)
         turn(1, 0)
         turn(1, 1)
+        prescale(1, 2, 4)
         times_noise(0, 1)
-        quant_g(0, 1)
+        quant_g(0, 2, 4)
+        direct(0, 1, 2)
         empty_turn(1, 0)
         empty_turn(1, 1)
         dpre(0, 2)
-        dpre(0, 3)
-        prescale(1, 1)
-        add_pair(0, 0)
         turn(1, 2)
         turn(1, 3)
-        times_noise(0, 2)
-        times_noise(0, 3)
+        dpre(0, 3)
+        prescale(2, 0, 2)
         empty_turn(1, 2)
         empty_turn(1, 3)
-        sigmoid(0)
-        quant_g(1, 0)
-        direct(0, 0)
-        direct(0, 1)
-        prescale(2, 0)
-        dpre(1, 0)
+        times_noise(0, 2)
+        quant_g(1, 0, 2)
+        times_noise(0, 3)
+        keep_dpre(0)
+        direct(0, 2, 3)
         turn(2, 0)
         turn(2, 1)
-        prescale(2, 1)
+        direct(0, 3, 4)
         empty_turn(2, 0)
         empty_turn(2, 1)
-        quant_g(1, 1)
-        add_pair(0, 1)
+        sigmoid(0)
+        quant_g(1, 2, 4)
+        prescale(2, 2, 4)
+        add_pairs(0)
+        prescale(3, 0, 2)
         add_all(0, nc.vector)
 
-        ft_raw = [load_w(features[0:512, :])]
-        load_n(4, 2)
-        load_g(6)
-        load_z(4)
-        ft_raw.append(load_w(features[512:1024, :]))
-        load_g(7)
-        load_n(6, 2)
-        load_z(6)
-
-        L = TILES - 1
-        acc = []
-        EARLY = ()
-        SIDE = {3: "f0", 4: "f1", 5: "dz"}
-        make_dz(0, full, nc.gpsimd)
-        dpre(1, 1)
-        times_noise(1, 0)
-        times_noise(1, 1)
-        dpre(1, 2)
-        times_noise(1, 2)
-        dpre(1, 3)
-        times_noise(1, 3)
-        direct(0, 2)
-        direct(0, 3)
-        turn(2, 2)
-        turn(2, 3)
-        turn_dz(0)
-        empty_turn(2, 2)
-        empty_turn(2, 3)
-        side = grouped_w()
-        interleave(nc.scalar.copy, side, wd_raw, right)
-        empty_dz(0)
-        prescale(3, 0)
-        quant_g(2, 0)
-        prescale(3, 1)
-        sigmoid(1)
-        add_pair(1, 0)
-        quant_g(2, 1)
-        for s in range(S):
-            turn(3, s)
-        add_pair(1, 1)
-        interleave(nc.vector.tensor_copy, side, wd_raw, left)
-        quant_dz(0)
-        quant_w(wd, side, E4M3)
-        add_all(1, nc.vector)
-
-        for J in range(2, TILES):
-            nxt = J < L
-            if nxt:
-                empty_turn(J + 1, 0)
-                empty_turn(J + 1, 1)
+        side_src = {1: wd_raw, 3: ft_raw[0], 4: ft_raw[1]}
+        side_dst = {1: (wd, E4M3), 3: (ft[0], E4M3), 4: (ft[1], E4M3), 5: (dzq[0], E5M2)}
+        side = {}
+        for J in range(1, TILES):
+            if J >= 3:
+                empty_out(J - 3)
+            if J in side_dst:
+                src = dz[0] if J == 5 else side_src[J]
+                side[J] = grouped_w()
+                interleave(nc.scalar.copy, side[J], src, left)
             dpre(J, 0)
             times_noise(J, 0)
-            make_dz(J - 1, full, nc.gpsimd)
+            make_dz(J - 1, nc.gpsimd)
             dpre(J, 1)
             times_noise(J, 1)
-            if J < L:
-                dz_pass(J - 2)
-                store_out(J - 2)
-            if nxt:
-                empty_turn(J + 1, 2)
-                empty_turn(J + 1, 3)
-            sigmoid(J)
-            if J in EARLY:
-                scalar_prescale(J + 3, 1)
             dpre(J, 2)
             times_noise(J, 2)
-            if J == L:
-                direct(J - 1, 0)
-                direct(J - 1, 1)
+            if J < LAST:
+                turn(J + 1, 2)
+                turn(J + 1, 3)
+                empty_turn(J + 1, 2)
+                empty_turn(J + 1, 3)
             dpre(J, 3)
-            if J == L:
-                quant_dz(J - 2)
-                dz_pass(J - 2)
-                store_out(J - 2)
-                add_pair(J, 0)
             times_noise(J, 3)
-            keep_last(J)
-            for s in range(2 if J == L else 0, S):
-                direct(J - 1, s)
+            if J == LAST:
+                break
+            keep_dpre(J)
+            sigmoid(J)
+            if J >= 2:
+                direct(J - 1, 0, S if J - 1 in SPLIT else 3)
             if J + 2 < TILES:
-                prescale(J + 2, 0)
-                if J - 1 not in EARLY:
-                    prescale(J + 2, 1)
-            if J - 1 in SIDE:
-                quant_w(pair, side, E5M2 if SIDE[J - 1] == "dz" else E4M3)
-            if nxt:
-                quant_g(J + 1, 0)
-                add_pair(J, 0)
-                quant_g(J + 1, 1)
+                turn(J + 2, 0)
+                turn(J + 2, 1)
             turn_dz(J - 1)
             if J + 2 < TILES:
-                for s in range(S):
-                    turn(J + 2, s)
-            if J == L:
-                break
-            if J in SIDE:
-                src = {"f0": ft_raw[0], "f1": ft_raw[1], "dz": dz[0]}[SIDE[J]]
-                pair = {"f0": ft[0], "f1": ft[1], "dz": dzq[0]}[SIDE[J]]
-                side = grouped_w()
-                interleave(nc.scalar.copy, side, src, left)
-                empty_dz(J - 1)
-                interleave(nc.scalar.copy, side, src, right)
-                add_pair(J, 1)
-                quant_dz(J - 1)
+                empty_turn(J + 2, 0)
+                empty_turn(J + 2, 1)
+            empty_dz(J - 1)
+            if J in side_dst:
+                interleave(nc.scalar.copy, side[J], src, right)
+            if J >= 2:
+                direct(J - 1, S if J - 1 in SPLIT else 3, S)
+            quant_g(J + 1, 0, 2)
+            if J >= 2:
+                quant_dz(J - 2)
+            if J - 1 in side_dst and J + 3 < TILES:
+                quant_w(side_dst[J - 1][0], side[J - 1], side_dst[J - 1][1])
+            if J >= 2:
+                dz_pass(J - 2)
+            if J + 2 < TILES:
+                prescale(J + 2, 2, 4)
+            if J + 3 < TILES:
+                quant_g(J + 1, 2, 4)
+                add_pairs(J)
+                prescale(J + 3, 0, 2)
+                add_all(J, nc.vector)
             else:
-                empty_dz(J - 1)
-                add_pair(J, 1)
-                if J < L - 1:
-                    quant_dz(J - 1)
-            add_all(J, nc.vector)
-            if J == L - 1:
-                acc = [ps("tr", [P, D], 4), ps("tr", [P, D], 4)]
-                weight_pass(0, 0)
-                weight_pass(1, 0)
+                quant_g(J + 1, 2, 4)
+                add_pairs(J)
+                quant_w(side_dst[J - 1][0], side[J - 1], side_dst[J - 1][1])
+                add_all(J, nc.vector)
+            if J == LAST - 1:
+                direct(J, 0, 2, tag="tr")
+                quant_dz(J - 1)
+            if J >= 4:
+                store_out(J - 4)
+        store_out(LAST - 4)
+        store_out(LAST - 3)
 
-        part[L, 1] = sb("part", [P, D], F32, 3)
-        nc.vector.tensor_tensor(out=part[L, 1][:], in0=part[L, 0][:], in1=prod[L, 1][:, 0, :], op=ADD)
+        L = LAST
+        keep_dpre(L)
+        sigmoid(L)
+        dz_pass(L - 2)
+        direct(L - 1, 2, S)
+        turn_dz(L - 1)
         empty_dz(L - 1)
-        for s in range(S):
-            direct(L, s)
-        dstd[L] = sb("dstd", [P, D], F32, 2)
+        direct(L)
+        empty_out(L - 2)
+        store_out(L - 2)
+        part[L] = sb("part", [P, 2, D], F32, 2)
         for cols in (left, right):
-            nc.vector.tensor_tensor(
-                out=dstd[L][:, cols], in0=part[L, 1][:, cols], in1=prod[L, 1][:, 1, cols], op=ADD
-            )
+            nc.vector.tensor_tensor(out=part[L][:, :, cols], in0=prod[L][:, 0, :, cols], in1=prod[L][:, 1, :, cols], op=ADD)
+        acc = [ps("tr", [P, D]), ps("dp", [P, D]), ps("dp", [P, D]), ps("dp", [P, D])]
         for cols in (left, right):
-            make_dz(L, cols, nc.vector)
-        acc += [ps("dp", [P, D], 3), ps("dp", [P, D], 3)]
-        turn_dz(L)
+            add_all(L, nc.vector, cols)
+        for cols in (left, right):
+            make_dz(L, nc.vector, cols)
+        quant_dz(L - 1)
+        weight_pass(0, 0)
+        turn_dz(L, "out")
+        dz_pass(L - 1)
         weight_pass(2, 0)
+        weight_pass(1, 0)
         weight_pass(3, 0)
         t = grouped_w()
-        quarter = [slice(m * P, (m + 1) * P) for m in range(4)]
         interleave(nc.vector.tensor_copy, t, dz[1], quarter[0])
         interleave(nc.scalar.copy, t, dz[1], quarter[1])
-        quant_dz(L - 1)
-        dz_pass(L - 1)
         interleave(nc.vector.tensor_copy, t, dz[1], quarter[2])
         quant_w(dzq[1], t, E5M2, quarter[0])
         interleave(nc.vector.tensor_copy, t, dz[1], quarter[3])
-        quant_w(dzq[1], t, E5M2, quarter[1])
         empty_dz(L)
         quant_w(dzq[1], t, E5M2, quarter[2])
+        quant_w(dzq[1], t, E5M2, quarter[1])
         quant_w(dzq[1], t, E5M2, quarter[3])
         quant_dz(L)
-        for m in range(4):
+        empty_out(L - 1)
+        store_out(L - 1)
+        for m in (0, 2, 1, 3):
             weight_pass(m, 1)
         dz_pass(L)
-        store_out(L - 1)
-        for m in range(4):
+        for i, m in enumerate((0, 2, 1, 3)):
             r = sb("res1", [P, D], F32, 4)
-            if m == 0:
+            if i % 2 == 0:
                 nc.vector.tensor_copy(out=r[:], in_=acc[m][:])
             else:
                 nc.scalar.copy(out=r[:], in_=acc[m][:])
             nc.sync.dma_start(out=out_1[m * P : (m + 1) * P, :], in_=r[:])
+        if L in SPLIT:
+            empty_out(L)
+        else:
+            res[L] = sb("res", [P, D], F32, 4)
+            nc.vector.tensor_copy(out=res[L][:], in_=outb[L][:])
         store_out(L)

@@ -18,7 +18,10 @@ TEMPERATURE = 1.5
 TILES = B // P
 LAST = TILES - 1
 KEPT = 1
-SPLIT = (7,)
+SPLIT = (2, 3, 7)
+PAIRS_ON_GPSIMD = (0, 1, 2, 3, 4, 5)
+SCALAR_LAST = (2, 3, 4, 5, 6, 7)
+SCALAR_SECOND = ()
 FLOPS = 2 * (B * S * C * D + B * D * D + D * D * B)
 BYTES = 2 * (B * S * C + B * S * D + B * D + D * D + C * D) + 4 * (B * D) + 4 * (B * D + D * D)
 
@@ -82,7 +85,7 @@ def tile_hetxlhead_pa_v_kernel(
             return t
 
         def scale_views(J, a, b):
-            t = sb("gs", [P, 2, 256 * (b - a), 2], BF16, 4)
+            t = sb("gs", [P, 2, 256 * (b - a), 2], BF16, 6)
             for s in range(a, b):
                 gs[J, s] = (t, s - a, b - a)
             src, at = raw[J, a]
@@ -96,6 +99,20 @@ def tile_hetxlhead_pa_v_kernel(
             dst, src = scale_views(J, a, b)
             nc.scalar.activation(dst, src, mybir.ActivationFunctionType.Copy, scale=1.0 / TEMPERATURE)
 
+        def first_half(J):
+            prescale(J, 0, 1 if J in SCALAR_SECOND else 2)
+
+        def second_half(J):
+            prescale(J, 2, 3 if J in SCALAR_LAST else 4)
+
+        def scalar_last(J):
+            if J in SCALAR_LAST:
+                scalar_prescale(J, 3, 4)
+
+        def scalar_second(J):
+            if J in SCALAR_SECOND:
+                scalar_prescale(J, 1, 2)
+
         def turn(J, s):
             trb[J, s] = ps("tr", [P, 2, 2, P])
             t, at, count = gs[J, s]
@@ -108,7 +125,10 @@ def tile_hetxlhead_pa_v_kernel(
         def empty_turn(J, s, count=2):
             at = s % count
             if at == 0:
-                t = sb("grp", [P, count, 2, P, 2], F32, 3)
+                if s == 2:
+                    t = sb("mix%d" % (J % 2), [P, count, 2, P, 2], F32, 1)
+                else:
+                    t = sb("grp", [P, count, 2, P, 2], F32, 2)
                 for k in range(count):
                     grp[J, s + k] = t
             nc.scalar.copy(out=grp[J, s][:, at], in_=trb[J, s][:].rearrange("p h u r -> p h r u"))
@@ -156,31 +176,54 @@ def tile_hetxlhead_pa_v_kernel(
                 out=prod[J][:, s % 2, s // 2, cols], in0=dpb[J, s][:, cols], in1=noise[J, s][:, cols], op=MULT
             )
 
-        def add_pairs(J):
-            part[J] = sb("part", [P, 2, D], F32, 2)
-            nc.vector.tensor_tensor(out=part[J][:], in0=prod[J][:, 0], in1=prod[J][:, 1], op=ADD)
-
-        def add_all(J, eng, cols=slice(0, D)):
+        def add_pairs(J, eng, cols=slice(0, D)):
             if cols.start == 0:
+                part[J] = sb("mix%d" % ((J + (J in PAIRS_ON_GPSIMD)) % 2), [P, 2, D], F32, 1)
+            eng.tensor_tensor(
+                out=part[J][:, :, cols], in0=prod[J][:, 0, :, cols], in1=prod[J][:, 1, :, cols], op=ADD
+            )
+
+        def natural(ap, words):
+            return ap.rearrange("p (w u e) -> p u w e", u=2, e=2)[:, :, words, :]
+
+        def sorted_by_half(ap, words):
+            return ap.rearrange("p (u w e) -> p u w e", u=2, e=2)[:, :, words, :]
+
+        def add_all(J, words=slice(0, P)):
+            if words.start == 0:
                 dstd[J] = sb("dstd", [P, D], F32, 2)
-            eng.tensor_tensor(out=dstd[J][:, cols], in0=part[J][:, 0, cols], in1=part[J][:, 1, cols], op=ADD)
+            nc.vector.tensor_tensor(
+                out=sorted_by_half(dstd[J][:], words), in0=natural(part[J][:, 0, :], words),
+                in1=natural(part[J][:, 1, :], words), op=ADD,
+            )
 
         def sigmoid(J):
             sig[J] = sb("sig", [P, D], F32, 3)
-            nc.scalar.activation(sig[J][:], zt[J], mybir.ActivationFunctionType.Sigmoid)
+            nc.scalar.activation(
+                sorted_by_half(sig[J][:], slice(0, P)), natural(zt[J], slice(0, P)),
+                mybir.ActivationFunctionType.Sigmoid,
+            )
 
-        def make_dz(J, eng, cols=slice(0, D)):
-            if J % 4 == 0 and cols.start == 0:
+        def make_dz(J, eng, words=slice(0, P)):
+            if J % 4 == 0 and words.start == 0:
                 dz[J // 4] = sb("dz", [P, 4, D], BF16, 2)
             eng.tensor_tensor(
-                out=dz[J // 4][:, J % 4, cols], in0=dstd[J][:, cols], in1=sig[J][:, cols], op=MULT
+                out=sorted_by_half(dz[J // 4][:, J % 4, :], words), in0=sorted_by_half(dstd[J][:], words),
+                in1=sorted_by_half(sig[J][:], words), op=MULT,
             )
 
         def turn_dz(J, tag="dp"):
             dzt_b[J] = ps(tag, [P, 2, P])
             words = dz[J // 4][:, J % 4, :].bitcast(F32)
             for u in range(2):
-                nc.tensor.transpose(dzt_b[J][:, u, :], words[:, u : 256 : 2], ident[:])
+                nc.tensor.transpose(dzt_b[J][:, u, :], words[:, u * P : (u + 1) * P], ident[:])
+
+        def interleave_dz(copy, dst, src, cols):
+            words = slice(cols.start // 4, cols.stop // 4)
+            copy(
+                out=dst[:].rearrange("p (w u e) j -> p u w j e", u=2, e=2)[:, :, words],
+                in_=src[:].rearrange("p j (u w e) -> p u w j e", u=2, e=2)[:, :, words],
+            )
 
         def empty_dz(J):
             dzt[J] = sb("dzt", [P, P, 2], F32, 2)
@@ -223,6 +266,11 @@ def tile_hetxlhead_pa_v_kernel(
 
         def grouped_w():
             return sb("wg", [P, D, 4], BF16, 2)
+
+        def store_weight(m, copy):
+            r = sb("res1", [P, D], F32, 4)
+            copy(out=r[:], in_=acc[m][:])
+            nc.sync.dma_start(out=out_1[m * P : (m + 1) * P, :], in_=r[:])
 
         def warm_up(count):
             bank = ps("dp", [P, D])
@@ -330,82 +378,108 @@ def tile_hetxlhead_pa_v_kernel(
         quant_g(1, 0, 2)
         times_noise(0, 3)
         keep_dpre(0)
-        direct(0, 2, 3)
         turn(2, 0)
         turn(2, 1)
-        direct(0, 3, 4)
         empty_turn(2, 0)
         empty_turn(2, 1)
         sigmoid(0)
+        scalar_last(2)
+        second_half(2)
+        if 0 not in PAIRS_ON_GPSIMD:
+            add_pairs(0, nc.vector)
         quant_g(1, 2, 4)
-        prescale(2, 2, 4)
-        add_pairs(0)
-        prescale(3, 0, 2)
-        add_all(0, nc.vector)
+        first_half(3)
+        if 0 not in PAIRS_ON_GPSIMD:
+            add_all(0)
 
-        side_src = {1: wd_raw, 3: ft_raw[0], 4: ft_raw[1]}
-        side_dst = {1: (wd, E4M3), 3: (ft[0], E4M3), 4: (ft[1], E4M3), 5: (dzq[0], E5M2)}
+        side_jobs = {"wd": (1, 2, 2), "f0": (3, 4, 4), "f1": (5, 5.5, 6), "dz": (6, 6.5, 6)}
         side = {}
+
+        def side_copy(J):
+            for name, halves in side_jobs.items():
+                for cols, step in zip((left, right), halves):
+                    if step == J:
+                        if cols.start == 0:
+                            side[name] = grouped_w()
+                        if name == "dz":
+                            interleave_dz(nc.scalar.copy, side[name], dz[0], cols)
+                        else:
+                            src = {"wd": wd_raw, "f0": ft_raw[0], "f1": ft_raw[1]}[name]
+                            interleave(nc.scalar.copy, side[name], src, cols)
+
+        def side_quant(J):
+            for name, halves in side_jobs.items():
+                if halves[2] == J:
+                    pair = {"wd": wd, "f0": ft[0], "f1": ft[1], "dz": dzq[0]}[name]
+                    quant_w(pair, side[name], E5M2 if name == "dz" else E4M3)
+
         for J in range(1, TILES):
+            late = J - 1 in PAIRS_ON_GPSIMD
             if J >= 3:
                 empty_out(J - 3)
-            if J in side_dst:
-                src = dz[0] if J == 5 else side_src[J]
-                side[J] = grouped_w()
-                interleave(nc.scalar.copy, side[J], src, left)
+            side_copy(J)
+            scalar_second(J + 2)
             dpre(J, 0)
             times_noise(J, 0)
-            make_dz(J - 1, nc.gpsimd)
-            dpre(J, 1)
-            times_noise(J, 1)
-            dpre(J, 2)
-            times_noise(J, 2)
-            if J < LAST:
-                turn(J + 1, 2)
-                turn(J + 1, 3)
-                empty_turn(J + 1, 2)
-                empty_turn(J + 1, 3)
-            dpre(J, 3)
-            times_noise(J, 3)
+            if late:
+                add_pairs(J - 1, nc.gpsimd)
+            else:
+                make_dz(J - 1, nc.gpsimd)
+            for s in range(1, S):
+                dpre(J, s)
+                if J < LAST or s < S - 1:
+                    times_noise(J, s)
             if J == LAST:
                 break
+            turn(J + 1, 2)
+            turn(J + 1, 3)
+            if J >= 2:
+                turn_dz(J - 2)
+            empty_turn(J + 1, 2)
+            empty_turn(J + 1, 3)
+            if J >= 2:
+                empty_dz(J - 2)
             keep_dpre(J)
             sigmoid(J)
-            if J >= 2:
+            scalar_last(J + 2)
+            side_copy(J + 0.5)
+            if J == 1:
+                direct(0, 2, S)
+            else:
                 direct(J - 1, 0, S if J - 1 in SPLIT else 3)
+            quant_g(J + 1, 0, 2)
+            if late:
+                add_all(J - 1)
+            if J + 2 < TILES:
+                second_half(J + 2)
+            if J >= 2:
+                quant_dz(J - 2)
+            if late:
+                make_dz(J - 1, nc.vector)
+            if J + 3 < TILES:
+                side_quant(J)
             if J + 2 < TILES:
                 turn(J + 2, 0)
                 turn(J + 2, 1)
-            turn_dz(J - 1)
-            if J + 2 < TILES:
                 empty_turn(J + 2, 0)
                 empty_turn(J + 2, 1)
-            empty_dz(J - 1)
-            if J in side_dst:
-                interleave(nc.scalar.copy, side[J], src, right)
             if J >= 2:
                 direct(J - 1, S if J - 1 in SPLIT else 3, S)
-            quant_g(J + 1, 0, 2)
-            if J >= 2:
-                quant_dz(J - 2)
-            if J - 1 in side_dst and J + 3 < TILES:
-                quant_w(side_dst[J - 1][0], side[J - 1], side_dst[J - 1][1])
-            if J >= 2:
                 dz_pass(J - 2)
-            if J + 2 < TILES:
-                prescale(J + 2, 2, 4)
-            if J + 3 < TILES:
-                quant_g(J + 1, 2, 4)
-                add_pairs(J)
-                prescale(J + 3, 0, 2)
-                add_all(J, nc.vector)
-            else:
-                quant_g(J + 1, 2, 4)
-                add_pairs(J)
-                quant_w(side_dst[J - 1][0], side[J - 1], side_dst[J - 1][1])
-                add_all(J, nc.vector)
             if J == LAST - 1:
                 direct(J, 0, 2, tag="tr")
+                turn_dz(J - 1)
+                empty_dz(J - 1)
+            if J not in PAIRS_ON_GPSIMD:
+                add_pairs(J, nc.vector)
+            quant_g(J + 1, 2, 4)
+            if J + 3 < TILES:
+                first_half(J + 3)
+            else:
+                side_quant(J)
+            if J not in PAIRS_ON_GPSIMD:
+                add_all(J)
+            if J == LAST - 1:
                 quant_dz(J - 1)
             if J >= 4:
                 store_out(J - 4)
@@ -413,6 +487,7 @@ def tile_hetxlhead_pa_v_kernel(
         store_out(LAST - 3)
 
         L = LAST
+        halves = (slice(0, P // 2), slice(P // 2, P))
         keep_dpre(L)
         sigmoid(L)
         dz_pass(L - 2)
@@ -422,47 +497,60 @@ def tile_hetxlhead_pa_v_kernel(
         direct(L)
         empty_out(L - 2)
         store_out(L - 2)
-        part[L] = sb("part", [P, 2, D], F32, 2)
-        for cols in (left, right):
-            nc.vector.tensor_tensor(out=part[L][:, :, cols], in0=prod[L][:, 0, :, cols], in1=prod[L][:, 1, :, cols], op=ADD)
-        acc = [ps("tr", [P, D]), ps("dp", [P, D]), ps("dp", [P, D]), ps("dp", [P, D])]
-        for cols in (left, right):
-            add_all(L, nc.vector, cols)
-        for cols in (left, right):
-            make_dz(L, nc.vector, cols)
-        quant_dz(L - 1)
-        weight_pass(0, 0)
-        turn_dz(L, "out")
-        dz_pass(L - 1)
-        weight_pass(2, 0)
-        weight_pass(1, 0)
-        weight_pass(3, 0)
+        acc = [ps("tr", [P, D])]
+        part[L] = sb("mix1", [P, 2, D], F32, 1)
+        dstd[L] = sb("dstd", [P, D], F32, 2)
         t = grouped_w()
-        interleave(nc.vector.tensor_copy, t, dz[1], quarter[0])
-        interleave(nc.scalar.copy, t, dz[1], quarter[1])
-        interleave(nc.vector.tensor_copy, t, dz[1], quarter[2])
+
+        def running(step, half):
+            cols = (left, right)[half]
+            if step == 0:
+                ins, out = (prod[L][:, 0, 0, cols], prod[L][:, 1, 0, cols]), part[L][:, 0, cols]
+            elif step == 1:
+                ins, out = (part[L][:, 0, cols], prod[L][:, 0, 1, cols]), part[L][:, 1, cols]
+            else:
+                ins = (natural(part[L][:, 1, :], halves[half]), natural(prod[L][:, 1, 1, :], halves[half]))
+                out = sorted_by_half(dstd[L][:], halves[half])
+            nc.vector.tensor_tensor(out=out, in0=ins[0], in1=ins[1], op=ADD)
+
+        running(0, 0)
+        times_noise(L, 3, left)
+        running(1, 0)
+        running(0, 1)
+        running(2, 0)
+        times_noise(L, 3, right)
+        make_dz(L, nc.vector, halves[0])
+        quant_dz(L - 1)
+        running(1, 1)
+        interleave_dz(nc.vector.tensor_copy, t, dz[1], quarter[0])
+        interleave_dz(nc.scalar.copy, t, dz[1], quarter[1])
+        running(2, 1)
         quant_w(dzq[1], t, E5M2, quarter[0])
-        interleave(nc.vector.tensor_copy, t, dz[1], quarter[3])
-        empty_dz(L)
-        quant_w(dzq[1], t, E5M2, quarter[2])
-        quant_w(dzq[1], t, E5M2, quarter[1])
-        quant_w(dzq[1], t, E5M2, quarter[3])
-        quant_dz(L)
+        acc += [ps("dp", [P, D]), ps("dp", [P, D]), ps("dp", [P, D])]
+        weight_pass(0, 0)
+        dz_pass(L - 1)
+        weight_pass(1, 0)
+        weight_pass(0, 1)
         empty_out(L - 1)
         store_out(L - 1)
-        for m in (0, 2, 1, 3):
-            weight_pass(m, 1)
+        store_weight(0, nc.scalar.copy)
+        make_dz(L, nc.vector, halves[1])
+        quant_w(dzq[1], t, E5M2, quarter[1])
+        weight_pass(2, 0)
+        turn_dz(L, "out")
+        weight_pass(1, 1)
+        weight_pass(3, 0)
+        interleave_dz(nc.vector.tensor_copy, t, dz[1], quarter[2])
+        empty_dz(L)
+        store_weight(1, nc.scalar.copy)
+        interleave_dz(nc.vector.tensor_copy, t, dz[1], quarter[3])
+        quant_w(dzq[1], t, E5M2, quarter[2])
+        weight_pass(2, 1)
+        quant_w(dzq[1], t, E5M2, quarter[3])
+        quant_dz(L)
+        weight_pass(3, 1)
         dz_pass(L)
-        for i, m in enumerate((0, 2, 1, 3)):
-            r = sb("res1", [P, D], F32, 4)
-            if i % 2 == 0:
-                nc.vector.tensor_copy(out=r[:], in_=acc[m][:])
-            else:
-                nc.scalar.copy(out=r[:], in_=acc[m][:])
-            nc.sync.dma_start(out=out_1[m * P : (m + 1) * P, :], in_=r[:])
-        if L in SPLIT:
-            empty_out(L)
-        else:
-            res[L] = sb("res", [P, D], F32, 4)
-            nc.vector.tensor_copy(out=res[L][:], in_=outb[L][:])
+        store_weight(2, nc.vector.tensor_copy)
+        store_weight(3, nc.scalar.copy)
+        empty_out(L)
         store_out(L)

@@ -18,10 +18,10 @@ TEMPERATURE = 1.5
 TILES = B // P
 LAST = TILES - 1
 KEPT = 1
-SPLIT = (2, 3, 7)
-PAIRS_ON_GPSIMD = (0, 1, 2, 3, 4, 5)
-SCALAR_LAST = (2, 3, 4, 5, 6, 7)
-SCALAR_SECOND = ()
+SPLIT = (7,)
+PAIRS_ON_GPSIMD = ()
+SCALAR_LAST = (2, 3, 4, 5)
+SCALAR_SECOND = (4,)
 FLOPS = 2 * (B * S * C * D + B * D * D + D * D * B)
 BYTES = 2 * (B * S * C + B * S * D + B * D + D * D + C * D) + 4 * (B * D) + 4 * (B * D + D * D)
 
@@ -304,8 +304,8 @@ def tile_hetxlhead_pa_v_kernel(
         load_g(0, 2, 4)
         load_n(0, 0, 2)
         load_g(1, 0, 2)
-        load_n(0, 2, 4)
         load_g(1, 2, 4)
+        load_n(0, 2, 4)
         load_g(2, 0, 2)
         load_n(1)
         load_z(0, 1)
@@ -362,11 +362,12 @@ def tile_hetxlhead_pa_v_kernel(
         turn(1, 0)
         turn(1, 1)
         prescale(1, 2, 4)
-        times_noise(0, 1)
         quant_g(0, 2, 4)
+        times_noise(0, 1)
         direct(0, 1, 2)
         empty_turn(1, 0)
         empty_turn(1, 1)
+        sigmoid(0)
         dpre(0, 2)
         turn(1, 2)
         turn(1, 3)
@@ -374,25 +375,23 @@ def tile_hetxlhead_pa_v_kernel(
         prescale(2, 0, 2)
         empty_turn(1, 2)
         empty_turn(1, 3)
+        scalar_last(2)
         times_noise(0, 2)
         quant_g(1, 0, 2)
         times_noise(0, 3)
         keep_dpre(0)
+        direct(0, 2, S)
         turn(2, 0)
         turn(2, 1)
         empty_turn(2, 0)
         empty_turn(2, 1)
-        sigmoid(0)
-        scalar_last(2)
         second_half(2)
-        if 0 not in PAIRS_ON_GPSIMD:
-            add_pairs(0, nc.vector)
         quant_g(1, 2, 4)
+        add_pairs(0, nc.vector)
         first_half(3)
-        if 0 not in PAIRS_ON_GPSIMD:
-            add_all(0)
+        add_all(0)
 
-        side_jobs = {"wd": (1, 2, 2), "f0": (3, 4, 4), "f1": (5, 5.5, 6), "dz": (6, 6.5, 6)}
+        side_jobs = {"wd": (1, 1, 1), "f0": (3, 4, 4), "f1": (4.5, 5, 5), "dz": (5.5, 6, 6)}
         side = {}
 
         def side_copy(J):
@@ -414,90 +413,64 @@ def tile_hetxlhead_pa_v_kernel(
                     quant_w(pair, side[name], E5M2 if name == "dz" else E4M3)
 
         for J in range(1, TILES):
-            late = J - 1 in PAIRS_ON_GPSIMD
-            if J >= 3:
-                empty_out(J - 3)
             side_copy(J)
             scalar_second(J + 2)
             dpre(J, 0)
             times_noise(J, 0)
-            if late:
-                add_pairs(J - 1, nc.gpsimd)
-            else:
-                make_dz(J - 1, nc.gpsimd)
-            for s in range(1, S):
-                dpre(J, s)
-                if J < LAST or s < S - 1:
-                    times_noise(J, s)
+            make_dz(J - 1, nc.gpsimd)
+            dpre(J, 1)
+            times_noise(J, 1)
+            dpre(J, 2)
+            times_noise(J, 2)
+            if J >= 2:
+                dz_pass(J - 2)
+                empty_out(J - 2)
+            dpre(J, 3)
             if J == LAST:
                 break
+            times_noise(J, 3)
             turn(J + 1, 2)
             turn(J + 1, 3)
-            if J >= 2:
-                turn_dz(J - 2)
             empty_turn(J + 1, 2)
             empty_turn(J + 1, 3)
-            if J >= 2:
-                empty_dz(J - 2)
             keep_dpre(J)
             sigmoid(J)
             scalar_last(J + 2)
             side_copy(J + 0.5)
-            if J == 1:
-                direct(0, 2, S)
-            else:
-                direct(J - 1, 0, S if J - 1 in SPLIT else 3)
+            direct(J, 0, 2 if J == LAST - 1 else S if J in SPLIT else 3)
+            if 3 < J + 2 < TILES:
+                first_half(J + 2)
             quant_g(J + 1, 0, 2)
-            if late:
-                add_all(J - 1)
-            if J + 2 < TILES:
-                second_half(J + 2)
-            if J >= 2:
-                quant_dz(J - 2)
-            if late:
-                make_dz(J - 1, nc.vector)
-            if J + 3 < TILES:
-                side_quant(J)
+            add_pairs(J, nc.vector)
+            quant_g(J + 1, 2, 4)
+            turn_dz(J - 1)
+            empty_dz(J - 1)
             if J + 2 < TILES:
                 turn(J + 2, 0)
                 turn(J + 2, 1)
                 empty_turn(J + 2, 0)
                 empty_turn(J + 2, 1)
-            if J >= 2:
-                direct(J - 1, S if J - 1 in SPLIT else 3, S)
-                dz_pass(J - 2)
-            if J == LAST - 1:
-                direct(J, 0, 2, tag="tr")
-                turn_dz(J - 1)
-                empty_dz(J - 1)
-            if J not in PAIRS_ON_GPSIMD:
-                add_pairs(J, nc.vector)
-            quant_g(J + 1, 2, 4)
-            if J + 3 < TILES:
-                first_half(J + 3)
-            else:
-                side_quant(J)
-            if J not in PAIRS_ON_GPSIMD:
-                add_all(J)
-            if J == LAST - 1:
-                quant_dz(J - 1)
+            if J < LAST - 1:
+                direct(J, S if J in SPLIT else 3, S)
+            side_quant(J)
+            if J + 2 < TILES:
+                second_half(J + 2)
+            add_all(J)
+            quant_dz(J - 1)
             if J >= 4:
                 store_out(J - 4)
-        store_out(LAST - 4)
-        store_out(LAST - 3)
+        for J in range(LAST - 4, LAST - 1):
+            store_out(J)
 
         L = LAST
         halves = (slice(0, P // 2), slice(P // 2, P))
         keep_dpre(L)
         sigmoid(L)
-        dz_pass(L - 2)
         direct(L - 1, 2, S)
         turn_dz(L - 1)
         empty_dz(L - 1)
         direct(L)
-        empty_out(L - 2)
-        store_out(L - 2)
-        acc = [ps("tr", [P, D])]
+        acc = [ps("tr", [P, D]), ps("tr", [P, D])]
         part[L] = sb("mix1", [P, 2, D], F32, 1)
         dstd[L] = sb("dstd", [P, D], F32, 2)
         t = grouped_w()
@@ -526,7 +499,7 @@ def tile_hetxlhead_pa_v_kernel(
         interleave_dz(nc.scalar.copy, t, dz[1], quarter[1])
         running(2, 1)
         quant_w(dzq[1], t, E5M2, quarter[0])
-        acc += [ps("dp", [P, D]), ps("dp", [P, D]), ps("dp", [P, D])]
+        acc += [ps("dp", [P, D]), ps("dp", [P, D])]
         weight_pass(0, 0)
         dz_pass(L - 1)
         weight_pass(1, 0)
@@ -537,7 +510,7 @@ def tile_hetxlhead_pa_v_kernel(
         make_dz(L, nc.vector, halves[1])
         quant_w(dzq[1], t, E5M2, quarter[1])
         weight_pass(2, 0)
-        turn_dz(L, "out")
+        turn_dz(L)
         weight_pass(1, 1)
         weight_pass(3, 0)
         interleave_dz(nc.vector.tensor_copy, t, dz[1], quarter[2])

@@ -20,7 +20,7 @@ LAST = TILES - 1
 KEPT = 1
 SPLIT = (7,)
 PAIRS_ON_GPSIMD = ()
-SCALAR_LAST = (2, 3, 4, 5)
+SCALAR_LAST = (2, 3, 6, 7)
 SCALAR_SECOND = (4,)
 FLOPS = 2 * (B * S * C * D + B * D * D + D * D * B)
 BYTES = 2 * (B * S * C + B * S * D + B * D + D * D + C * D) + 4 * (B * D) + 4 * (B * D + D * D)
@@ -316,14 +316,14 @@ def tile_hetxlhead_pa_v_kernel(
         load_z(1, 1)
         load_g(3, 2, 4)
         load_g(4)
+        ft_raw = [load_w(features[0:512, :])]
         load_z(2, 2)
         load_n(3)
-        ft_raw = [load_w(features[0:512, :])]
         load_g(5)
+        ft_raw.append(load_w(features[512:1024, :]))
         load_n(4)
         load_z(4, 2)
         load_g(6)
-        ft_raw.append(load_w(features[512:1024, :]))
         load_n(5)
         load_g(7)
         load_n(6)
@@ -391,7 +391,7 @@ def tile_hetxlhead_pa_v_kernel(
         first_half(3)
         add_all(0)
 
-        side_jobs = {"wd": (1, 1, 1), "f0": (3, 4, 4), "f1": (4.5, 5, 5), "dz": (5.5, 6, 6)}
+        side_jobs = {"wd": (1, 1, 1), "f0": (2.5, 3, 3), "f1": (3.5, 4, 4), "dz": (5, 6, 6)}
         side = {}
 
         def side_copy(J):
@@ -412,7 +412,7 @@ def tile_hetxlhead_pa_v_kernel(
                     pair = {"wd": wd, "f0": ft[0], "f1": ft[1], "dz": dzq[0]}[name]
                     quant_w(pair, side[name], E5M2 if name == "dz" else E4M3)
 
-        for J in range(1, TILES):
+        for J in range(1, LAST):
             side_copy(J)
             scalar_second(J + 2)
             dpre(J, 0)
@@ -426,8 +426,6 @@ def tile_hetxlhead_pa_v_kernel(
                 dz_pass(J - 2)
                 empty_out(J - 2)
             dpre(J, 3)
-            if J == LAST:
-                break
             times_noise(J, 3)
             turn(J + 1, 2)
             turn(J + 1, 3)
@@ -437,7 +435,7 @@ def tile_hetxlhead_pa_v_kernel(
             sigmoid(J)
             scalar_last(J + 2)
             side_copy(J + 0.5)
-            direct(J, 0, 2 if J == LAST - 1 else S if J in SPLIT else 3)
+            direct(J, 0, 4 if J == LAST - 1 else S if J in SPLIT else 3)
             if 3 < J + 2 < TILES:
                 first_half(J + 2)
             quant_g(J + 1, 0, 2)
@@ -453,24 +451,34 @@ def tile_hetxlhead_pa_v_kernel(
             if J < LAST - 1:
                 direct(J, S if J in SPLIT else 3, S)
             side_quant(J)
-            if J + 2 < TILES:
-                second_half(J + 2)
             add_all(J)
             quant_dz(J - 1)
+            if J + 2 < TILES:
+                second_half(J + 2)
             if J >= 4:
                 store_out(J - 4)
-        for J in range(LAST - 4, LAST - 1):
-            store_out(J)
+        store_out(LAST - 4)
+        store_out(LAST - 3)
 
         L = LAST
         halves = (slice(0, P // 2), slice(P // 2, P))
-        keep_dpre(L)
+        make_dz(L - 1, nc.vector)
         sigmoid(L)
-        direct(L - 1, 2, S)
+        for s in range(S):
+            dpre(L, s)
+            if s < S - 1:
+                times_noise(L, s)
+        dz_pass(L - 2)
+        empty_out(L - 2)
+        store_out(L - 2)
+        direct(L - 1, 4, S)
         turn_dz(L - 1)
         empty_dz(L - 1)
-        direct(L)
+        keep_dpre(L)
         acc = [ps("tr", [P, D]), ps("tr", [P, D])]
+        weight_pass(0, 0)
+        weight_pass(1, 0)
+        direct(L, 0, 3)
         part[L] = sb("mix1", [P, 2, D], F32, 1)
         dstd[L] = sb("dstd", [P, D], F32, 2)
         t = grouped_w()
@@ -489,39 +497,38 @@ def tile_hetxlhead_pa_v_kernel(
         running(0, 0)
         times_noise(L, 3, left)
         running(1, 0)
+        quant_dz(L - 1)
+        dz_pass(L - 1)
+        empty_out(L - 1)
+        store_out(L - 1)
+        direct(L, 3, S)
         running(0, 1)
         running(2, 0)
         times_noise(L, 3, right)
         make_dz(L, nc.vector, halves[0])
-        quant_dz(L - 1)
         running(1, 1)
         interleave_dz(nc.vector.tensor_copy, t, dz[1], quarter[0])
         interleave_dz(nc.scalar.copy, t, dz[1], quarter[1])
         running(2, 1)
         quant_w(dzq[1], t, E5M2, quarter[0])
         acc += [ps("dp", [P, D]), ps("dp", [P, D])]
-        weight_pass(0, 0)
-        dz_pass(L - 1)
-        weight_pass(1, 0)
+        weight_pass(2, 0)
+        weight_pass(3, 0)
         weight_pass(0, 1)
-        empty_out(L - 1)
-        store_out(L - 1)
-        store_weight(0, nc.scalar.copy)
         make_dz(L, nc.vector, halves[1])
         quant_w(dzq[1], t, E5M2, quarter[1])
-        weight_pass(2, 0)
         turn_dz(L)
         weight_pass(1, 1)
-        weight_pass(3, 0)
-        interleave_dz(nc.vector.tensor_copy, t, dz[1], quarter[2])
+        store_weight(0, nc.scalar.copy)
         empty_dz(L)
-        store_weight(1, nc.scalar.copy)
+        interleave_dz(nc.vector.tensor_copy, t, dz[1], quarter[2])
         interleave_dz(nc.vector.tensor_copy, t, dz[1], quarter[3])
         quant_w(dzq[1], t, E5M2, quarter[2])
         weight_pass(2, 1)
+        store_weight(1, nc.scalar.copy)
         quant_w(dzq[1], t, E5M2, quarter[3])
-        quant_dz(L)
         weight_pass(3, 1)
+        quant_dz(L)
         dz_pass(L)
         store_weight(2, nc.vector.tensor_copy)
         store_weight(3, nc.scalar.copy)

@@ -20,8 +20,8 @@ LAST = TILES - 1
 KEPT = 1
 SPLIT = (7,)
 PAIRS_ON_GPSIMD = ()
-SCALAR_LAST = (2, 3, 6, 7)
-SCALAR_SECOND = (4,)
+SCALAR_LAST = (1, 2, 3, 6, 7)
+SCALAR_SECOND = (2, 4)
 FLOPS = 2 * (B * S * C * D + B * D * D + D * D * B)
 BYTES = 2 * (B * S * C + B * S * D + B * D + D * D + C * D) + 4 * (B * D) + 4 * (B * D + D * D)
 
@@ -155,6 +155,14 @@ def tile_hetxlhead_pa_v_kernel(
             for h in range(2):
                 g_pass(dpb[J, s][:], J, s, h, h == 0, h == 1)
 
+        def first_passes(s, h):
+            if h == 0:
+                dpb[0, s] = ps("dp", [P, D])
+                if s == 0:
+                    outb[0] = ps("out", [P, D])
+            g_pass(dpb[0, s][:], 0, s, h, h == 0, h == 1)
+            g_pass(outb[0][:], 0, s, h, s == 0 and h == 0, False)
+
         def direct(J, a=0, b=S, tag="out"):
             if a == 0:
                 outb[J] = ps(tag, [P, D])
@@ -166,7 +174,7 @@ def tile_hetxlhead_pa_v_kernel(
 
         def keep_dpre(J):
             if J in SPLIT:
-                kept[J] = sb("kept", [P, D], F32, 4)
+                kept[J] = sb("kept", [P, D], F32, 1)
                 nc.scalar.copy(out=kept[J][:], in_=dpb[J, KEPT][:])
 
         def times_noise(J, s, cols=slice(0, D)):
@@ -275,7 +283,7 @@ def tile_hetxlhead_pa_v_kernel(
         def warm_up(count):
             bank = ps("dp", [P, D])
             for k in range(count):
-                nc.tensor.matmul(bank[:], lhsT=wc_raw[0][:, 1, 0:P], rhs=wc_raw[0][:, 0, :], start=True, stop=True)
+                nc.tensor.matmul(bank[:], lhsT=raw[0, 0][0][:, 0:P], rhs=raw[0, 0][0][:, 0:D], start=True, stop=True)
 
         def weight_pass(m, g):
             cols = slice(m * P, (m + 1) * P)
@@ -297,21 +305,21 @@ def tile_hetxlhead_pa_v_kernel(
         nc.vector.memset(dummy[:], 0.0)
         nc.scalar.activation(dummy[:], dummy[:], mybir.ActivationFunctionType.Sigmoid)
 
-        wc_raw = [load_w(w_cls[0:512, :])]
         load_g(0, 0, 1)
-        wc_raw.append(load_w(w_cls[512:1024, :]))
+        wc_raw = [load_w(w_cls[0:512, :])]
         load_g(0, 1, 2)
+        wc_raw.append(load_w(w_cls[512:1024, :]))
         load_g(0, 2, 4)
         load_n(0, 0, 2)
         load_g(1, 0, 2)
         load_g(1, 2, 4)
         load_n(0, 2, 4)
         load_g(2, 0, 2)
-        load_n(1)
         load_z(0, 1)
         load_g(2, 2, 4)
-        load_g(3, 0, 2)
+        load_n(1)
         wd_raw = load_w(w_diag)
+        load_g(3, 0, 2)
         load_n(2)
         load_z(1, 1)
         load_g(3, 2, 4)
@@ -332,51 +340,51 @@ def tile_hetxlhead_pa_v_kernel(
 
         on_vector, on_scalar = slice(0, 320), slice(320, D)
         wg = [grouped_w(), grouped_w()]
-        warm_up(3)
-        interleave(nc.vector.tensor_copy, wg[0], wc_raw[0], on_vector)
-        interleave(nc.scalar.copy, wg[0], wc_raw[0], on_scalar)
         prescale(0, 0, 1)
         turn(0, 0)
-        warm_up(2)
-        quant_w(wc[0], wg[0], E4M3)
-        interleave(nc.vector.tensor_copy, wg[1], wc_raw[1], on_vector)
-        interleave(nc.scalar.copy, wg[1], wc_raw[1], on_scalar)
+        warm_up(4)
+        interleave(nc.vector.tensor_copy, wg[0], wc_raw[0], on_vector)
+        interleave(nc.scalar.copy, wg[0], wc_raw[0], on_scalar)
         empty_turn(0, 0, 1)
         prescale(0, 1, 2)
         turn(0, 1)
-        warm_up(1)
-        quant_w(wc[1], wg[1], E4M3)
+        quant_w(wc[0], wg[0], E4M3)
         quant_g(0, 0, 1)
+        first_passes(0, 0)
+        interleave(nc.vector.tensor_copy, wg[1], wc_raw[1], on_vector)
+        interleave(nc.scalar.copy, wg[1], wc_raw[1], on_scalar)
         empty_turn(0, 1, 1)
         prescale(0, 2, 4)
-        dpre(0, 0)
+        quant_w(wc[1], wg[1], E4M3)
+        quant_g(0, 1, 2)
         turn(0, 2)
         turn(0, 3)
-        quant_g(0, 1, 2)
-        direct(0, 0, 1)
+        first_passes(0, 1)
         empty_turn(0, 2)
         empty_turn(0, 3)
-        dpre(0, 1)
-        times_noise(0, 0)
+        first_passes(1, 0)
+        first_passes(1, 1)
         prescale(1, 0, 2)
+        times_noise(0, 0)
         turn(1, 0)
         turn(1, 1)
-        prescale(1, 2, 4)
         quant_g(0, 2, 4)
+        second_half(1)
+        scalar_last(1)
         times_noise(0, 1)
-        direct(0, 1, 2)
         empty_turn(1, 0)
         empty_turn(1, 1)
-        sigmoid(0)
+        scalar_second(2)
         dpre(0, 2)
+        dpre(0, 3)
         turn(1, 2)
         turn(1, 3)
-        dpre(0, 3)
-        prescale(2, 0, 2)
+        times_noise(0, 2)
+        first_half(2)
         empty_turn(1, 2)
         empty_turn(1, 3)
+        sigmoid(0)
         scalar_last(2)
-        times_noise(0, 2)
         quant_g(1, 0, 2)
         times_noise(0, 3)
         keep_dpre(0)
@@ -385,11 +393,10 @@ def tile_hetxlhead_pa_v_kernel(
         turn(2, 1)
         empty_turn(2, 0)
         empty_turn(2, 1)
-        second_half(2)
-        quant_g(1, 2, 4)
         add_pairs(0, nc.vector)
-        first_half(3)
+        quant_g(1, 2, 4)
         add_all(0)
+        second_half(2)
 
         side_jobs = {"wd": (1, 1, 1), "f0": (2.5, 3, 3), "f1": (3.5, 4, 4), "dz": (5, 6, 6)}
         side = {}
@@ -435,8 +442,10 @@ def tile_hetxlhead_pa_v_kernel(
             sigmoid(J)
             scalar_last(J + 2)
             side_copy(J + 0.5)
-            direct(J, 0, 4 if J == LAST - 1 else S if J in SPLIT else 3)
-            if 3 < J + 2 < TILES:
+            if J == LAST - 1:
+                direct(J - 1, 2, S)
+            direct(J, 0, {LAST - 2: 2, LAST - 1: 3}.get(J, S if J in SPLIT else 3))
+            if J + 2 < TILES:
                 first_half(J + 2)
             quant_g(J + 1, 0, 2)
             add_pairs(J, nc.vector)
@@ -448,7 +457,7 @@ def tile_hetxlhead_pa_v_kernel(
                 turn(J + 2, 1)
                 empty_turn(J + 2, 0)
                 empty_turn(J + 2, 1)
-            if J < LAST - 1:
+            if J < LAST - 2:
                 direct(J, S if J in SPLIT else 3, S)
             side_quant(J)
             add_all(J)
@@ -471,7 +480,7 @@ def tile_hetxlhead_pa_v_kernel(
         dz_pass(L - 2)
         empty_out(L - 2)
         store_out(L - 2)
-        direct(L - 1, 4, S)
+        direct(L - 1, 3, S)
         turn_dz(L - 1)
         empty_dz(L - 1)
         keep_dpre(L)

@@ -21,7 +21,7 @@ KEPT = 1
 SPLIT = (7,)
 PAIRS_ON_GPSIMD = ()
 SCALAR_LAST = (1, 2, 3, 6, 7)
-SCALAR_SECOND = (2, 4)
+SCALAR_SECOND = (2,)
 FLOPS = 2 * (B * S * C * D + B * D * D + D * D * B)
 BYTES = 2 * (B * S * C + B * S * D + B * D + D * D + C * D) + 4 * (B * D) + 4 * (B * D + D * D)
 
@@ -39,8 +39,8 @@ def tile_hetxlhead_pa_v_kernel(
         pool = ctx.enter_context(tc.tile_pool(name="sbuf", bufs=1))
         psum = ctx.enter_context(tc.psum_pool(name="psum", bufs=1))
 
-        def sb(tag, shape, dtype, bufs):
-            return pool.tile(shape, dtype, name=tag, tag=tag, bufs=bufs, align_bytes=64)
+        def sb(tag, shape, dtype, bufs, align=64):
+            return pool.tile(shape, dtype, name=tag, tag=tag, bufs=bufs, align_bytes=align)
 
         def ps(tag, shape):
             return psum.tile(shape, F32, name=tag, tag=tag, bufs={"tr": 2, "dp": 4, "out": 2}[tag])
@@ -53,7 +53,7 @@ def tile_hetxlhead_pa_v_kernel(
         prod, part, dstd, sig, dz, dzt_b, dzt, dzc, outb, res = {}, {}, {}, {}, {}, {}, {}, {}, {}, {}
 
         def quantised(tag, cols, bufs):
-            return sb(tag + "_c", [P, cols], U32, bufs), sb(tag + "_s", [P, cols], U8, bufs)
+            return sb(tag + "_c", [P, cols], U32, bufs, 256), sb(tag + "_s", [P, cols], U8, bufs, 256)
 
         def load_g(J, a=0, b=S):
             if b - a == S:

@@ -18,10 +18,11 @@ TEMPERATURE = 1.5
 TILES = B // P
 LAST = TILES - 1
 KEPT = 1
-SPLIT = (7,)
-PAIRS_ON_GPSIMD = ()
-SCALAR_LAST = (1, 2, 3, 6, 7)
-SCALAR_SECOND = (2,)
+VECTOR_COLUMNS = 320
+WARM_UPS = 4
+FEATURES_FROM = 5
+BETWEEN_RUNS = 2
+BEFORE_LAST = 3
 FLOPS = 2 * (B * S * C * D + B * D * D + D * D * B)
 BYTES = 2 * (B * S * C + B * S * D + B * D + D * D + C * D) + 4 * (B * D) + 4 * (B * D + D * D)
 
@@ -48,7 +49,6 @@ def tile_hetxlhead_pa_v_kernel(
         ident = sb("ident", [P, P], F32, 1)
         make_identity(nc, ident[:])
 
-        kept = {}
         raw, noise, zt, gs, trb, grp, cod, dpb = {}, {}, {}, {}, {}, {}, {}, {}
         prod, part, dstd, sig, dz, dzt_b, dzt, dzc, outb, res = {}, {}, {}, {}, {}, {}, {}, {}, {}, {}
 
@@ -98,20 +98,6 @@ def tile_hetxlhead_pa_v_kernel(
         def scalar_prescale(J, a, b):
             dst, src = scale_views(J, a, b)
             nc.scalar.activation(dst, src, mybir.ActivationFunctionType.Copy, scale=1.0 / TEMPERATURE)
-
-        def first_half(J):
-            prescale(J, 0, 1 if J in SCALAR_SECOND else 2)
-
-        def second_half(J):
-            prescale(J, 2, 3 if J in SCALAR_LAST else 4)
-
-        def scalar_last(J):
-            if J in SCALAR_LAST:
-                scalar_prescale(J, 3, 4)
-
-        def scalar_second(J):
-            if J in SCALAR_SECOND:
-                scalar_prescale(J, 1, 2)
 
         def turn(J, s):
             trb[J, s] = ps("tr", [P, 2, 2, P])
@@ -163,19 +149,14 @@ def tile_hetxlhead_pa_v_kernel(
             g_pass(dpb[0, s][:], 0, s, h, h == 0, h == 1)
             g_pass(outb[0][:], 0, s, h, s == 0 and h == 0, False)
 
-        def direct(J, a=0, b=S, tag="out"):
+        def direct(J, a, b):
             if a == 0:
-                outb[J] = ps(tag, [P, D])
+                outb[J] = ps("out", [P, D])
             for s in range(a, b):
-                if s == KEPT and J in SPLIT:
+                if s == KEPT and J == LAST:
                     continue
                 for h in range(2):
                     g_pass(outb[J][:], J, s, h, s == 0 and h == 0, False)
-
-        def keep_dpre(J):
-            if J in SPLIT:
-                kept[J] = sb("kept", [P, D], F32, 1)
-                nc.scalar.copy(out=kept[J][:], in_=dpb[J, KEPT][:])
 
         def times_noise(J, s, cols=slice(0, D)):
             if s == 0:
@@ -184,31 +165,26 @@ def tile_hetxlhead_pa_v_kernel(
                 out=prod[J][:, s % 2, s // 2, cols], in0=dpb[J, s][:, cols], in1=noise[J, s][:, cols], op=MULT
             )
 
-        def add_pairs(J, eng, cols=slice(0, D)):
-            if cols.start == 0:
-                part[J] = sb("mix%d" % ((J + (J in PAIRS_ON_GPSIMD)) % 2), [P, 2, D], F32, 1)
-            eng.tensor_tensor(
-                out=part[J][:, :, cols], in0=prod[J][:, 0, :, cols], in1=prod[J][:, 1, :, cols], op=ADD
-            )
+        def add_pairs(J):
+            part[J] = sb("mix%d" % (J % 2), [P, 2, D], F32, 1)
+            nc.vector.tensor_tensor(out=part[J][:], in0=prod[J][:, 0], in1=prod[J][:, 1], op=ADD)
 
-        def natural(ap, words):
+        def natural(ap, words=slice(0, P)):
             return ap.rearrange("p (w u e) -> p u w e", u=2, e=2)[:, :, words, :]
 
-        def sorted_by_half(ap, words):
+        def sorted_by_half(ap, words=slice(0, P)):
             return ap.rearrange("p (u w e) -> p u w e", u=2, e=2)[:, :, words, :]
 
-        def add_all(J, words=slice(0, P)):
-            if words.start == 0:
-                dstd[J] = sb("dstd", [P, D], F32, 2)
+        def add_all(J):
+            dstd[J] = sb("dstd", [P, D], F32, 2)
             nc.vector.tensor_tensor(
-                out=sorted_by_half(dstd[J][:], words), in0=natural(part[J][:, 0, :], words),
-                in1=natural(part[J][:, 1, :], words), op=ADD,
+                out=sorted_by_half(dstd[J][:]), in0=natural(part[J][:, 0, :]), in1=natural(part[J][:, 1, :]), op=ADD
             )
 
         def sigmoid(J):
             sig[J] = sb("sig", [P, D], F32, 3)
             nc.scalar.activation(
-                sorted_by_half(sig[J][:], slice(0, P)), natural(zt[J], slice(0, P)),
+                sorted_by_half(sig[J][:]), natural(zt[J]),
                 mybir.ActivationFunctionType.Sigmoid,
             )
 
@@ -220,8 +196,8 @@ def tile_hetxlhead_pa_v_kernel(
                 in1=sorted_by_half(sig[J][:], words), op=MULT,
             )
 
-        def turn_dz(J, tag="dp"):
-            dzt_b[J] = ps(tag, [P, 2, P])
+        def turn_dz(J):
+            dzt_b[J] = ps("dp", [P, 2, P])
             words = dz[J // 4][:, J % 4, :].bitcast(F32)
             for u in range(2):
                 nc.tensor.transpose(dzt_b[J][:, u, :], words[:, u * P : (u + 1) * P], ident[:])
@@ -252,8 +228,8 @@ def tile_hetxlhead_pa_v_kernel(
 
         def empty_out(J):
             res[J] = sb("res", [P, D], F32, 4)
-            if J in SPLIT:
-                nc.vector.tensor_tensor(out=res[J][:], in0=outb[J][:], in1=kept[J][:], op=ADD)
+            if J == LAST:
+                nc.vector.tensor_tensor(out=res[J][:], in0=outb[J][:], in1=kept[:], op=ADD)
             else:
                 nc.scalar.copy(out=res[J][:], in_=outb[J][:])
 
@@ -279,11 +255,6 @@ def tile_hetxlhead_pa_v_kernel(
             r = sb("res1", [P, D], F32, 4)
             copy(out=r[:], in_=acc[m][:])
             nc.sync.dma_start(out=out_1[m * P : (m + 1) * P, :], in_=r[:])
-
-        def warm_up(count):
-            bank = ps("dp", [P, D])
-            for k in range(count):
-                nc.tensor.matmul(bank[:], lhsT=raw[0, 0][0][:, 0:P], rhs=raw[0, 0][0][:, 0:D], start=True, stop=True)
 
         def weight_pass(m, g):
             cols = slice(m * P, (m + 1) * P)
@@ -338,11 +309,13 @@ def tile_hetxlhead_pa_v_kernel(
         load_z(6, 2)
         load_n(7)
 
-        on_vector, on_scalar = slice(0, 320), slice(320, D)
+        on_vector, on_scalar = slice(0, VECTOR_COLUMNS), slice(VECTOR_COLUMNS, D)
         wg = [grouped_w(), grouped_w()]
         prescale(0, 0, 1)
         turn(0, 0)
-        warm_up(4)
+        unread = ps("dp", [P, D])
+        for k in range(WARM_UPS):
+            nc.tensor.matmul(unread[:], lhsT=raw[0, 0][0][:, 0:P], rhs=raw[0, 0][0][:, 0:D], start=True, stop=True)
         interleave(nc.vector.tensor_copy, wg[0], wc_raw[0], on_vector)
         interleave(nc.scalar.copy, wg[0], wc_raw[0], on_scalar)
         empty_turn(0, 0, 1)
@@ -369,101 +342,103 @@ def tile_hetxlhead_pa_v_kernel(
         turn(1, 0)
         turn(1, 1)
         quant_g(0, 2, 4)
-        second_half(1)
-        scalar_last(1)
+        prescale(1, 2, 3)
+        scalar_prescale(1, 3, 4)
         times_noise(0, 1)
         empty_turn(1, 0)
         empty_turn(1, 1)
-        scalar_second(2)
+        scalar_prescale(2, 1, 2)
         dpre(0, 2)
         dpre(0, 3)
         turn(1, 2)
         turn(1, 3)
         times_noise(0, 2)
-        first_half(2)
+        prescale(2, 0, 1)
         empty_turn(1, 2)
         empty_turn(1, 3)
         sigmoid(0)
-        scalar_last(2)
         quant_g(1, 0, 2)
         times_noise(0, 3)
-        keep_dpre(0)
         direct(0, 2, S)
         turn(2, 0)
         turn(2, 1)
         empty_turn(2, 0)
         empty_turn(2, 1)
-        add_pairs(0, nc.vector)
+        add_pairs(0)
         quant_g(1, 2, 4)
         add_all(0)
-        second_half(2)
+        prescale(2, 2, 4)
 
-        side_jobs = {"wd": (1, 1, 1), "f0": (2.5, 3, 3), "f1": (3.5, 4, 4), "dz": (5, 6, 6)}
-        side = {}
+        beside = [(wd_raw, wd, E4M3, 2, 2)]
+        beside += [(ft_raw[g], ft[g], E4M3, FEATURES_FROM + 2 * g, FEATURES_FROM + 2 * g + 1) for g in range(2)]
+        beside += [(None, dzq[0], E5M2, 2 * (LAST - 2), 2 * (LAST - 1))]
+        grouped = {}
 
-        def side_copy(J):
-            for name, halves in side_jobs.items():
-                for cols, step in zip((left, right), halves):
-                    if step == J:
+        def slot_is_free(slot):
+            return all(slot not in job[3:] for job in beside)
+
+        def fill_slot(slot):
+            for k, job in enumerate(beside):
+                for cols, at in zip((left, right), job[3:]):
+                    if at == slot:
                         if cols.start == 0:
-                            side[name] = grouped_w()
-                        if name == "dz":
-                            interleave_dz(nc.scalar.copy, side[name], dz[0], cols)
+                            grouped[k] = grouped_w()
+                        if job[0] is None:
+                            interleave_dz(nc.scalar.copy, grouped[k], dz[0], cols)
                         else:
-                            src = {"wd": wd_raw, "f0": ft_raw[0], "f1": ft_raw[1]}[name]
-                            interleave(nc.scalar.copy, side[name], src, cols)
+                            interleave(nc.scalar.copy, grouped[k], job[0], cols)
 
-        def side_quant(J):
-            for name, halves in side_jobs.items():
-                if halves[2] == J:
-                    pair = {"wd": wd, "f0": ft[0], "f1": ft[1], "dz": dzq[0]}[name]
-                    quant_w(pair, side[name], E5M2 if name == "dz" else E4M3)
+        def quant_beside(J):
+            for k, job in enumerate(beside):
+                if job[4] // 2 == J:
+                    quant_w(job[1], grouped[k], job[2])
 
         for J in range(1, LAST):
-            side_copy(J)
-            scalar_second(J + 2)
-            dpre(J, 0)
-            times_noise(J, 0)
-            make_dz(J - 1, nc.gpsimd)
-            dpre(J, 1)
-            times_noise(J, 1)
-            dpre(J, 2)
-            times_noise(J, 2)
-            if J >= 2:
-                dz_pass(J - 2)
-                empty_out(J - 2)
-            dpre(J, 3)
-            times_noise(J, 3)
+            more = J + 2 < TILES
+            shared = more and slot_is_free(2 * J + 1)
+            fill_slot(2 * J)
+            for s in range(S):
+                dpre(J, s)
+                times_noise(J, s)
+                if s == 0:
+                    make_dz(J - 1, nc.gpsimd)
+                if s == 2 and J >= 2:
+                    dz_pass(J - 2)
+                    empty_out(J - 2)
             turn(J + 1, 2)
             turn(J + 1, 3)
             empty_turn(J + 1, 2)
             empty_turn(J + 1, 3)
-            keep_dpre(J)
             sigmoid(J)
-            scalar_last(J + 2)
-            side_copy(J + 0.5)
-            if J == LAST - 1:
-                direct(J - 1, 2, S)
-            direct(J, 0, {LAST - 2: 2, LAST - 1: 3}.get(J, S if J in SPLIT else 3))
-            if J + 2 < TILES:
-                first_half(J + 2)
-            quant_g(J + 1, 0, 2)
-            add_pairs(J, nc.vector)
-            quant_g(J + 1, 2, 4)
+            if more:
+                direct(J, 0, BETWEEN_RUNS)
+                prescale(J + 2, 0, 2)
+            else:
+                direct(J - 1, BETWEEN_RUNS, S)
             turn_dz(J - 1)
             empty_dz(J - 1)
-            if J + 2 < TILES:
+            if shared:
+                scalar_prescale(J + 2, 3, 4)
+            fill_slot(2 * J + 1)
+            quant_g(J + 1, 0, 2)
+            add_pairs(J)
+            quant_g(J + 1, 2, 4)
+            if more:
                 turn(J + 2, 0)
                 turn(J + 2, 1)
                 empty_turn(J + 2, 0)
                 empty_turn(J + 2, 1)
-            if J < LAST - 2:
-                direct(J, S if J in SPLIT else 3, S)
-            side_quant(J)
-            add_all(J)
-            quant_dz(J - 1)
-            if J + 2 < TILES:
-                second_half(J + 2)
+                if J + 3 < TILES:
+                    direct(J, BETWEEN_RUNS, S)
+                quant_beside(J)
+                quant_dz(J - 1)
+                add_all(J)
+                prescale(J + 2, 2, 3 if shared else 4)
+            else:
+                direct(J, 0, BEFORE_LAST)
+                add_all(J)
+                quant_dz(J - 1)
+                quant_beside(J)
             if J >= 4:
                 store_out(J - 4)
         store_out(LAST - 4)
@@ -480,10 +455,11 @@ def tile_hetxlhead_pa_v_kernel(
         dz_pass(L - 2)
         empty_out(L - 2)
         store_out(L - 2)
-        direct(L - 1, 3, S)
+        direct(L - 1, BEFORE_LAST, S)
         turn_dz(L - 1)
         empty_dz(L - 1)
-        keep_dpre(L)
+        kept = sb("kept", [P, D], F32, 1)
+        nc.scalar.copy(out=kept[:], in_=dpb[L, KEPT][:])
         acc = [ps("tr", [P, D]), ps("tr", [P, D])]
         weight_pass(0, 0)
         weight_pass(1, 0)
@@ -506,18 +482,18 @@ def tile_hetxlhead_pa_v_kernel(
         running(0, 0)
         times_noise(L, 3, left)
         running(1, 0)
-        quant_dz(L - 1)
-        dz_pass(L - 1)
-        empty_out(L - 1)
-        store_out(L - 1)
-        direct(L, 3, S)
         running(0, 1)
+        quant_dz(L - 1)
+        direct(L, 3, S)
+        dz_pass(L - 1)
         running(2, 0)
         times_noise(L, 3, right)
         make_dz(L, nc.vector, halves[0])
         running(1, 1)
         interleave_dz(nc.vector.tensor_copy, t, dz[1], quarter[0])
         interleave_dz(nc.scalar.copy, t, dz[1], quarter[1])
+        empty_out(L - 1)
+        store_out(L - 1)
         running(2, 1)
         quant_w(dzq[1], t, E5M2, quarter[0])
         acc += [ps("dp", [P, D]), ps("dp", [P, D])]

@@ -17,12 +17,11 @@ B, S, D, C = 1024, 4, 512, 1024
 TEMPERATURE = 1.5
 TILES = B // P
 LAST = TILES - 1
-KEPT = 1
 VECTOR_COLUMNS = 320
 WARM_UPS = 4
-FEATURES_FROM = 5
-BETWEEN_RUNS = 2
-BEFORE_LAST = 3
+UNITS = 2 * S
+SCALAR_UNITS = 5
+ROTATING, SUMS = 5, 3
 FLOPS = 2 * (B * S * C * D + B * D * D + D * D * B)
 BYTES = 2 * (B * S * C + B * S * D + B * D + D * D + C * D) + 4 * (B * D) + 4 * (B * D + D * D)
 
@@ -43,14 +42,26 @@ def tile_hetxlhead_pa_v_kernel(
         def sb(tag, shape, dtype, bufs, align=64):
             return pool.tile(shape, dtype, name=tag, tag=tag, bufs=bufs, align_bytes=align)
 
-        def ps(tag, shape):
-            return psum.tile(shape, F32, name=tag, tag=tag, bufs={"tr": 2, "dp": 4, "out": 2}[tag])
+        turns, bank_of = [], {}
+
+        def in_bank(k, key, shape):
+            bank_of[key] = k
+            return psum.tile(shape, F32, name="bank%d" % k, tag="bank%d" % k, bufs=1)
+
+        def rotating(key, shape):
+            turns.append(key)
+            return in_bank((len(turns) - 1) % ROTATING, key, shape)
+
+        def summing(J):
+            return in_bank(ROTATING + J % SUMS, ("sum", J), [P, D])
 
         ident = sb("ident", [P, P], F32, 1)
         make_identity(nc, ident[:])
 
         raw, noise, zt, gs, trb, grp, cod, dpb = {}, {}, {}, {}, {}, {}, {}, {}
         prod, part, dstd, sig, dz, dzt_b, dzt, dzc, outb, res = {}, {}, {}, {}, {}, {}, {}, {}, {}, {}
+
+        noise_tile = {}
 
         def quantised(tag, cols, bufs):
             return sb(tag + "_c", [P, cols], U32, bufs, 256), sb(tag + "_s", [P, cols], U8, bufs, 256)
@@ -70,6 +81,7 @@ def tile_hetxlhead_pa_v_kernel(
             else:
                 t = sb("noise%d_%d" % (J, a), [P, b - a, D], BF16, 1)
             nc.sync.dma_start(out=t[:], in_=n_view[J // 4, J % 4][:, a:b, :])
+            noise_tile[J] = t
             for s in range(a, b):
                 noise[J, s] = t[:, s - a, :]
 
@@ -84,43 +96,41 @@ def tile_hetxlhead_pa_v_kernel(
             nc.sync.dma_start(out=t[:], in_=src.rearrange("(p j) w -> p j w", j=4))
             return t
 
-        def scale_views(J, a, b):
-            t = sb("gs", [P, 2, 256 * (b - a), 2], BF16, 6)
-            for s in range(a, b):
-                gs[J, s] = (t, s - a, b - a)
-            src, at = raw[J, a]
-            return t[:], src[:, C * at : C * (at + b - a)].rearrange("p (q u e) -> p u q e", u=2, e=2)
+        def scale_views(J, a, b, tag):
+            t = sb(tag, [P, 2, P * (b - a), 2], BF16, 3)
+            for k in range(a, b):
+                gs[J, k] = (t, k - a, b - a)
+            src, at = raw[J, a // 2]
+            first = C * at + (a % 2) * C // 2
+            return t[:], src[:, first : first + (b - a) * C // 2].rearrange("p (q u e) -> p u q e", u=2, e=2)
 
         def prescale(J, a, b):
-            dst, src = scale_views(J, a, b)
+            dst, src = scale_views(J, a, b, "gs")
             nc.vector.tensor_scalar(out=dst, in0=src, scalar1=1.0 / TEMPERATURE, scalar2=None, op0=MULT)
 
         def scalar_prescale(J, a, b):
-            dst, src = scale_views(J, a, b)
+            dst, src = scale_views(J, a, b, "gs_scalar")
             nc.scalar.activation(dst, src, mybir.ActivationFunctionType.Copy, scale=1.0 / TEMPERATURE)
 
         def turn(J, s):
-            trb[J, s] = ps("tr", [P, 2, 2, P])
-            t, at, count = gs[J, s]
-            words = t[:].rearrange("p u q e -> p (u q e)").bitcast(F32)
+            trb[J, s] = rotating(("turn", J, s), [P, 2, 2, P])
             for h in range(2):
+                t, at, count = gs[J, 2 * s + h]
+                words = t[:].rearrange("p u q e -> p (u q e)").bitcast(F32)
                 for u in range(2):
-                    a = u * 256 * count + at * 256 + h * P
+                    a = (u * count + at) * P
                     nc.tensor.transpose(trb[J, s][:, h, u, :], words[:, a : a + P], ident[:])
 
         def empty_turn(J, s, count=2):
             at = s % count
             if at == 0:
-                if s == 2:
-                    t = sb("mix%d" % (J % 2), [P, count, 2, P, 2], F32, 1)
-                else:
-                    t = sb("grp", [P, count, 2, P, 2], F32, 2)
+                t = sb("grp", [P, count, 2, P, 2], F32, 3)
                 for k in range(count):
                     grp[J, s + k] = t
             nc.scalar.copy(out=grp[J, s][:, at], in_=trb[J, s][:].rearrange("p h u r -> p h r u"))
 
         def quant_g(J, a, b):
-            codes, scales = quantised("g", 256 * (b - a), 7)
+            codes, scales = quantised("g", 256 * (b - a), 5)
             nc.vector.quantize_mx(
                 out=codes[:].bitcast(E5M2), scales=scales[:],
                 in_=grp[J, a][:].rearrange("p s h r u -> p (s h r u)").bitcast(BF16),
@@ -128,46 +138,47 @@ def tile_hetxlhead_pa_v_kernel(
             for s in range(a, b):
                 cod[J, s] = (codes, scales, s - a)
 
-        def g_pass(out, J, s, h, start, stop):
+        def g_pass(out, J, s, h, start, stop, moving=slice(0, D)):
             codes, scales, at = cod[J, s]
             cols = slice((at * 2 + h) * P, (at * 2 + h + 1) * P)
             nc.tensor.matmul_mx(
                 out=out, lhsT=codes[:, cols].bitcast(E5M2), lhsT_scale=scales[:, cols],
-                rhs=wc[h][0][:].bitcast(E4M3), rhs_scale=wc[h][1][:], start=start, stop=stop,
+                rhs=wc[h][0][:, moving].bitcast(E4M3), rhs_scale=wc[h][1][:, moving], start=start, stop=stop,
             )
 
         def dpre(J, s):
-            dpb[J, s] = ps("dp", [P, D])
+            dpb[J, s] = rotating(("dpre", J, s), [P, D])
             for h in range(2):
                 g_pass(dpb[J, s][:], J, s, h, h == 0, h == 1)
 
         def first_passes(s, h):
             if h == 0:
-                dpb[0, s] = ps("dp", [P, D])
+                dpb[0, s] = rotating(("dpre", 0, s), [P, D])
                 if s == 0:
-                    outb[0] = ps("out", [P, D])
+                    outb[0] = summing(0)
             g_pass(dpb[0, s][:], 0, s, h, h == 0, h == 1)
             g_pass(outb[0][:], 0, s, h, s == 0 and h == 0, False)
 
         def direct(J, a, b):
             if a == 0:
-                outb[J] = ps("out", [P, D])
+                outb[J] = summing(J)
             for s in range(a, b):
-                if s == KEPT and J == LAST:
-                    continue
                 for h in range(2):
                     g_pass(outb[J][:], J, s, h, s == 0 and h == 0, False)
 
         def times_noise(J, s, cols=slice(0, D)):
-            if s == 0:
+            if s == 0 and cols.start == 0:
                 prod[J] = sb("prod", [P, 2, 2, D], F32, 2)
             nc.vector.tensor_tensor(
                 out=prod[J][:, s % 2, s // 2, cols], in0=dpb[J, s][:, cols], in1=noise[J, s][:, cols], op=MULT
             )
 
-        def add_pairs(J):
-            part[J] = sb("mix%d" % (J % 2), [P, 2, D], F32, 1)
-            nc.vector.tensor_tensor(out=part[J][:], in0=prod[J][:, 0], in1=prod[J][:, 1], op=ADD)
+        def add_pairs(J, cols=slice(0, D)):
+            if cols.start == 0:
+                part[J] = sb("part", [P, 2, D], F32, 1)
+            nc.vector.tensor_tensor(
+                out=part[J][:, :, cols], in0=prod[J][:, 0, :, cols], in1=prod[J][:, 1, :, cols], op=ADD
+            )
 
         def natural(ap, words=slice(0, P)):
             return ap.rearrange("p (w u e) -> p u w e", u=2, e=2)[:, :, words, :]
@@ -175,10 +186,12 @@ def tile_hetxlhead_pa_v_kernel(
         def sorted_by_half(ap, words=slice(0, P)):
             return ap.rearrange("p (u w e) -> p u w e", u=2, e=2)[:, :, words, :]
 
-        def add_all(J):
-            dstd[J] = sb("dstd", [P, D], F32, 2)
+        def add_all(J, words=slice(0, P)):
+            if words.start == 0:
+                dstd[J] = sb("dstd", [P, D], F32, 2)
             nc.vector.tensor_tensor(
-                out=sorted_by_half(dstd[J][:]), in0=natural(part[J][:, 0, :]), in1=natural(part[J][:, 1, :]), op=ADD
+                out=sorted_by_half(dstd[J][:], words), in0=natural(part[J][:, 0, :], words),
+                in1=natural(part[J][:, 1, :], words), op=ADD,
             )
 
         def sigmoid(J):
@@ -196,8 +209,11 @@ def tile_hetxlhead_pa_v_kernel(
                 in1=sorted_by_half(sig[J][:], words), op=MULT,
             )
 
-        def turn_dz(J):
-            dzt_b[J] = ps("dp", [P, 2, P])
+        def turn_dz(J, bank=None):
+            if bank is None:
+                dzt_b[J] = rotating(("dz", J), [P, 2, P])
+            else:
+                dzt_b[J] = in_bank(bank, ("dz", J), [P, 2, P])
             words = dz[J // 4][:, J % 4, :].bitcast(F32)
             for u in range(2):
                 nc.tensor.transpose(dzt_b[J][:, u, :], words[:, u * P : (u + 1) * P], ident[:])
@@ -226,12 +242,9 @@ def tile_hetxlhead_pa_v_kernel(
                 rhs=wd[0][:].bitcast(E4M3), rhs_scale=wd[1][:], start=False, stop=True,
             )
 
-        def empty_out(J):
+        def empty_out(J, copy=nc.scalar.copy):
             res[J] = sb("res", [P, D], F32, 4)
-            if J == LAST:
-                nc.vector.tensor_tensor(out=res[J][:], in0=outb[J][:], in1=kept[:], op=ADD)
-            else:
-                nc.scalar.copy(out=res[J][:], in_=outb[J][:])
+            copy(out=res[J][:], in_=outb[J][:])
 
         def store_out(J):
             nc.sync.dma_start(out=o_view[J // 4, J % 4], in_=res[J][:])
@@ -269,7 +282,7 @@ def tile_hetxlhead_pa_v_kernel(
         dzq = [quantised("dz0", D, 1), quantised("dz1", D, 1)]
         left, right = slice(0, D // 2), slice(D // 2, D)
         quarter = [slice(m * P, (m + 1) * P) for m in range(4)]
-        acc = []
+        acc = {}
         ctx.enter_context(tc.manual_schedule())
 
         dummy = sb("dummy", [P, 1], F32, 1)
@@ -283,26 +296,25 @@ def tile_hetxlhead_pa_v_kernel(
         load_g(0, 2, 4)
         load_n(0, 0, 2)
         load_g(1, 0, 2)
-        load_g(1, 2, 4)
         load_n(0, 2, 4)
+        load_g(1, 2, 4)
         load_g(2, 0, 2)
-        load_z(0, 1)
         load_g(2, 2, 4)
+        load_z(0, 1)
         load_n(1)
         wd_raw = load_w(w_diag)
-        load_g(3, 0, 2)
-        load_n(2)
+        load_g(3)
         load_z(1, 1)
-        load_g(3, 2, 4)
+        load_n(2)
         load_g(4)
         ft_raw = [load_w(features[0:512, :])]
         load_z(2, 2)
         load_n(3)
         load_g(5)
-        ft_raw.append(load_w(features[512:1024, :]))
         load_n(4)
-        load_z(4, 2)
+        ft_raw.append(load_w(features[512:1024, :]))
         load_g(6)
+        load_z(4, 2)
         load_n(5)
         load_g(7)
         load_n(6)
@@ -311,15 +323,15 @@ def tile_hetxlhead_pa_v_kernel(
 
         on_vector, on_scalar = slice(0, VECTOR_COLUMNS), slice(VECTOR_COLUMNS, D)
         wg = [grouped_w(), grouped_w()]
-        prescale(0, 0, 1)
+        prescale(0, 0, 2)
         turn(0, 0)
-        unread = ps("dp", [P, D])
+        unread = rotating("unread", [P, D])
         for k in range(WARM_UPS):
             nc.tensor.matmul(unread[:], lhsT=raw[0, 0][0][:, 0:P], rhs=raw[0, 0][0][:, 0:D], start=True, stop=True)
         interleave(nc.vector.tensor_copy, wg[0], wc_raw[0], on_vector)
         interleave(nc.scalar.copy, wg[0], wc_raw[0], on_scalar)
         empty_turn(0, 0, 1)
-        prescale(0, 1, 2)
+        prescale(0, 2, 4)
         turn(0, 1)
         quant_w(wc[0], wg[0], E4M3)
         quant_g(0, 0, 1)
@@ -327,7 +339,7 @@ def tile_hetxlhead_pa_v_kernel(
         interleave(nc.vector.tensor_copy, wg[1], wc_raw[1], on_vector)
         interleave(nc.scalar.copy, wg[1], wc_raw[1], on_scalar)
         empty_turn(0, 1, 1)
-        prescale(0, 2, 4)
+        prescale(0, 4, 8)
         quant_w(wc[1], wg[1], E4M3)
         quant_g(0, 1, 2)
         turn(0, 2)
@@ -337,108 +349,87 @@ def tile_hetxlhead_pa_v_kernel(
         empty_turn(0, 3)
         first_passes(1, 0)
         first_passes(1, 1)
-        prescale(1, 0, 2)
+        prescale(1, 0, 4)
         times_noise(0, 0)
         turn(1, 0)
         turn(1, 1)
         quant_g(0, 2, 4)
-        prescale(1, 2, 3)
-        scalar_prescale(1, 3, 4)
         times_noise(0, 1)
+        prescale(1, 4, 6)
+        scalar_prescale(1, 6, 8)
         empty_turn(1, 0)
         empty_turn(1, 1)
-        scalar_prescale(2, 1, 2)
         dpre(0, 2)
         dpre(0, 3)
         turn(1, 2)
         turn(1, 3)
         times_noise(0, 2)
-        prescale(2, 0, 1)
+        scalar_prescale(2, 2, 4)
         empty_turn(1, 2)
         empty_turn(1, 3)
-        sigmoid(0)
         quant_g(1, 0, 2)
         times_noise(0, 3)
+        prescale(2, 0, 2)
         direct(0, 2, S)
-        turn(2, 0)
-        turn(2, 1)
-        empty_turn(2, 0)
-        empty_turn(2, 1)
+        prescale(2, 4, 8)
+        sigmoid(0)
         add_pairs(0)
         quant_g(1, 2, 4)
         add_all(0)
-        prescale(2, 2, 4)
 
-        beside = [(wd_raw, wd, E4M3, 2, 2)]
-        beside += [(ft_raw[g], ft[g], E4M3, FEATURES_FROM + 2 * g, FEATURES_FROM + 2 * g + 1) for g in range(2)]
-        beside += [(None, dzq[0], E5M2, 2 * (LAST - 2), 2 * (LAST - 1))]
         grouped = {}
+        beside = [(wd_raw, wd, E4M3), (ft_raw[0], ft[0], E4M3), (ft_raw[1], ft[1], E4M3), (None, dzq[0], E5M2)]
 
-        def slot_is_free(slot):
-            return all(slot not in job[3:] for job in beside)
+        def side_half(n):
+            k, cols = n // 2, (left, right)[n % 2]
+            if n % 2 == 0:
+                grouped[k] = grouped_w()
+            if beside[k][0] is None:
+                interleave_dz(nc.scalar.copy, grouped[k], dz[0], cols)
+            else:
+                interleave(nc.scalar.copy, grouped[k], beside[k][0], cols)
 
-        def fill_slot(slot):
-            for k, job in enumerate(beside):
-                for cols, at in zip((left, right), job[3:]):
-                    if at == slot:
-                        if cols.start == 0:
-                            grouped[k] = grouped_w()
-                        if job[0] is None:
-                            interleave_dz(nc.scalar.copy, grouped[k], dz[0], cols)
-                        else:
-                            interleave(nc.scalar.copy, grouped[k], job[0], cols)
+        def side_quant(k):
+            quant_w(beside[k][1], grouped[k], beside[k][2])
 
-        def quant_beside(J):
-            for k, job in enumerate(beside):
-                if job[4] // 2 == J:
-                    quant_w(job[1], grouped[k], job[2])
-
+        for s in range(S):
+            turn(2, s)
+            empty_turn(2, s)
+        done = 0
         for J in range(1, LAST):
             more = J + 2 < TILES
-            shared = more and slot_is_free(2 * J + 1)
-            fill_slot(2 * J)
+            count = 1 + J % 2 if more else 0
             for s in range(S):
                 dpre(J, s)
                 times_noise(J, s)
                 if s == 0:
                     make_dz(J - 1, nc.gpsimd)
-                if s == 2 and J >= 2:
-                    dz_pass(J - 2)
-                    empty_out(J - 2)
-            turn(J + 1, 2)
-            turn(J + 1, 3)
-            empty_turn(J + 1, 2)
-            empty_turn(J + 1, 3)
-            sigmoid(J)
+            if J >= 2:
+                quant_dz(J - 2)
             if more:
-                direct(J, 0, BETWEEN_RUNS)
-                prescale(J + 2, 0, 2)
-            else:
-                direct(J - 1, BETWEEN_RUNS, S)
-            turn_dz(J - 1)
-            empty_dz(J - 1)
-            if shared:
-                scalar_prescale(J + 2, 3, 4)
-            fill_slot(2 * J + 1)
+                split = UNITS - (SCALAR_UNITS - 2 * count)
+                prescale(J + 2, 0, split)
+                scalar_prescale(J + 2, split, UNITS)
+            sigmoid(J)
+            for n in range(done, done + count):
+                side_half(n)
+            direct(J, 0, S)
+            if J >= 2:
+                dz_pass(J - 2)
+                empty_out(J - 2)
             quant_g(J + 1, 0, 2)
             add_pairs(J)
             quant_g(J + 1, 2, 4)
+            add_all(J)
+            if more and (done + count) // 2 > done // 2 and J + 3 < TILES:
+                side_quant(done // 2)
+            done += count
+            turn_dz(J - 1)
+            empty_dz(J - 1)
             if more:
-                turn(J + 2, 0)
-                turn(J + 2, 1)
-                empty_turn(J + 2, 0)
-                empty_turn(J + 2, 1)
-                if J + 3 < TILES:
-                    direct(J, BETWEEN_RUNS, S)
-                quant_beside(J)
-                quant_dz(J - 1)
-                add_all(J)
-                prescale(J + 2, 2, 3 if shared else 4)
-            else:
-                direct(J, 0, BEFORE_LAST)
-                add_all(J)
-                quant_dz(J - 1)
-                quant_beside(J)
+                for s in range(S):
+                    turn(J + 2, s)
+                    empty_turn(J + 2, s)
             if J >= 4:
                 store_out(J - 4)
         store_out(LAST - 4)
@@ -446,76 +437,78 @@ def tile_hetxlhead_pa_v_kernel(
 
         L = LAST
         halves = (slice(0, P // 2), slice(P // 2, P))
-        make_dz(L - 1, nc.vector)
+        side_quant(3)
         sigmoid(L)
-        for s in range(S):
-            dpre(L, s)
-            if s < S - 1:
-                times_noise(L, s)
+        last = {}
+        prod[L] = sb("prod", [P, 2, 2, D], F32, 2)
+
+        def last_dpre(half, pair):
+            last[half, pair] = rotating(("last", half, pair), [P, 2, D // 2])
+            for k in range(2):
+                for h in range(2):
+                    g_pass(last[half, pair][:, k, :], L, 2 * pair + k, h, h == 0, h == 1, (left, right)[half])
+
+        def last_times_noise(half, pair):
+            cols = (left, right)[half]
+            nc.vector.tensor_tensor(
+                out=prod[L][:, :, pair, cols], in0=last[half, pair][:],
+                in1=noise_tile[L][:, 2 * pair : 2 * pair + 2, cols], op=MULT,
+            )
+
+        def open_weight(m, key):
+            acc[m] = in_bank(bank_of[key], ("weight", m), [P, D])
+            weight_pass(m, 0)
+
+        quant_dz(L - 2)
+        for half in range(2):
+            for pair in range(2):
+                last_dpre(half, pair)
+        last_times_noise(0, 0)
+        make_dz(L - 1, nc.gpsimd)
+        last_times_noise(0, 1)
+        last_times_noise(1, 0)
         dz_pass(L - 2)
         empty_out(L - 2)
         store_out(L - 2)
-        direct(L - 1, BEFORE_LAST, S)
-        turn_dz(L - 1)
+        direct(L, 0, 1)
+        turn_dz(L - 1, bank_of["last", 0, 0])
         empty_dz(L - 1)
-        kept = sb("kept", [P, D], F32, 1)
-        nc.scalar.copy(out=kept[:], in_=dpb[L, KEPT][:])
-        acc = [ps("tr", [P, D]), ps("tr", [P, D])]
-        weight_pass(0, 0)
-        weight_pass(1, 0)
-        direct(L, 0, 3)
-        part[L] = sb("mix1", [P, 2, D], F32, 1)
-        dstd[L] = sb("dstd", [P, D], F32, 2)
-        t = grouped_w()
-
-        def running(step, half):
-            cols = (left, right)[half]
-            if step == 0:
-                ins, out = (prod[L][:, 0, 0, cols], prod[L][:, 1, 0, cols]), part[L][:, 0, cols]
-            elif step == 1:
-                ins, out = (part[L][:, 0, cols], prod[L][:, 0, 1, cols]), part[L][:, 1, cols]
-            else:
-                ins = (natural(part[L][:, 1, :], halves[half]), natural(prod[L][:, 1, 1, :], halves[half]))
-                out = sorted_by_half(dstd[L][:], halves[half])
-            nc.vector.tensor_tensor(out=out, in0=ins[0], in1=ins[1], op=ADD)
-
-        running(0, 0)
-        times_noise(L, 3, left)
-        running(1, 0)
-        running(0, 1)
+        direct(L, 1, S)
+        add_pairs(L, left)
+        last_times_noise(1, 1)
+        add_all(L, halves[0])
         quant_dz(L - 1)
-        direct(L, 3, S)
         dz_pass(L - 1)
-        running(2, 0)
-        times_noise(L, 3, right)
+        open_weight(0, ("dz", L - 2))
+        open_weight(1, ("last", 0, 1))
         make_dz(L, nc.vector, halves[0])
-        running(1, 1)
+        t = grouped_w()
+        add_pairs(L, right)
         interleave_dz(nc.vector.tensor_copy, t, dz[1], quarter[0])
         interleave_dz(nc.scalar.copy, t, dz[1], quarter[1])
         empty_out(L - 1)
         store_out(L - 1)
-        running(2, 1)
+        add_all(L, halves[1])
         quant_w(dzq[1], t, E5M2, quarter[0])
-        acc += [ps("dp", [P, D]), ps("dp", [P, D])]
-        weight_pass(2, 0)
-        weight_pass(3, 0)
-        weight_pass(0, 1)
-        make_dz(L, nc.vector, halves[1])
         quant_w(dzq[1], t, E5M2, quarter[1])
-        turn_dz(L)
+        make_dz(L, nc.vector, halves[1])
+        open_weight(2, ("last", 1, 0))
+        weight_pass(0, 1)
         weight_pass(1, 1)
         store_weight(0, nc.scalar.copy)
+        turn_dz(L, bank_of["last", 0, 0])
         empty_dz(L)
+        open_weight(3, ("last", 1, 1))
         interleave_dz(nc.vector.tensor_copy, t, dz[1], quarter[2])
         interleave_dz(nc.vector.tensor_copy, t, dz[1], quarter[3])
         quant_w(dzq[1], t, E5M2, quarter[2])
         weight_pass(2, 1)
         store_weight(1, nc.scalar.copy)
         quant_w(dzq[1], t, E5M2, quarter[3])
-        weight_pass(3, 1)
         quant_dz(L)
+        weight_pass(3, 1)
         dz_pass(L)
         store_weight(2, nc.vector.tensor_copy)
         store_weight(3, nc.scalar.copy)
-        empty_out(L)
+        empty_out(L, nc.vector.tensor_copy)
         store_out(L)

@@ -21,6 +21,7 @@ VECTOR_COLUMNS = 320
 WARM_UPS = 4
 UNITS = 2 * S
 SCALAR_UNITS = 5
+RUN = 8
 ROTATING, SUMS = 5, 3
 FLOPS = 2 * (B * S * C * D + B * D * D + D * D * B)
 BYTES = 2 * (B * S * C + B * S * D + B * D + D * D + C * D) + 4 * (B * D) + 4 * (B * D + D * D)
@@ -96,13 +97,20 @@ def tile_hetxlhead_pa_v_kernel(
             nc.sync.dma_start(out=t[:], in_=src.rearrange("(p j) w -> p j w", j=4))
             return t
 
+        def load_classes(src):
+            t = sb("wraw", [P, 4, D], BF16, 3)
+            rows = src.rearrange("(a u b e) w -> u a b (e w)", u=2, b=RUN // 2, e=2)
+            for u in range(2):
+                nc.sync.dma_start(out=t[:, 2 * u : 2 * u + 2, :].rearrange("p e w -> p (e w)"), in_=rows[u])
+            return t
+
         def scale_views(J, a, b, tag):
-            t = sb(tag, [P, 2, P * (b - a), 2], BF16, 3)
+            t = sb(tag, [P, 2, 2 * P * (b - a) // RUN, RUN], BF16, 3)
             for k in range(a, b):
                 gs[J, k] = (t, k - a, b - a)
             src, at = raw[J, a // 2]
             first = C * at + (a % 2) * C // 2
-            return t[:], src[:, first : first + (b - a) * C // 2].rearrange("p (q u e) -> p u q e", u=2, e=2)
+            return t[:], src[:, first : first + (b - a) * C // 2].rearrange("p (q u e) -> p u q e", u=2, e=RUN)
 
         def prescale(J, a, b):
             dst, src = scale_views(J, a, b, "gs")
@@ -290,9 +298,9 @@ def tile_hetxlhead_pa_v_kernel(
         nc.scalar.activation(dummy[:], dummy[:], mybir.ActivationFunctionType.Sigmoid)
 
         load_g(0, 0, 1)
-        wc_raw = [load_w(w_cls[0:512, :])]
+        wc_raw = [load_classes(w_cls[0:512, :])]
         load_g(0, 1, 2)
-        wc_raw.append(load_w(w_cls[512:1024, :]))
+        wc_raw.append(load_classes(w_cls[512:1024, :]))
         load_g(0, 2, 4)
         load_n(0, 0, 2)
         load_g(1, 0, 2)

@@ -17,11 +17,14 @@ B, S, D, C = 1024, 4, 512, 1024
 TEMPERATURE = 1.5
 TILES = B // P
 LAST = TILES - 1
+PAIRS = 2 * TILES
+RUN = 8
 VECTOR_COLUMNS = 320
 WARM_UPS = 4
-UNITS = 2 * S
-SCALAR_UNITS = 5
-RUN = 8
+UNITS = 8
+VECTOR_UNITS = 6
+GPSIMD_COLUMNS = 384
+KEPT = 2
 ROTATING, SUMS = 5, 3
 FLOPS = 2 * (B * S * C * D + B * D * D + D * D * B)
 BYTES = 2 * (B * S * C + B * S * D + B * D + D * D + C * D) + 4 * (B * D) + 4 * (B * D + D * D)
@@ -31,10 +34,11 @@ def tile_hetxlhead_pa_v_kernel(
     tc, features, w_diag, b_diag, w_cls, b_cls, noise_diag, lr_samples, z, grad_out, out_0, out_1
 ):
     nc = tc.nc
-    g_view = grad_out.rearrange("(g p j) s c -> g j p s c", p=P, j=4)
-    n_view = noise_diag.rearrange("(g p j) s d -> g j p s d", p=P, j=4)
+    g_view = grad_out.rearrange("(g p j) s c -> g p (j s c)", p=P, j=4)
+    n_view = noise_diag.rearrange("(g p j) s d -> g p (j s d)", p=P, j=4)
     z_view = z.rearrange("(g p j) d -> g p j d", p=P, j=4)
     o_view = out_0.rearrange("(g p j) d -> g j p d", p=P, j=4)
+    w_view = out_1.rearrange("(h a u e) n -> u h a e n", h=2, u=2, e=RUN)
 
     with ExitStack() as ctx:
         pool = ctx.enter_context(tc.tile_pool(name="sbuf", bufs=1))
@@ -60,31 +64,32 @@ def tile_hetxlhead_pa_v_kernel(
         make_identity(nc, ident[:])
 
         raw, noise, zt, gs, trb, grp, cod, dpb = {}, {}, {}, {}, {}, {}, {}, {}
-        prod, part, dstd, sig, dz, dzt_b, dzt, dzc, outb, res = {}, {}, {}, {}, {}, {}, {}, {}, {}, {}
+        prod, part, dstd, sig, dz, dzt_b, dzt, dzc, outb, res, acc = {}, {}, {}, {}, {}, {}, {}, {}, {}, {}, {}
 
-        noise_tile = {}
+        kept = {}
 
         def quantised(tag, cols, bufs):
             return sb(tag + "_c", [P, cols], U32, bufs, 256), sb(tag + "_s", [P, cols], U8, bufs, 256)
 
-        def load_g(J, a=0, b=S):
-            if b - a == S:
-                t = sb("raw", [P, S * C], BF16, 3)
-            else:
-                t = sb("raw_part", [P, (b - a) * C], BF16, 5)
-            nc.sync.dma_start(out=t[:].rearrange("p (s c) -> p s c", c=C), in_=g_view[J // 4, J % 4][:, a:b, :])
-            for s in range(a, b):
-                raw[J, s] = (t, s - a)
+        def load_samples(view, width, tag, bufs, into, a, b):
+            t = sb(tag, [P, (b - a) * width], BF16, bufs)
+            cuts = [a] + [i for i in range(a + 1, b) if i % 16 == 0] + [b]
+            for lo, hi in zip(cuts, cuts[1:]):
+                nc.sync.dma_start(
+                    out=t[:, (lo - a) * width : (hi - a) * width],
+                    in_=view[lo // 16][:, (lo % 16) * width : ((hi - 1) % 16 + 1) * width],
+                )
+            for i in range(a, b):
+                into[i] = (t, i - a)
 
-        def load_n(J, a=0, b=S):
-            if b - a == S:
-                t = sb("noise", [P, S, D], BF16, 4)
+        def load_g(a, b):
+            if b - a == 4:
+                load_samples(g_view, C, "raw", 3, raw, a, b)
             else:
-                t = sb("noise%d_%d" % (J, a), [P, b - a, D], BF16, 1)
-            nc.sync.dma_start(out=t[:], in_=n_view[J // 4, J % 4][:, a:b, :])
-            noise_tile[J] = t
-            for s in range(a, b):
-                noise[J, s] = t[:, s - a, :]
+                load_samples(g_view, C, "raw_part", 5, raw, a, b)
+
+        def load_n(a, b):
+            load_samples(n_view, D, "noise", 4, noise, a, b)
 
         def load_z(J, count):
             t = sb("z", [P, count, D], F32, 3)
@@ -92,130 +97,142 @@ def tile_hetxlhead_pa_v_kernel(
             for k in range(count):
                 zt[J + k] = t[:, k, :]
 
-        def load_w(src):
+        def load_rows(src):
             t = sb("wraw", [P, 4, D], BF16, 3)
             nc.sync.dma_start(out=t[:], in_=src.rearrange("(p j) w -> p j w", j=4))
             return t
 
-        def load_classes(src):
+        def load_sorted(src):
             t = sb("wraw", [P, 4, D], BF16, 3)
             rows = src.rearrange("(a u b e) w -> u a b (e w)", u=2, b=RUN // 2, e=2)
             for u in range(2):
                 nc.sync.dma_start(out=t[:, 2 * u : 2 * u + 2, :].rearrange("p e w -> p (e w)"), in_=rows[u])
             return t
 
-        def scale_views(J, a, b, tag):
+        def scale_views(a, b, tag):
             t = sb(tag, [P, 2, 2 * P * (b - a) // RUN, RUN], BF16, 3)
             for k in range(a, b):
-                gs[J, k] = (t, k - a, b - a)
-            src, at = raw[J, a // 2]
+                gs[k] = (t, k - a, b - a)
+            src, at = raw[a // 2]
             first = C * at + (a % 2) * C // 2
             return t[:], src[:, first : first + (b - a) * C // 2].rearrange("p (q u e) -> p u q e", u=2, e=RUN)
 
-        def prescale(J, a, b):
-            dst, src = scale_views(J, a, b, "gs")
+        def prescale(a, b):
+            dst, src = scale_views(a, b, "gs")
             nc.vector.tensor_scalar(out=dst, in0=src, scalar1=1.0 / TEMPERATURE, scalar2=None, op0=MULT)
 
-        def scalar_prescale(J, a, b):
-            dst, src = scale_views(J, a, b, "gs_scalar")
+        def scalar_prescale(a, b):
+            dst, src = scale_views(a, b, "gs_scalar")
             nc.scalar.activation(dst, src, mybir.ActivationFunctionType.Copy, scale=1.0 / TEMPERATURE)
 
-        def turn(J, s):
-            trb[J, s] = rotating(("turn", J, s), [P, 2, 2, P])
+        def turn(i):
+            trb[i] = rotating(("turn", i), [P, 2, 2, P])
             for h in range(2):
-                t, at, count = gs[J, 2 * s + h]
+                t, at, count = gs[2 * i + h]
                 words = t[:].rearrange("p u q e -> p (u q e)").bitcast(F32)
                 for u in range(2):
                     a = (u * count + at) * P
-                    nc.tensor.transpose(trb[J, s][:, h, u, :], words[:, a : a + P], ident[:])
+                    nc.tensor.transpose(trb[i][:, h, u, :], words[:, a : a + P], ident[:])
 
-        def empty_turn(J, s, count=2):
-            at = s % count
+        def empty_turn(i, count=2):
+            at = i % count
             if at == 0:
                 t = sb("grp", [P, count, 2, P, 2], F32, 3)
                 for k in range(count):
-                    grp[J, s + k] = t
-            nc.scalar.copy(out=grp[J, s][:, at], in_=trb[J, s][:].rearrange("p h u r -> p h r u"))
+                    grp[i + k] = t
+            nc.scalar.copy(out=grp[i][:, at], in_=trb[i][:].rearrange("p h u r -> p h r u"))
 
-        def quant_g(J, a, b):
-            codes, scales = quantised("g", 256 * (b - a), 5)
+        def quant_g(a, b):
+            codes, scales = quantised("g", 256 * (b - a), 6)
             nc.vector.quantize_mx(
                 out=codes[:].bitcast(E5M2), scales=scales[:],
-                in_=grp[J, a][:].rearrange("p s h r u -> p (s h r u)").bitcast(BF16),
+                in_=grp[a][:].rearrange("p s h r u -> p (s h r u)").bitcast(BF16),
             )
-            for s in range(a, b):
-                cod[J, s] = (codes, scales, s - a)
+            for i in range(a, b):
+                cod[i] = (codes, scales, i - a)
 
-        def g_pass(out, J, s, h, start, stop, moving=slice(0, D)):
-            codes, scales, at = cod[J, s]
+        def g_pass(out, i, h, start, stop, moving=slice(0, D)):
+            codes, scales, at = cod[i]
             cols = slice((at * 2 + h) * P, (at * 2 + h + 1) * P)
             nc.tensor.matmul_mx(
                 out=out, lhsT=codes[:, cols].bitcast(E5M2), lhsT_scale=scales[:, cols],
                 rhs=wc[h][0][:, moving].bitcast(E4M3), rhs_scale=wc[h][1][:, moving], start=start, stop=stop,
             )
 
-        def dpre(J, s):
-            dpb[J, s] = rotating(("dpre", J, s), [P, D])
+        def dpre(i):
+            dpb[i] = rotating(("dpre", i), [P, D])
             for h in range(2):
-                g_pass(dpb[J, s][:], J, s, h, h == 0, h == 1)
+                g_pass(dpb[i][:], i, h, h == 0, h == 1)
 
-        def first_passes(s, h):
+        def first_passes(i, h):
             if h == 0:
-                dpb[0, s] = rotating(("dpre", 0, s), [P, D])
-                if s == 0:
+                dpb[i] = rotating(("dpre", i), [P, D])
+                if i == 0:
                     outb[0] = summing(0)
-            g_pass(dpb[0, s][:], 0, s, h, h == 0, h == 1)
-            g_pass(outb[0][:], 0, s, h, s == 0 and h == 0, False)
+            g_pass(dpb[i][:], i, h, h == 0, h == 1)
+            g_pass(outb[0][:], i, h, i == 0 and h == 0, False)
 
-        def direct(J, a, b):
-            if a == 0:
+        def keeps(J):
+            return J == LAST
+
+        def kept_sample(J):
+            return S * J + (KEPT if J < LAST else KEPT - 1)
+
+        def keep(J):
+            kept[J] = sb("kept", [P, D], F32, 2)
+            nc.scalar.copy(out=kept[J][:], in_=dpb[kept_sample(J)][:])
+
+        def direct(a, b):
+            J = a // S
+            if a % S == 0:
                 outb[J] = summing(J)
-            for s in range(a, b):
-                for h in range(2):
-                    g_pass(outb[J][:], J, s, h, s == 0 and h == 0, False)
+            for i in range(a, b):
+                if not (keeps(J) and i == kept_sample(J)):
+                    for h in range(2):
+                        g_pass(outb[J][:], i, h, i % S == 0 and h == 0, False)
 
-        def times_noise(J, s, cols=slice(0, D)):
-            if s == 0 and cols.start == 0:
-                prod[J] = sb("prod", [P, 2, 2, D], F32, 2)
+        def times_noise(i):
+            J, s = divmod(i, S)
+            if s == 0:
+                prod[J] = sb("prod", [P, 2, 2 * D], F32, 2)
+            t, at = noise[i]
             nc.vector.tensor_tensor(
-                out=prod[J][:, s % 2, s // 2, cols], in0=dpb[J, s][:, cols], in1=noise[J, s][:, cols], op=MULT
+                out=prod[J][:, s % 2, (s // 2) * D : (s // 2 + 1) * D], in0=dpb[i][:],
+                in1=t[:, at * D : (at + 1) * D], op=MULT,
             )
 
-        def add_pairs(J, cols=slice(0, D)):
-            if cols.start == 0:
-                part[J] = sb("part", [P, 2, D], F32, 1)
+        def add_pairs(J, eng, a, b):
+            if J not in part:
+                part[J] = sb("part", [P, 2 * D], F32, 2)
+            eng.tensor_tensor(out=part[J][:, a:b], in0=prod[J][:, 0, a:b], in1=prod[J][:, 1, a:b], op=ADD)
+
+        def natural(ap, half):
+            return ap.rearrange("p (h a u e) -> p h u a e", h=2, u=2, e=RUN)[:, half]
+
+        def by_line(ap, half):
+            return ap.rearrange("p (u h a e) -> p h u a e", h=2, u=2, e=RUN)[:, half]
+
+        def whole_natural(ap):
+            return ap.rearrange("p (a u e) -> p u a e", u=2, e=RUN)
+
+        def whole_by_line(ap):
+            return ap.rearrange("p (u a e) -> p u a e", u=2, e=RUN)
+
+        def add_all(J):
+            dstd[J] = sb("dstd", [P, D], F32, 2)
             nc.vector.tensor_tensor(
-                out=part[J][:, :, cols], in0=prod[J][:, 0, :, cols], in1=prod[J][:, 1, :, cols], op=ADD
-            )
-
-        def natural(ap, words=slice(0, P)):
-            return ap.rearrange("p (w u e) -> p u w e", u=2, e=2)[:, :, words, :]
-
-        def sorted_by_half(ap, words=slice(0, P)):
-            return ap.rearrange("p (u w e) -> p u w e", u=2, e=2)[:, :, words, :]
-
-        def add_all(J, words=slice(0, P)):
-            if words.start == 0:
-                dstd[J] = sb("dstd", [P, D], F32, 2)
-            nc.vector.tensor_tensor(
-                out=sorted_by_half(dstd[J][:], words), in0=natural(part[J][:, 0, :], words),
-                in1=natural(part[J][:, 1, :], words), op=ADD,
+                out=whole_by_line(dstd[J][:]), in0=whole_natural(part[J][:, 0:D]),
+                in1=whole_natural(part[J][:, D : 2 * D]), op=ADD,
             )
 
         def sigmoid(J):
             sig[J] = sb("sig", [P, D], F32, 3)
-            nc.scalar.activation(
-                sorted_by_half(sig[J][:]), natural(zt[J]),
-                mybir.ActivationFunctionType.Sigmoid,
-            )
+            nc.scalar.activation(whole_by_line(sig[J][:]), whole_natural(zt[J]), mybir.ActivationFunctionType.Sigmoid)
 
-        def make_dz(J, eng, words=slice(0, P)):
-            if J % 4 == 0 and words.start == 0:
+        def make_dz(J):
+            if J % 4 == 0:
                 dz[J // 4] = sb("dz", [P, 4, D], BF16, 2)
-            eng.tensor_tensor(
-                out=sorted_by_half(dz[J // 4][:, J % 4, :], words), in0=sorted_by_half(dstd[J][:], words),
-                in1=sorted_by_half(sig[J][:], words), op=MULT,
-            )
+            nc.gpsimd.tensor_tensor(out=dz[J // 4][:, J % 4, :], in0=dstd[J][:], in1=sig[J][:], op=MULT)
 
         def turn_dz(J, bank=None):
             if bank is None:
@@ -225,13 +242,6 @@ def tile_hetxlhead_pa_v_kernel(
             words = dz[J // 4][:, J % 4, :].bitcast(F32)
             for u in range(2):
                 nc.tensor.transpose(dzt_b[J][:, u, :], words[:, u * P : (u + 1) * P], ident[:])
-
-        def interleave_dz(copy, dst, src, cols):
-            words = slice(cols.start // 4, cols.stop // 4)
-            copy(
-                out=dst[:].rearrange("p (w u e) j -> p u w j e", u=2, e=2)[:, :, words],
-                in_=src[:].rearrange("p j (u w e) -> p u w j e", u=2, e=2)[:, :, words],
-            )
 
         def empty_dz(J):
             dzt[J] = sb("dzt", [P, P, 2], F32, 2)
@@ -250,9 +260,12 @@ def tile_hetxlhead_pa_v_kernel(
                 rhs=wd[0][:].bitcast(E4M3), rhs_scale=wd[1][:], start=False, stop=True,
             )
 
-        def empty_out(J, copy=nc.scalar.copy):
+        def empty_out(J):
             res[J] = sb("res", [P, D], F32, 4)
-            copy(out=res[J][:], in_=outb[J][:])
+            if keeps(J):
+                nc.vector.tensor_tensor(out=res[J][:], in0=outb[J][:], in1=kept[J][:], op=ADD)
+            else:
+                nc.scalar.copy(out=res[J][:], in_=outb[J][:])
 
         def store_out(J):
             nc.sync.dma_start(out=o_view[J // 4, J % 4], in_=res[J][:])
@@ -275,10 +288,10 @@ def tile_hetxlhead_pa_v_kernel(
         def store_weight(m, copy):
             r = sb("res1", [P, D], F32, 4)
             copy(out=r[:], in_=acc[m][:])
-            nc.sync.dma_start(out=out_1[m * P : (m + 1) * P, :], in_=r[:])
+            nc.sync.dma_start(out=w_view[m // 2, m % 2], in_=r[:])
 
         def weight_pass(m, g):
-            cols = slice(m * P, (m + 1) * P)
+            cols = quarter[m]
             nc.tensor.matmul_mx(
                 out=acc[m][:], lhsT=dzq[g][0][:, cols].bitcast(E5M2), lhsT_scale=dzq[g][1][:, cols],
                 rhs=ft[g][0][:].bitcast(E4M3), rhs_scale=ft[g][1][:], start=g == 0, stop=g == 1,
@@ -290,100 +303,105 @@ def tile_hetxlhead_pa_v_kernel(
         dzq = [quantised("dz0", D, 1), quantised("dz1", D, 1)]
         left, right = slice(0, D // 2), slice(D // 2, D)
         quarter = [slice(m * P, (m + 1) * P) for m in range(4)]
-        acc = {}
         ctx.enter_context(tc.manual_schedule())
 
         dummy = sb("dummy", [P, 1], F32, 1)
         nc.vector.memset(dummy[:], 0.0)
         nc.scalar.activation(dummy[:], dummy[:], mybir.ActivationFunctionType.Sigmoid)
 
-        load_g(0, 0, 1)
-        wc_raw = [load_classes(w_cls[0:512, :])]
-        load_g(0, 1, 2)
-        wc_raw.append(load_classes(w_cls[512:1024, :]))
-        load_g(0, 2, 4)
-        load_n(0, 0, 2)
-        load_g(1, 0, 2)
-        load_n(0, 2, 4)
-        load_g(1, 2, 4)
-        load_g(2, 0, 2)
-        load_g(2, 2, 4)
+        load_g(0, 1)
+        wc_raw = [load_sorted(w_cls[0:512, :])]
+        load_g(1, 2)
+        wc_raw.append(load_sorted(w_cls[512:1024, :]))
+        load_g(2, 4)
+        load_n(0, 2)
+        load_g(4, 6)
+        load_g(6, 8)
+        load_n(2, 6)
+        load_g(8, 10)
+        load_g(10, 14)
         load_z(0, 1)
-        load_n(1)
-        wd_raw = load_w(w_diag)
-        load_g(3)
+        load_n(6, 10)
+        load_g(14, 18)
+        wd_raw = load_sorted(w_diag)
         load_z(1, 1)
-        load_n(2)
-        load_g(4)
-        ft_raw = [load_w(features[0:512, :])]
+        load_n(10, 14)
+        load_g(18, 22)
+        ft_raw = [load_rows(features[0:512, :])]
         load_z(2, 2)
-        load_n(3)
-        load_g(5)
-        load_n(4)
-        ft_raw.append(load_w(features[512:1024, :]))
-        load_g(6)
+        load_n(14, 18)
+        load_g(22, 26)
+        ft_raw.append(load_rows(features[512:1024, :]))
+        load_n(18, 22)
+        load_g(26, 30)
         load_z(4, 2)
-        load_n(5)
-        load_g(7)
-        load_n(6)
+        load_n(22, 26)
+        load_g(30, 32)
+        load_n(26, 30)
         load_z(6, 2)
-        load_n(7)
+        load_n(30, 32)
 
         on_vector, on_scalar = slice(0, VECTOR_COLUMNS), slice(VECTOR_COLUMNS, D)
         wg = [grouped_w(), grouped_w()]
-        prescale(0, 0, 2)
-        turn(0, 0)
+        prescale(0, 2)
+        turn(0)
         unread = rotating("unread", [P, D])
         for k in range(WARM_UPS):
-            nc.tensor.matmul(unread[:], lhsT=raw[0, 0][0][:, 0:P], rhs=raw[0, 0][0][:, 0:D], start=True, stop=True)
+            nc.tensor.matmul(unread[:], lhsT=raw[0][0][:, 0:P], rhs=raw[0][0][:, 0:D], start=True, stop=True)
         interleave(nc.vector.tensor_copy, wg[0], wc_raw[0], on_vector)
         interleave(nc.scalar.copy, wg[0], wc_raw[0], on_scalar)
-        empty_turn(0, 0, 1)
-        prescale(0, 2, 4)
-        turn(0, 1)
+        empty_turn(0, 1)
+        prescale(2, 4)
+        turn(1)
         quant_w(wc[0], wg[0], E4M3)
-        quant_g(0, 0, 1)
+        quant_g(0, 1)
         first_passes(0, 0)
         interleave(nc.vector.tensor_copy, wg[1], wc_raw[1], on_vector)
         interleave(nc.scalar.copy, wg[1], wc_raw[1], on_scalar)
-        empty_turn(0, 1, 1)
-        prescale(0, 4, 8)
+        empty_turn(1, 1)
+        prescale(4, 8)
         quant_w(wc[1], wg[1], E4M3)
-        quant_g(0, 1, 2)
-        turn(0, 2)
-        turn(0, 3)
+        quant_g(1, 2)
+        turn(2)
+        turn(3)
         first_passes(0, 1)
-        empty_turn(0, 2)
-        empty_turn(0, 3)
+        empty_turn(2)
+        empty_turn(3)
         first_passes(1, 0)
         first_passes(1, 1)
-        prescale(1, 0, 4)
-        times_noise(0, 0)
-        turn(1, 0)
-        turn(1, 1)
-        quant_g(0, 2, 4)
-        times_noise(0, 1)
-        prescale(1, 4, 6)
-        scalar_prescale(1, 6, 8)
-        empty_turn(1, 0)
-        empty_turn(1, 1)
-        dpre(0, 2)
-        dpre(0, 3)
-        turn(1, 2)
-        turn(1, 3)
-        times_noise(0, 2)
-        scalar_prescale(2, 2, 4)
-        empty_turn(1, 2)
-        empty_turn(1, 3)
-        quant_g(1, 0, 2)
-        times_noise(0, 3)
-        prescale(2, 0, 2)
-        direct(0, 2, S)
-        prescale(2, 4, 8)
+        prescale(8, 12)
+        times_noise(0)
+        turn(4)
+        turn(5)
+        quant_g(2, 4)
+        times_noise(1)
+        prescale(12, 16)
+        empty_turn(4)
+        empty_turn(5)
+        dpre(2)
+        dpre(3)
+        direct(2, 4)
+        times_noise(2)
+        scalar_prescale(16, 18)
+        prescale(18, 20)
+        times_noise(3)
+        quant_g(4, 6)
+        for i in range(6, 10):
+            turn(i)
+            empty_turn(i)
+        add_pairs(0, nc.vector, 0, 2 * D)
+        prescale(20, 20 + VECTOR_UNITS)
+        dpre(4)
+        dpre(5)
+        direct(4, 6)
+        times_noise(4)
+        quant_g(6, 8)
+        times_noise(5)
+        scalar_prescale(20 + VECTOR_UNITS, 28)
         sigmoid(0)
-        add_pairs(0)
-        quant_g(1, 2, 4)
+        quant_g(8, 10)
         add_all(0)
+        prescale(28, 28 + VECTOR_UNITS)
 
         grouped = {}
         beside = [(wd_raw, wd, E4M3), (ft_raw[0], ft[0], E4M3), (ft_raw[1], ft[1], E4M3), (None, dzq[0], E5M2)]
@@ -392,131 +410,178 @@ def tile_hetxlhead_pa_v_kernel(
             k, cols = n // 2, (left, right)[n % 2]
             if n % 2 == 0:
                 grouped[k] = grouped_w()
-            if beside[k][0] is None:
-                interleave_dz(nc.scalar.copy, grouped[k], dz[0], cols)
-            else:
-                interleave(nc.scalar.copy, grouped[k], beside[k][0], cols)
+            interleave(nc.scalar.copy, grouped[k], dz[0] if beside[k][0] is None else beside[k][0], cols)
 
         def side_quant(k):
             quant_w(beside[k][1], grouped[k], beside[k][2])
 
-        for s in range(S):
-            turn(2, s)
-            empty_turn(2, s)
-        done = 0
-        for J in range(1, LAST):
-            more = J + 2 < TILES
-            count = 1 + J % 2 if more else 0
-            for s in range(S):
-                dpre(J, s)
-                times_noise(J, s)
-                if s == 0:
-                    make_dz(J - 1, nc.gpsimd)
-            if J >= 2:
-                quant_dz(J - 2)
-            if more:
-                split = UNITS - (SCALAR_UNITS - 2 * count)
-                prescale(J + 2, 0, split)
-                scalar_prescale(J + 2, split, UNITS)
-            sigmoid(J)
-            for n in range(done, done + count):
-                side_half(n)
-            direct(J, 0, S)
-            if J >= 2:
-                dz_pass(J - 2)
-                empty_out(J - 2)
-            quant_g(J + 1, 0, 2)
-            add_pairs(J)
-            quant_g(J + 1, 2, 4)
-            add_all(J)
-            if more and (done + count) // 2 > done // 2 and J + 3 < TILES:
-                side_quant(done // 2)
-            done += count
-            turn_dz(J - 1)
-            empty_dz(J - 1)
-            if more:
-                for s in range(S):
-                    turn(J + 2, s)
-                    empty_turn(J + 2, s)
-            if J >= 4:
-                store_out(J - 4)
-        store_out(LAST - 4)
-        store_out(LAST - 3)
+        for i in range(10, 14):
+            turn(i)
+            empty_turn(i)
+
+        def window(K):
+            first = 4 * K - 2
+            if K >= 4 and keeps(K - 4):
+                empty_out(K - 4)
+            for i in range(first, first + 4):
+                dpre(i)
+                times_noise(i)
+                if i == first:
+                    make_dz(K - 2)
+                    add_pairs(K - 1, nc.gpsimd, 0, GPSIMD_COLUMNS)
+
+        for K in range(2, LAST):
+            first = 4 * K - 2
+            window(K)
+            ahead = [i for i in range(first + 8, first + 12) if i < S * TILES]
+            side_half(K - 2)
+            if len(ahead) == 4:
+                scalar_prescale(2 * ahead[0] + VECTOR_UNITS, 2 * ahead[0] + UNITS)
+            if keeps(K - 1):
+                keep(K - 1)
+            if K == LAST - 1:
+                side_half(K - 1)
+            sigmoid(K - 1)
+            if K >= 3:
+                quant_dz(K - 3)
+            if K == 3:
+                side_quant(0)
+            direct(max(S * (K - 1), 6), S * K)
+            if K >= 3:
+                dz_pass(K - 3)
+                if not keeps(K - 3):
+                    empty_out(K - 3)
+            quant_g(first + 4, first + 6)
+            add_pairs(K - 1, nc.vector, GPSIMD_COLUMNS, 2 * D)
+            quant_g(first + 6, first + 8)
+            if K == 5:
+                side_quant(1)
+            add_all(K - 1)
+            later = [i for i in range(first + 12, first + 16) if i < S * TILES]
+            if later:
+                prescale(2 * later[0], 2 * later[0] + min(VECTOR_UNITS, 2 * len(later)))
+            else:
+                side_quant(2)
+            turn_dz(K - 2)
+            empty_dz(K - 2)
+            for i in ahead:
+                turn(i)
+                empty_turn(i)
+            if K >= 5:
+                store_out(K - 5)
+        store_out(LAST - 5)
 
         L = LAST
-        halves = (slice(0, P // 2), slice(P // 2, P))
-        side_quant(3)
-        sigmoid(L)
         last = {}
-        prod[L] = sb("prod", [P, 2, 2, D], F32, 2)
 
-        def last_dpre(half, pair):
-            last[half, pair] = rotating(("last", half, pair), [P, 2, D // 2])
+        def last_dpre(half):
+            last[half] = rotating(("last", half), [P, 2, D // 2])
             for k in range(2):
                 for h in range(2):
-                    g_pass(last[half, pair][:, k, :], L, 2 * pair + k, h, h == 0, h == 1, (left, right)[half])
+                    g_pass(last[half][:, k, :], S * L + 2 + k, h, h == 0, h == 1, (left, right)[half])
 
-        def last_times_noise(half, pair):
+        def last_times_noise(half):
             cols = (left, right)[half]
             nc.vector.tensor_tensor(
-                out=prod[L][:, :, pair, cols], in0=last[half, pair][:],
-                in1=noise_tile[L][:, 2 * pair : 2 * pair + 2, cols], op=MULT,
+                out=prod[L][:, :, D : 2 * D][:, :, cols], in0=last[half][:],
+                in1=noise[S * L + 2][0][:].rearrange("p (s d) -> p s d", s=2)[:, :, cols], op=MULT,
             )
 
-        def open_weight(m, key):
-            acc[m] = in_bank(bank_of[key], ("weight", m), [P, D])
+        def last_add_pairs(half):
+            cols = (left, right)[half]
+            views = [ap.rearrange("p (k d) -> p k d", k=2)[:, :, cols] for ap in (part[L][:], prod[L][:, 0], prod[L][:, 1])]
+            nc.vector.tensor_tensor(out=views[0], in0=views[1], in1=views[2], op=ADD)
+
+        def last_add_all(half):
+            nc.vector.tensor_tensor(
+                out=by_line(dstd[L][:], half), in0=natural(part[L][:, 0:D], half),
+                in1=natural(part[L][:, D : 2 * D], half), op=ADD,
+            )
+
+        def last_make_dz(half):
+            nc.vector.tensor_tensor(
+                out=by_line(dz[1][:, 3, :], half), in0=by_line(dstd[L][:], half), in1=by_line(sig[L][:], half), op=MULT
+            )
+
+        def open_weight(m, bank):
+            acc[m] = in_bank(bank, ("weight", m), [P, D])
             weight_pass(m, 0)
 
+        window(L)
+        store_out(L - 4)
+        side_half(6)
+        side_half(7)
+        if keeps(L - 1):
+            keep(L - 1)
+        direct(S * (L - 1), S * (L - 1) + 2)
+        turn_dz(L - 2)
+        empty_dz(L - 2)
+        sigmoid(L - 1)
+        keep(L)
+        quant_g(S * L + 2, S * L + 4)
+        quant_dz(L - 3)
+        direct(S * (L - 1) + 2, S * L)
+        dz_pass(L - 3)
+        if not keeps(L - 3):
+            empty_out(L - 3)
+            store_out(L - 3)
+        add_pairs(L - 1, nc.vector, GPSIMD_COLUMNS, 2 * D)
         quant_dz(L - 2)
-        for half in range(2):
-            for pair in range(2):
-                last_dpre(half, pair)
-        last_times_noise(0, 0)
-        make_dz(L - 1, nc.gpsimd)
-        last_times_noise(0, 1)
-        last_times_noise(1, 0)
+        add_all(L - 1)
+        side_quant(3)
+        part[L] = sb("part", [P, 2 * D], F32, 2)
+        dstd[L] = sb("dstd", [P, D], F32, 2)
+        sigmoid(L)
+        last_dpre(0)
         dz_pass(L - 2)
+        last_dpre(1)
+        make_dz(L - 1)
+        if keeps(L - 3):
+            empty_out(L - 3)
+            store_out(L - 3)
+        last_times_noise(0)
         empty_out(L - 2)
         store_out(L - 2)
-        direct(L, 0, 1)
-        turn_dz(L - 1, bank_of["last", 0, 0])
+        last_times_noise(1)
+        free = [k for k in range(ROTATING) if k not in (bank_of["last", 0], bank_of["last", 1], bank_of["dz", L - 2])]
+        direct(S * L, S * L + 2)
+        open_weight(0, free[0])
+        open_weight(2, free[1])
+        turn_dz(L - 1, bank_of["dz", L - 2])
         empty_dz(L - 1)
-        direct(L, 1, S)
-        add_pairs(L, left)
-        last_times_noise(1, 1)
-        add_all(L, halves[0])
+        direct(S * L + 2, S * L + 4)
+        last_add_pairs(0)
+        last_add_pairs(1)
+        last_add_all(0)
         quant_dz(L - 1)
+        last_make_dz(0)
+        last_add_all(1)
         dz_pass(L - 1)
-        open_weight(0, ("dz", L - 2))
-        open_weight(1, ("last", 0, 1))
-        make_dz(L, nc.vector, halves[0])
         t = grouped_w()
-        add_pairs(L, right)
-        interleave_dz(nc.vector.tensor_copy, t, dz[1], quarter[0])
-        interleave_dz(nc.scalar.copy, t, dz[1], quarter[1])
+        interleave(nc.vector.tensor_copy, t, dz[1], quarter[0])
+        interleave(nc.scalar.copy, t, dz[1], quarter[2])
+        last_make_dz(1)
+        quant_w(dzq[1], t, E5M2, quarter[0])
+        open_weight(1, bank_of["last", 0])
+        open_weight(3, bank_of["last", 1])
         empty_out(L - 1)
         store_out(L - 1)
-        add_all(L, halves[1])
-        quant_w(dzq[1], t, E5M2, quarter[0])
-        quant_w(dzq[1], t, E5M2, quarter[1])
-        make_dz(L, nc.vector, halves[1])
-        open_weight(2, ("last", 1, 0))
+        turn_dz(L, bank_of["dz", L - 2])
         weight_pass(0, 1)
-        weight_pass(1, 1)
-        store_weight(0, nc.scalar.copy)
-        turn_dz(L, bank_of["last", 0, 0])
         empty_dz(L)
-        open_weight(3, ("last", 1, 1))
-        interleave_dz(nc.vector.tensor_copy, t, dz[1], quarter[2])
-        interleave_dz(nc.vector.tensor_copy, t, dz[1], quarter[3])
         quant_w(dzq[1], t, E5M2, quarter[2])
         weight_pass(2, 1)
-        store_weight(1, nc.scalar.copy)
-        quant_w(dzq[1], t, E5M2, quarter[3])
+        interleave(nc.vector.tensor_copy, t, dz[1], quarter[1])
+        interleave(nc.vector.tensor_copy, t, dz[1], quarter[3])
+        quant_w(dzq[1], t, E5M2, quarter[1])
+        weight_pass(1, 1)
         quant_dz(L)
-        weight_pass(3, 1)
         dz_pass(L)
+        quant_w(dzq[1], t, E5M2, quarter[3])
+        weight_pass(3, 1)
+        store_weight(0, nc.scalar.copy)
         store_weight(2, nc.vector.tensor_copy)
-        store_weight(3, nc.scalar.copy)
-        empty_out(L, nc.vector.tensor_copy)
+        store_weight(1, nc.scalar.copy)
+        empty_out(L)
         store_out(L)
+        store_weight(3, nc.scalar.copy)

@@ -23,8 +23,6 @@ VECTOR_COLUMNS = 320
 WARM_UPS = 4
 UNITS = 8
 VECTOR_UNITS = 6
-GPSIMD_COLUMNS = 384
-KEPT = 2
 ROTATING, SUMS = 5, 3
 FLOPS = 2 * (B * S * C * D + B * D * D + D * D * B)
 BYTES = 2 * (B * S * C + B * S * D + B * D + D * D + C * D) + 4 * (B * D) + 4 * (B * D + D * D)
@@ -65,8 +63,6 @@ def tile_hetxlhead_pa_v_kernel(
 
         raw, noise, zt, gs, trb, grp, cod, dpb = {}, {}, {}, {}, {}, {}, {}, {}
         prod, part, dstd, sig, dz, dzt_b, dzt, dzc, outb, res, acc = {}, {}, {}, {}, {}, {}, {}, {}, {}, {}, {}
-
-        kept = {}
 
         def quantised(tag, cols, bufs):
             return sb(tag + "_c", [P, cols], U32, bufs, 256), sb(tag + "_s", [P, cols], U8, bufs, 256)
@@ -172,24 +168,13 @@ def tile_hetxlhead_pa_v_kernel(
             g_pass(dpb[i][:], i, h, h == 0, h == 1)
             g_pass(outb[0][:], i, h, i == 0 and h == 0, False)
 
-        def keeps(J):
-            return J == LAST
-
-        def kept_sample(J):
-            return S * J + (KEPT if J < LAST else KEPT - 1)
-
-        def keep(J):
-            kept[J] = sb("kept", [P, D], F32, 2)
-            nc.scalar.copy(out=kept[J][:], in_=dpb[kept_sample(J)][:])
-
         def direct(a, b):
             J = a // S
             if a % S == 0:
                 outb[J] = summing(J)
             for i in range(a, b):
-                if not (keeps(J) and i == kept_sample(J)):
-                    for h in range(2):
-                        g_pass(outb[J][:], i, h, i % S == 0 and h == 0, False)
+                for h in range(2):
+                    g_pass(outb[J][:], i, h, i % S == 0 and h == 0, False)
 
         def times_noise(i):
             J, s = divmod(i, S)
@@ -201,10 +186,9 @@ def tile_hetxlhead_pa_v_kernel(
                 in1=t[:, at * D : (at + 1) * D], op=MULT,
             )
 
-        def add_pairs(J, eng, a, b):
-            if J not in part:
-                part[J] = sb("part", [P, 2 * D], F32, 2)
-            eng.tensor_tensor(out=part[J][:, a:b], in0=prod[J][:, 0, a:b], in1=prod[J][:, 1, a:b], op=ADD)
+        def add_pairs(J):
+            part[J] = sb("part", [P, 2 * D], F32, 2)
+            nc.vector.tensor_tensor(out=part[J][:], in0=prod[J][:, 0], in1=prod[J][:, 1], op=ADD)
 
         def natural(ap, half):
             return ap.rearrange("p (h a u e) -> p h u a e", h=2, u=2, e=RUN)[:, half]
@@ -229,10 +213,10 @@ def tile_hetxlhead_pa_v_kernel(
             sig[J] = sb("sig", [P, D], F32, 3)
             nc.scalar.activation(whole_by_line(sig[J][:]), whole_natural(zt[J]), mybir.ActivationFunctionType.Sigmoid)
 
-        def make_dz(J):
+        def make_dz(J, eng=nc.gpsimd):
             if J % 4 == 0:
                 dz[J // 4] = sb("dz", [P, 4, D], BF16, 2)
-            nc.gpsimd.tensor_tensor(out=dz[J // 4][:, J % 4, :], in0=dstd[J][:], in1=sig[J][:], op=MULT)
+            eng.tensor_tensor(out=dz[J // 4][:, J % 4, :], in0=dstd[J][:], in1=sig[J][:], op=MULT)
 
         def turn_dz(J, bank=None):
             if bank is None:
@@ -260,12 +244,9 @@ def tile_hetxlhead_pa_v_kernel(
                 rhs=wd[0][:].bitcast(E4M3), rhs_scale=wd[1][:], start=False, stop=True,
             )
 
-        def empty_out(J):
+        def empty_out(J, copy=nc.scalar.copy):
             res[J] = sb("res", [P, D], F32, 4)
-            if keeps(J):
-                nc.vector.tensor_tensor(out=res[J][:], in0=outb[J][:], in1=kept[J][:], op=ADD)
-            else:
-                nc.scalar.copy(out=res[J][:], in_=outb[J][:])
+            copy(out=res[J][:], in_=outb[J][:])
 
         def store_out(J):
             nc.sync.dma_start(out=o_view[J // 4, J % 4], in_=res[J][:])
@@ -316,30 +297,30 @@ def tile_hetxlhead_pa_v_kernel(
         load_g(2, 4)
         load_n(0, 2)
         load_g(4, 6)
+        load_n(2, 4)
         load_g(6, 8)
-        load_n(2, 6)
         load_g(8, 10)
-        load_g(10, 14)
+        load_g(10, 12)
         load_z(0, 1)
-        load_n(6, 10)
-        load_g(14, 18)
+        load_n(4, 8)
+        load_g(12, 16)
         wd_raw = load_sorted(w_diag)
         load_z(1, 1)
-        load_n(10, 14)
-        load_g(18, 22)
+        load_n(8, 12)
+        load_g(16, 20)
         ft_raw = [load_rows(features[0:512, :])]
         load_z(2, 2)
-        load_n(14, 18)
-        load_g(22, 26)
+        load_n(12, 16)
+        load_g(20, 24)
         ft_raw.append(load_rows(features[512:1024, :]))
-        load_n(18, 22)
-        load_g(26, 30)
+        load_n(16, 20)
+        load_g(24, 28)
         load_z(4, 2)
-        load_n(22, 26)
-        load_g(30, 32)
-        load_n(26, 30)
+        load_n(20, 24)
+        load_g(28, 32)
+        load_n(24, 28)
         load_z(6, 2)
-        load_n(30, 32)
+        load_n(28, 32)
 
         on_vector, on_scalar = slice(0, VECTOR_COLUMNS), slice(VECTOR_COLUMNS, D)
         wg = [grouped_w(), grouped_w()]
@@ -375,116 +356,101 @@ def tile_hetxlhead_pa_v_kernel(
         turn(5)
         quant_g(2, 4)
         times_noise(1)
-        prescale(12, 16)
+        prescale(12, 14)
+        scalar_prescale(14, 16)
         empty_turn(4)
         empty_turn(5)
         dpre(2)
         dpre(3)
-        direct(2, 4)
+        turn(6)
+        turn(7)
         times_noise(2)
-        scalar_prescale(16, 18)
-        prescale(18, 20)
-        times_noise(3)
+        scalar_prescale(18, 20)
+        empty_turn(6)
+        empty_turn(7)
         quant_g(4, 6)
-        for i in range(6, 10):
-            turn(i)
-            empty_turn(i)
-        add_pairs(0, nc.vector, 0, 2 * D)
-        prescale(20, 20 + VECTOR_UNITS)
-        dpre(4)
-        dpre(5)
-        direct(4, 6)
-        times_noise(4)
-        quant_g(6, 8)
-        times_noise(5)
-        scalar_prescale(20 + VECTOR_UNITS, 28)
+        times_noise(3)
+        prescale(16, 18)
+        direct(2, 4)
+        prescale(20, 24)
         sigmoid(0)
-        quant_g(8, 10)
+        add_pairs(0)
+        quant_g(6, 8)
         add_all(0)
-        prescale(28, 28 + VECTOR_UNITS)
+        prescale(24, 24 + VECTOR_UNITS)
 
         grouped = {}
         beside = [(wd_raw, wd, E4M3), (ft_raw[0], ft[0], E4M3), (ft_raw[1], ft[1], E4M3), (None, dzq[0], E5M2)]
 
-        def side_half(n):
-            k, cols = n // 2, (left, right)[n % 2]
-            if n % 2 == 0:
-                grouped[k] = grouped_w()
-            interleave(nc.scalar.copy, grouped[k], dz[0] if beside[k][0] is None else beside[k][0], cols)
+        def side_quarters(a, b):
+            for k in range(a // 4, (b - 1) // 4 + 1):
+                lo, hi = max(a, 4 * k) - 4 * k, min(b, 4 * k + 4) - 4 * k
+                if lo == 0:
+                    grouped[k] = grouped_w()
+                src = dz[0] if beside[k][0] is None else beside[k][0]
+                interleave(nc.scalar.copy, grouped[k], src, slice(lo * P, hi * P))
 
         def side_quant(k):
             quant_w(beside[k][1], grouped[k], beside[k][2])
 
-        for i in range(10, 14):
+        for i in range(8, 12):
             turn(i)
             empty_turn(i)
-
-        def window(K):
-            first = 4 * K - 2
-            if K >= 4 and keeps(K - 4):
-                empty_out(K - 4)
-            for i in range(first, first + 4):
+        for J in range(1, LAST):
+            first = S * J
+            for i in range(first, first + S):
                 dpre(i)
                 times_noise(i)
                 if i == first:
-                    make_dz(K - 2)
-                    add_pairs(K - 1, nc.gpsimd, 0, GPSIMD_COLUMNS)
-
-        for K in range(2, LAST):
-            first = 4 * K - 2
-            window(K)
-            ahead = [i for i in range(first + 8, first + 12) if i < S * TILES]
-            side_half(K - 2)
-            if len(ahead) == 4:
-                scalar_prescale(2 * ahead[0] + VECTOR_UNITS, 2 * ahead[0] + UNITS)
-            if keeps(K - 1):
-                keep(K - 1)
-            if K == LAST - 1:
-                side_half(K - 1)
-            sigmoid(K - 1)
-            if K >= 3:
-                quant_dz(K - 3)
-            if K == 3:
+                    make_dz(J - 1)
+            side_quarters(3 * (J - 1), min(3 * J, 16))
+            if J + 2 < TILES:
+                scalar_prescale(2 * S * (J + 2) + VECTOR_UNITS, 2 * S * (J + 3))
+            sigmoid(J)
+            if J >= 2:
+                quant_dz(J - 2)
+            if J == 2:
                 side_quant(0)
-            direct(max(S * (K - 1), 6), S * K)
-            if K >= 3:
-                dz_pass(K - 3)
-                if not keeps(K - 3):
-                    empty_out(K - 3)
+            direct(first, first + S)
+            if J >= 2:
+                dz_pass(J - 2)
+                empty_out(J - 2)
             quant_g(first + 4, first + 6)
-            add_pairs(K - 1, nc.vector, GPSIMD_COLUMNS, 2 * D)
+            add_pairs(J)
             quant_g(first + 6, first + 8)
-            if K == 5:
+            if J == 3:
                 side_quant(1)
-            add_all(K - 1)
-            later = [i for i in range(first + 12, first + 16) if i < S * TILES]
-            if later:
-                prescale(2 * later[0], 2 * later[0] + min(VECTOR_UNITS, 2 * len(later)))
-            else:
+            add_all(J)
+            if J + 3 < TILES:
+                prescale(2 * S * (J + 3), 2 * S * (J + 3) + VECTOR_UNITS)
+            elif J < LAST - 1:
                 side_quant(2)
-            turn_dz(K - 2)
-            empty_dz(K - 2)
-            for i in ahead:
-                turn(i)
-                empty_turn(i)
-            if K >= 5:
-                store_out(K - 5)
-        store_out(LAST - 5)
+            turn_dz(J - 1)
+            empty_dz(J - 1)
+            if J + 2 < TILES:
+                for i in range(first + 8, first + 12):
+                    turn(i)
+                    empty_turn(i)
+            if J >= 4:
+                store_out(J - 4)
+        store_out(LAST - 4)
+        store_out(LAST - 3)
 
         L = LAST
         last = {}
+        prod[L] = sb("prod", [P, 2, 2 * D], F32, 2)
 
-        def last_dpre(half):
-            last[half] = rotating(("last", half), [P, 2, D // 2])
+        def last_dpre(half, pair):
+            last[half, pair] = rotating(("last", half, pair), [P, 2, D // 2])
             for k in range(2):
                 for h in range(2):
-                    g_pass(last[half][:, k, :], S * L + 2 + k, h, h == 0, h == 1, (left, right)[half])
+                    g_pass(last[half, pair][:, k, :], S * L + 2 * pair + k, h, h == 0, h == 1, (left, right)[half])
 
-        def last_times_noise(half):
+        def last_times_noise(half, pair):
             cols = (left, right)[half]
             nc.vector.tensor_tensor(
-                out=prod[L][:, :, D : 2 * D][:, :, cols], in0=last[half][:],
-                in1=noise[S * L + 2][0][:].rearrange("p (s d) -> p s d", s=2)[:, :, cols], op=MULT,
+                out=prod[L][:, :, pair * D : (pair + 1) * D][:, :, cols], in0=last[half, pair][:],
+                in1=noise[S * L][0][:].rearrange("p (s d) -> p s d", s=S)[:, 2 * pair : 2 * pair + 2, cols], op=MULT,
             )
 
         def last_add_pairs(half):
@@ -507,81 +473,60 @@ def tile_hetxlhead_pa_v_kernel(
             acc[m] = in_bank(bank, ("weight", m), [P, D])
             weight_pass(m, 0)
 
-        window(L)
-        store_out(L - 4)
-        side_half(6)
-        side_half(7)
-        if keeps(L - 1):
-            keep(L - 1)
-        direct(S * (L - 1), S * (L - 1) + 2)
-        turn_dz(L - 2)
-        empty_dz(L - 2)
-        sigmoid(L - 1)
-        keep(L)
-        quant_g(S * L + 2, S * L + 4)
-        quant_dz(L - 3)
-        direct(S * (L - 1) + 2, S * L)
-        dz_pass(L - 3)
-        if not keeps(L - 3):
-            empty_out(L - 3)
-            store_out(L - 3)
-        add_pairs(L - 1, nc.vector, GPSIMD_COLUMNS, 2 * D)
-        quant_dz(L - 2)
-        add_all(L - 1)
-        side_quant(3)
         part[L] = sb("part", [P, 2 * D], F32, 2)
         dstd[L] = sb("dstd", [P, D], F32, 2)
         sigmoid(L)
-        last_dpre(0)
-        dz_pass(L - 2)
-        last_dpre(1)
+        quant_dz(L - 2)
+        side_quant(3)
+        for half in range(2):
+            for pair in range(2):
+                last_dpre(half, pair)
+        last_times_noise(0, 0)
         make_dz(L - 1)
-        if keeps(L - 3):
-            empty_out(L - 3)
-            store_out(L - 3)
-        last_times_noise(0)
+        last_times_noise(0, 1)
+        last_times_noise(1, 0)
+        dz_pass(L - 2)
         empty_out(L - 2)
         store_out(L - 2)
-        last_times_noise(1)
-        free = [k for k in range(ROTATING) if k not in (bank_of["last", 0], bank_of["last", 1], bank_of["dz", L - 2])]
-        direct(S * L, S * L + 2)
-        open_weight(0, free[0])
-        open_weight(2, free[1])
-        turn_dz(L - 1, bank_of["dz", L - 2])
+        direct(S * L, S * L + 1)
+        turn_dz(L - 1, bank_of["last", 0, 0])
         empty_dz(L - 1)
-        direct(S * L + 2, S * L + 4)
+        direct(S * L + 1, S * L + 4)
         last_add_pairs(0)
-        last_add_pairs(1)
+        last_times_noise(1, 1)
         last_add_all(0)
         quant_dz(L - 1)
-        last_make_dz(0)
-        last_add_all(1)
         dz_pass(L - 1)
+        open_weight(0, bank_of["dz", L - 2])
+        open_weight(2, bank_of["last", 0, 1])
+        last_make_dz(0)
         t = grouped_w()
+        last_add_pairs(1)
         interleave(nc.vector.tensor_copy, t, dz[1], quarter[0])
         interleave(nc.scalar.copy, t, dz[1], quarter[2])
-        last_make_dz(1)
-        quant_w(dzq[1], t, E5M2, quarter[0])
-        open_weight(1, bank_of["last", 0])
-        open_weight(3, bank_of["last", 1])
         empty_out(L - 1)
         store_out(L - 1)
-        turn_dz(L, bank_of["dz", L - 2])
-        weight_pass(0, 1)
-        empty_dz(L)
+        last_add_all(1)
+        quant_w(dzq[1], t, E5M2, quarter[0])
         quant_w(dzq[1], t, E5M2, quarter[2])
+        last_make_dz(1)
+        open_weight(1, bank_of["last", 1, 0])
+        weight_pass(0, 1)
         weight_pass(2, 1)
+        store_weight(0, nc.scalar.copy)
+        turn_dz(L, bank_of["last", 0, 0])
+        empty_dz(L)
+        open_weight(3, bank_of["last", 1, 1])
         interleave(nc.vector.tensor_copy, t, dz[1], quarter[1])
         interleave(nc.vector.tensor_copy, t, dz[1], quarter[3])
         quant_w(dzq[1], t, E5M2, quarter[1])
         weight_pass(1, 1)
-        quant_dz(L)
-        dz_pass(L)
+        store_weight(2, nc.scalar.copy)
         quant_w(dzq[1], t, E5M2, quarter[3])
+        quant_dz(L)
         weight_pass(3, 1)
-        store_weight(0, nc.scalar.copy)
-        store_weight(2, nc.vector.tensor_copy)
-        store_weight(1, nc.scalar.copy)
-        empty_out(L)
-        store_out(L)
+        dz_pass(L)
+        store_weight(1, nc.vector.tensor_copy)
         store_weight(3, nc.scalar.copy)
+        empty_out(L, nc.vector.tensor_copy)
+        store_out(L)

@@ -19,6 +19,7 @@ TILES = B // P
 LAST = TILES - 1
 PAIRS = 2 * TILES
 RUN = 8
+DZ_RUN = 4
 VECTOR_COLUMNS = 320
 WARM_UPS = 4
 UNITS = 8
@@ -36,7 +37,6 @@ def tile_hetxlhead_pa_v_kernel(
     n_view = noise_diag.rearrange("(g p j) s d -> g p (j s d)", p=P, j=4)
     z_view = z.rearrange("(g p j) d -> g p j d", p=P, j=4)
     o_view = out_0.rearrange("(g p j) d -> g j p d", p=P, j=4)
-    w_view = out_1.rearrange("(h a u e) n -> u h a e n", h=2, u=2, e=RUN)
 
     with ExitStack() as ctx:
         pool = ctx.enter_context(tc.tile_pool(name="sbuf", bufs=1))
@@ -98,9 +98,9 @@ def tile_hetxlhead_pa_v_kernel(
             nc.sync.dma_start(out=t[:], in_=src.rearrange("(p j) w -> p j w", j=4))
             return t
 
-        def load_sorted(src):
+        def load_sorted(src, run):
             t = sb("wraw", [P, 4, D], BF16, 3)
-            rows = src.rearrange("(a u b e) w -> u a b (e w)", u=2, b=RUN // 2, e=2)
+            rows = src.rearrange("(a u b e) w -> u a b (e w)", u=2, b=run // 2, e=2)
             for u in range(2):
                 nc.sync.dma_start(out=t[:, 2 * u : 2 * u + 2, :].rearrange("p e w -> p (e w)"), in_=rows[u])
             return t
@@ -191,16 +191,16 @@ def tile_hetxlhead_pa_v_kernel(
             nc.vector.tensor_tensor(out=part[J][:], in0=prod[J][:, 0], in1=prod[J][:, 1], op=ADD)
 
         def natural(ap, half):
-            return ap.rearrange("p (h a u e) -> p h u a e", h=2, u=2, e=RUN)[:, half]
+            return ap.rearrange("p (h a u e) -> p h u a e", h=2, u=2, e=DZ_RUN)[:, half]
 
         def by_line(ap, half):
-            return ap.rearrange("p (u h a e) -> p h u a e", h=2, u=2, e=RUN)[:, half]
+            return ap.rearrange("p (u h a e) -> p h u a e", h=2, u=2, e=DZ_RUN)[:, half]
 
         def whole_natural(ap):
-            return ap.rearrange("p (a u e) -> p u a e", u=2, e=RUN)
+            return ap.rearrange("p (a u e) -> p u a e", u=2, e=DZ_RUN)
 
         def whole_by_line(ap):
-            return ap.rearrange("p (u a e) -> p u a e", u=2, e=RUN)
+            return ap.rearrange("p (u a e) -> p u a e", u=2, e=DZ_RUN)
 
         def add_all(J):
             dstd[J] = sb("dstd", [P, D], F32, 2)
@@ -257,6 +257,13 @@ def tile_hetxlhead_pa_v_kernel(
                 in_=src[:, :, cols].rearrange("p j (c i) -> p c j i", i=4),
             )
 
+        def interleave_dz(copy, dst, src, cols):
+            lines = slice(cols.start // (2 * DZ_RUN), cols.stop // (2 * DZ_RUN))
+            copy(
+                out=dst[:].rearrange("p (a u e) j -> p u a j e", u=2, e=DZ_RUN)[:, :, lines],
+                in_=src[:].rearrange("p j (u a e) -> p u a j e", u=2, e=DZ_RUN)[:, :, lines],
+            )
+
         def quant_w(pair, t, fmt, cols=slice(0, D)):
             nc.vector.quantize_mx(
                 out=pair[0][:, cols].bitcast(fmt), scales=pair[1][:, cols],
@@ -269,7 +276,7 @@ def tile_hetxlhead_pa_v_kernel(
         def store_weight(m, copy):
             r = sb("res1", [P, D], F32, 4)
             copy(out=r[:], in_=acc[m][:])
-            nc.sync.dma_start(out=w_view[m // 2, m % 2], in_=r[:])
+            nc.sync.dma_start(out=out_1[quarter[m], :], in_=r[:])
 
         def weight_pass(m, g):
             cols = quarter[m]
@@ -291,9 +298,9 @@ def tile_hetxlhead_pa_v_kernel(
         nc.scalar.activation(dummy[:], dummy[:], mybir.ActivationFunctionType.Sigmoid)
 
         load_g(0, 1)
-        wc_raw = [load_sorted(w_cls[0:512, :])]
+        wc_raw = [load_sorted(w_cls[0:512, :], RUN)]
         load_g(1, 2)
-        wc_raw.append(load_sorted(w_cls[512:1024, :]))
+        wc_raw.append(load_sorted(w_cls[512:1024, :], RUN))
         load_g(2, 4)
         load_n(0, 2)
         load_g(4, 6)
@@ -304,7 +311,7 @@ def tile_hetxlhead_pa_v_kernel(
         load_z(0, 1)
         load_n(4, 8)
         load_g(12, 16)
-        wd_raw = load_sorted(w_diag)
+        wd_raw = load_sorted(w_diag, DZ_RUN)
         load_z(1, 1)
         load_n(8, 12)
         load_g(16, 20)
@@ -387,8 +394,10 @@ def tile_hetxlhead_pa_v_kernel(
                 lo, hi = max(a, 4 * k) - 4 * k, min(b, 4 * k + 4) - 4 * k
                 if lo == 0:
                     grouped[k] = grouped_w()
-                src = dz[0] if beside[k][0] is None else beside[k][0]
-                interleave(nc.scalar.copy, grouped[k], src, slice(lo * P, hi * P))
+                if beside[k][0] is None:
+                    interleave_dz(nc.scalar.copy, grouped[k], dz[0], slice(lo * P, hi * P))
+                else:
+                    interleave(nc.scalar.copy, grouped[k], beside[k][0], slice(lo * P, hi * P))
 
         def side_quant(k):
             quant_w(beside[k][1], grouped[k], beside[k][2])
@@ -498,35 +507,35 @@ def tile_hetxlhead_pa_v_kernel(
         quant_dz(L - 1)
         dz_pass(L - 1)
         open_weight(0, bank_of["dz", L - 2])
-        open_weight(2, bank_of["last", 0, 1])
+        open_weight(1, bank_of["last", 0, 1])
         last_make_dz(0)
         t = grouped_w()
         last_add_pairs(1)
-        interleave(nc.vector.tensor_copy, t, dz[1], quarter[0])
-        interleave(nc.scalar.copy, t, dz[1], quarter[2])
+        interleave_dz(nc.vector.tensor_copy, t, dz[1], quarter[0])
+        interleave_dz(nc.scalar.copy, t, dz[1], quarter[1])
         empty_out(L - 1)
         store_out(L - 1)
         last_add_all(1)
         quant_w(dzq[1], t, E5M2, quarter[0])
-        quant_w(dzq[1], t, E5M2, quarter[2])
+        quant_w(dzq[1], t, E5M2, quarter[1])
         last_make_dz(1)
-        open_weight(1, bank_of["last", 1, 0])
+        open_weight(2, bank_of["last", 1, 0])
         weight_pass(0, 1)
-        weight_pass(2, 1)
+        weight_pass(1, 1)
         store_weight(0, nc.scalar.copy)
         turn_dz(L, bank_of["last", 0, 0])
         empty_dz(L)
         open_weight(3, bank_of["last", 1, 1])
-        interleave(nc.vector.tensor_copy, t, dz[1], quarter[1])
-        interleave(nc.vector.tensor_copy, t, dz[1], quarter[3])
-        quant_w(dzq[1], t, E5M2, quarter[1])
-        weight_pass(1, 1)
-        store_weight(2, nc.scalar.copy)
+        interleave_dz(nc.vector.tensor_copy, t, dz[1], quarter[2])
+        interleave_dz(nc.vector.tensor_copy, t, dz[1], quarter[3])
+        quant_w(dzq[1], t, E5M2, quarter[2])
+        weight_pass(2, 1)
+        store_weight(1, nc.scalar.copy)
         quant_w(dzq[1], t, E5M2, quarter[3])
         quant_dz(L)
         weight_pass(3, 1)
         dz_pass(L)
-        store_weight(1, nc.vector.tensor_copy)
+        store_weight(2, nc.vector.tensor_copy)
         store_weight(3, nc.scalar.copy)
         empty_out(L, nc.vector.tensor_copy)
         store_out(L)

@@ -310,8 +310,8 @@ def tile_hetxlhead_pa_v_kernel(
         load_g(10, 12)
         load_z(0, 1)
         load_n(4, 8)
-        load_g(12, 16)
         wd_raw = load_sorted(w_diag, DZ_RUN)
+        load_g(12, 16)
         load_z(1, 1)
         load_n(8, 12)
         load_g(16, 20)
@@ -384,7 +384,6 @@ def tile_hetxlhead_pa_v_kernel(
         add_pairs(0)
         quant_g(6, 8)
         add_all(0)
-        prescale(24, 24 + VECTOR_UNITS)
 
         grouped = {}
         beside = [(wd_raw, wd, E4M3), (ft_raw[0], ft[0], E4M3), (ft_raw[1], ft[1], E4M3), (None, dzq[0], E5M2)]
@@ -418,6 +417,8 @@ def tile_hetxlhead_pa_v_kernel(
             sigmoid(J)
             if J >= 2:
                 quant_dz(J - 2)
+            if J + 2 < TILES:
+                prescale(2 * S * (J + 2), 2 * S * (J + 2) + VECTOR_UNITS)
             if J == 2:
                 side_quant(0)
             direct(first, first + S)
@@ -427,13 +428,9 @@ def tile_hetxlhead_pa_v_kernel(
             quant_g(first + 4, first + 6)
             add_pairs(J)
             quant_g(first + 6, first + 8)
-            if J == 3:
-                side_quant(1)
             add_all(J)
-            if J + 3 < TILES:
-                prescale(2 * S * (J + 3), 2 * S * (J + 3) + VECTOR_UNITS)
-            elif J < LAST - 1:
-                side_quant(2)
+            if J in (3, 4):
+                side_quant(J - 2)
             turn_dz(J - 1)
             empty_dz(J - 1)
             if J + 2 < TILES:

@@ -21,9 +21,9 @@ PAIRS = 2 * TILES
 RUN = 8
 DZ_RUN = 4
 VECTOR_COLUMNS = 320
-WARM_UPS = 4
+WARM_UPS = 3
 UNITS = 8
-VECTOR_UNITS = 6
+SCALAR_UNITS = 5
 ROTATING, SUMS = 5, 3
 FLOPS = 2 * (B * S * C * D + B * D * D + D * D * B)
 BYTES = 2 * (B * S * C + B * S * D + B * D + D * D + C * D) + 4 * (B * D) + 4 * (B * D + D * D)
@@ -160,12 +160,14 @@ def tile_hetxlhead_pa_v_kernel(
             for h in range(2):
                 g_pass(dpb[i][:], i, h, h == 0, h == 1)
 
-        def first_passes(i, h):
+        def dpre_half(i, h):
             if h == 0:
-                dpb[i] = rotating(("dpre", i), [P, D])
-                if i == 0:
-                    outb[0] = summing(0)
+                dpb[i] = in_bank(ROTATING + 1 + i, ("dpre", i), [P, D])
             g_pass(dpb[i][:], i, h, h == 0, h == 1)
+
+        def direct_half(i, h):
+            if i == 0 and h == 0:
+                outb[0] = summing(0)
             g_pass(outb[0][:], i, h, i == 0 and h == 0, False)
 
         def direct(a, b):
@@ -310,17 +312,17 @@ def tile_hetxlhead_pa_v_kernel(
         load_g(10, 12)
         load_z(0, 1)
         load_n(4, 8)
-        wd_raw = load_sorted(w_diag, DZ_RUN)
         load_g(12, 16)
-        load_z(1, 1)
         load_n(8, 12)
+        load_z(1, 1)
+        wd_raw = load_sorted(w_diag, DZ_RUN)
         load_g(16, 20)
-        ft_raw = [load_rows(features[0:512, :])]
-        load_z(2, 2)
         load_n(12, 16)
+        load_z(2, 2)
+        ft_raw = [load_rows(features[0:512, :])]
         load_g(20, 24)
-        ft_raw.append(load_rows(features[512:1024, :]))
         load_n(16, 20)
+        ft_raw.append(load_rows(features[512:1024, :]))
         load_g(24, 28)
         load_z(4, 2)
         load_n(20, 24)
@@ -343,42 +345,45 @@ def tile_hetxlhead_pa_v_kernel(
         turn(1)
         quant_w(wc[0], wg[0], E4M3)
         quant_g(0, 1)
-        first_passes(0, 0)
+        dpre_half(0, 0)
+        direct_half(0, 0)
+        empty_turn(1, 1)
         interleave(nc.vector.tensor_copy, wg[1], wc_raw[1], on_vector)
         interleave(nc.scalar.copy, wg[1], wc_raw[1], on_scalar)
-        empty_turn(1, 1)
+        quant_g(1, 2)
+        dpre_half(1, 0)
+        direct_half(1, 0)
         prescale(4, 8)
         quant_w(wc[1], wg[1], E4M3)
-        quant_g(1, 2)
         turn(2)
         turn(3)
-        first_passes(0, 1)
+        dpre_half(0, 1)
+        dpre_half(1, 1)
+        direct_half(0, 1)
+        direct_half(1, 1)
         empty_turn(2)
         empty_turn(3)
-        first_passes(1, 0)
-        first_passes(1, 1)
         prescale(8, 12)
         times_noise(0)
-        turn(4)
-        turn(5)
         quant_g(2, 4)
         times_noise(1)
-        prescale(12, 14)
-        scalar_prescale(14, 16)
+        turn(4)
+        turn(5)
         empty_turn(4)
         empty_turn(5)
         dpre(2)
         dpre(3)
-        turn(6)
-        turn(7)
+        prescale(12, 16)
         times_noise(2)
         scalar_prescale(18, 20)
+        turn(6)
+        turn(7)
+        times_noise(3)
+        quant_g(4, 6)
         empty_turn(6)
         empty_turn(7)
-        quant_g(4, 6)
-        times_noise(3)
-        prescale(16, 18)
         direct(2, 4)
+        prescale(16, 18)
         prescale(20, 24)
         sigmoid(0)
         add_pairs(0)
@@ -388,52 +393,60 @@ def tile_hetxlhead_pa_v_kernel(
         grouped = {}
         beside = [(wd_raw, wd, E4M3), (ft_raw[0], ft[0], E4M3), (ft_raw[1], ft[1], E4M3), (None, dzq[0], E5M2)]
 
-        def side_quarters(a, b):
-            for k in range(a // 4, (b - 1) // 4 + 1):
-                lo, hi = max(a, 4 * k) - 4 * k, min(b, 4 * k + 4) - 4 * k
-                if lo == 0:
-                    grouped[k] = grouped_w()
-                if beside[k][0] is None:
-                    interleave_dz(nc.scalar.copy, grouped[k], dz[0], slice(lo * P, hi * P))
-                else:
-                    interleave(nc.scalar.copy, grouped[k], beside[k][0], slice(lo * P, hi * P))
+        def side_half(n):
+            k, cols = n // 2, (left, right)[n % 2]
+            if n % 2 == 0:
+                grouped[k] = grouped_w()
+            if beside[k][0] is None:
+                interleave_dz(nc.scalar.copy, grouped[k], dz[0], cols)
+            else:
+                interleave(nc.scalar.copy, grouped[k], beside[k][0], cols)
 
-        def side_quant(k):
-            quant_w(beside[k][1], grouped[k], beside[k][2])
+        def side_quant(a, b):
+            k = a // 2
+            quant_w(beside[k][1], grouped[k], beside[k][2], slice((a - 2 * k) * D // 2, (b - 2 * k) * D // 2))
 
         for i in range(8, 12):
             turn(i)
             empty_turn(i)
+        done = 0
         for J in range(1, LAST):
             first = S * J
+            more = J + 2 < TILES
+            count = 0 if J == 1 else 2 - J % 2
+            if J == 3:
+                dz_pass(0)
+                empty_out(0)
             for i in range(first, first + S):
                 dpre(i)
                 times_noise(i)
                 if i == first:
                     make_dz(J - 1)
-            side_quarters(3 * (J - 1), min(3 * J, 16))
-            if J + 2 < TILES:
-                scalar_prescale(2 * S * (J + 2) + VECTOR_UNITS, 2 * S * (J + 3))
-            sigmoid(J)
             if J >= 2:
                 quant_dz(J - 2)
-            if J + 2 < TILES:
-                prescale(2 * S * (J + 2), 2 * S * (J + 2) + VECTOR_UNITS)
-            if J == 2:
-                side_quant(0)
+            for n in range(done, done + count):
+                side_half(n)
+            if more:
+                split = 2 * S * (J + 3) - (SCALAR_UNITS - 2 * count)
+                prescale(2 * S * (J + 2), split)
+                scalar_prescale(split, 2 * S * (J + 3))
+            sigmoid(J)
             direct(first, first + S)
-            if J >= 2:
+            if J >= 3:
                 dz_pass(J - 2)
                 empty_out(J - 2)
             quant_g(first + 4, first + 6)
+            if J == 2:
+                side_quant(0, 2)
             add_pairs(J)
             quant_g(first + 6, first + 8)
             add_all(J)
-            if J in (3, 4):
-                side_quant(J - 2)
+            if J > 2 and (done + count) // 2 > done // 2:
+                side_quant(done // 2 * 2, done // 2 * 2 + 2)
+            done += count
             turn_dz(J - 1)
             empty_dz(J - 1)
-            if J + 2 < TILES:
+            if more:
                 for i in range(first + 8, first + 12):
                     turn(i)
                     empty_turn(i)
@@ -483,7 +496,6 @@ def tile_hetxlhead_pa_v_kernel(
         dstd[L] = sb("dstd", [P, D], F32, 2)
         sigmoid(L)
         quant_dz(L - 2)
-        side_quant(3)
         for half in range(2):
             for pair in range(2):
                 last_dpre(half, pair)

@@ -171,10 +171,10 @@ def tile_hetxlhead_pa_v_kernel(
             g_pass(outb[0][:], i, h, i == 0 and h == 0, False)
 
         def direct(a, b):
-            J = a // S
-            if a % S == 0:
-                outb[J] = summing(J)
             for i in range(a, b):
+                J = i // S
+                if i % S == 0:
+                    outb[J] = summing(J)
                 for h in range(2):
                     g_pass(outb[J][:], i, h, i % S == 0 and h == 0, False)
 
@@ -431,7 +431,7 @@ def tile_hetxlhead_pa_v_kernel(
                 prescale(2 * S * (J + 2), split)
                 scalar_prescale(split, 2 * S * (J + 3))
             sigmoid(J)
-            direct(first, first + S)
+            direct(max(first - 1, S), first + S - (1 if more else 0))
             if J >= 3:
                 dz_pass(J - 2)
                 empty_out(J - 2)

@@ -229,9 +229,9 @@ def tile_hetxlhead_pa_v_kernel(
             for u in range(2):
                 nc.tensor.transpose(dzt_b[J][:, u, :], words[:, u * P : (u + 1) * P], ident[:])
 
-        def empty_dz(J):
+        def empty_dz(J, copy=nc.scalar.copy):
             dzt[J] = sb("dzt", [P, P, 2], F32, 2)
-            nc.scalar.copy(out=dzt[J][:], in_=dzt_b[J][:].rearrange("p u r -> p r u"))
+            copy(out=dzt[J][:], in_=dzt_b[J][:].rearrange("p u r -> p r u"))
 
         def quant_dz(J):
             dzc[J] = quantised("dzt", P, 2)
@@ -347,19 +347,19 @@ def tile_hetxlhead_pa_v_kernel(
         quant_g(0, 1)
         dpre_half(0, 0)
         direct_half(0, 0)
-        empty_turn(1, 1)
         interleave(nc.vector.tensor_copy, wg[1], wc_raw[1], on_vector)
         interleave(nc.scalar.copy, wg[1], wc_raw[1], on_scalar)
-        quant_g(1, 2)
-        dpre_half(1, 0)
-        direct_half(1, 0)
+        empty_turn(1, 1)
         prescale(4, 8)
         quant_w(wc[1], wg[1], E4M3)
+        quant_g(1, 2)
         turn(2)
         turn(3)
         dpre_half(0, 1)
+        dpre_half(1, 0)
         dpre_half(1, 1)
         direct_half(0, 1)
+        direct_half(1, 0)
         direct_half(1, 1)
         empty_turn(2)
         empty_turn(3)
@@ -441,7 +441,7 @@ def tile_hetxlhead_pa_v_kernel(
             add_pairs(J)
             quant_g(first + 6, first + 8)
             add_all(J)
-            if J > 2 and (done + count) // 2 > done // 2:
+            if 2 < J < LAST - 1 and (done + count) // 2 > done // 2:
                 side_quant(done // 2 * 2, done // 2 * 2 + 2)
             done += count
             turn_dz(J - 1)
@@ -488,6 +488,13 @@ def tile_hetxlhead_pa_v_kernel(
                 out=by_line(dz[1][:, 3, :], half), in0=by_line(dstd[L][:], half), in1=by_line(sig[L][:], half), op=MULT
             )
 
+        def last_make_dz_quarter(m):
+            lines = slice(16 * m, 16 * (m + 1))
+            nc.vector.tensor_tensor(
+                out=whole_by_line(dz[1][:, 3, :])[:, :, lines], in0=whole_by_line(dstd[L][:])[:, :, lines],
+                in1=whole_by_line(sig[L][:])[:, :, lines], op=MULT,
+            )
+
         def open_weight(m, bank):
             acc[m] = in_bank(bank, ("weight", m), [P, D])
             weight_pass(m, 0)
@@ -495,7 +502,7 @@ def tile_hetxlhead_pa_v_kernel(
         part[L] = sb("part", [P, 2 * D], F32, 2)
         dstd[L] = sb("dstd", [P, D], F32, 2)
         sigmoid(L)
-        quant_dz(L - 2)
+        side_quant(6, 7)
         for half in range(2):
             for pair in range(2):
                 last_dpre(half, pair)
@@ -503,20 +510,23 @@ def tile_hetxlhead_pa_v_kernel(
         make_dz(L - 1)
         last_times_noise(0, 1)
         last_times_noise(1, 0)
-        dz_pass(L - 2)
-        empty_out(L - 2)
-        store_out(L - 2)
+        quant_dz(L - 2)
         direct(S * L, S * L + 1)
         turn_dz(L - 1, bank_of["last", 0, 0])
         empty_dz(L - 1)
+        dz_pass(L - 2)
+        empty_out(L - 2)
+        store_out(L - 2)
         direct(S * L + 1, S * L + 4)
         last_add_pairs(0)
         last_times_noise(1, 1)
         last_add_all(0)
         quant_dz(L - 1)
+        quant_w(dzq[0], grouped[3], E5M2, quarter[2])
         dz_pass(L - 1)
         open_weight(0, bank_of["dz", L - 2])
         open_weight(1, bank_of["last", 0, 1])
+        open_weight(2, bank_of["last", 1, 0])
         last_make_dz(0)
         t = grouped_w()
         last_add_pairs(1)
@@ -527,24 +537,25 @@ def tile_hetxlhead_pa_v_kernel(
         last_add_all(1)
         quant_w(dzq[1], t, E5M2, quarter[0])
         quant_w(dzq[1], t, E5M2, quarter[1])
-        last_make_dz(1)
-        open_weight(2, bank_of["last", 1, 0])
+        last_make_dz_quarter(2)
+        last_make_dz_quarter(3)
+        quant_w(dzq[0], grouped[3], E5M2, quarter[3])
         weight_pass(0, 1)
         weight_pass(1, 1)
         store_weight(0, nc.scalar.copy)
         turn_dz(L, bank_of["last", 0, 0])
-        empty_dz(L)
+        store_weight(1, nc.scalar.copy)
         open_weight(3, bank_of["last", 1, 1])
         interleave_dz(nc.vector.tensor_copy, t, dz[1], quarter[2])
         interleave_dz(nc.vector.tensor_copy, t, dz[1], quarter[3])
         quant_w(dzq[1], t, E5M2, quarter[2])
         weight_pass(2, 1)
-        store_weight(1, nc.scalar.copy)
+        empty_dz(L, nc.vector.tensor_copy)
         quant_w(dzq[1], t, E5M2, quarter[3])
-        quant_dz(L)
         weight_pass(3, 1)
+        quant_dz(L)
         dz_pass(L)
-        store_weight(2, nc.vector.tensor_copy)
-        store_weight(3, nc.scalar.copy)
-        empty_out(L, nc.vector.tensor_copy)
+        store_weight(2, nc.scalar.copy)
+        store_weight(3, nc.vector.tensor_copy)
+        empty_out(L)
         store_out(L)

@@ -189,7 +189,7 @@ def tile_hetxlhead_pa_v_kernel(
             )
 
         def add_pairs(J):
-            part[J] = sb("part", [P, 2 * D], F32, 2)
+            part[J] = sb("part", [P, 2 * D], F32, 1)
             nc.vector.tensor_tensor(out=part[J][:], in0=prod[J][:, 0], in1=prod[J][:, 1], op=ADD)
 
         def natural(ap, half):
@@ -359,8 +359,6 @@ def tile_hetxlhead_pa_v_kernel(
         dpre_half(1, 0)
         dpre_half(1, 1)
         direct_half(0, 1)
-        direct_half(1, 0)
-        direct_half(1, 1)
         empty_turn(2)
         empty_turn(3)
         prescale(8, 12)
@@ -382,7 +380,9 @@ def tile_hetxlhead_pa_v_kernel(
         quant_g(4, 6)
         empty_turn(6)
         empty_turn(7)
-        direct(2, 4)
+        direct_half(1, 0)
+        direct_half(1, 1)
+        direct(2, 3)
         prescale(16, 18)
         prescale(20, 24)
         sigmoid(0)
@@ -431,7 +431,7 @@ def tile_hetxlhead_pa_v_kernel(
                 prescale(2 * S * (J + 2), split)
                 scalar_prescale(split, 2 * S * (J + 3))
             sigmoid(J)
-            direct(max(first - 1, S), first + S - (1 if more else 0))
+            direct(first - (1 if J == 1 else 2), first + S - (2 if more else 1))
             if J >= 3:
                 dz_pass(J - 2)
                 empty_out(J - 2)
@@ -499,7 +499,8 @@ def tile_hetxlhead_pa_v_kernel(
             acc[m] = in_bank(bank, ("weight", m), [P, D])
             weight_pass(m, 0)
 
-        part[L] = sb("part", [P, 2 * D], F32, 2)
+        kept = sb("kept", [P, D], F32, 1)
+        part[L] = sb("part", [P, 2 * D], F32, 1)
         dstd[L] = sb("dstd", [P, D], F32, 2)
         sigmoid(L)
         side_quant(6, 7)
@@ -511,15 +512,17 @@ def tile_hetxlhead_pa_v_kernel(
         last_times_noise(0, 1)
         last_times_noise(1, 0)
         quant_dz(L - 2)
-        direct(S * L, S * L + 1)
+        direct(S * L - 1, S * L)
         turn_dz(L - 1, bank_of["last", 0, 0])
         empty_dz(L - 1)
         dz_pass(L - 2)
         empty_out(L - 2)
         store_out(L - 2)
-        direct(S * L + 1, S * L + 4)
+        direct(S * L, S * L + 3)
         last_add_pairs(0)
         last_times_noise(1, 1)
+        for half in range(2):
+            nc.scalar.copy(out=kept[:, (left, right)[half]], in_=last[half, 1][:, 1, :])
         last_add_all(0)
         quant_dz(L - 1)
         quant_w(dzq[0], grouped[3], E5M2, quarter[2])
@@ -556,6 +559,7 @@ def tile_hetxlhead_pa_v_kernel(
         quant_dz(L)
         dz_pass(L)
         store_weight(2, nc.scalar.copy)
-        store_weight(3, nc.vector.tensor_copy)
-        empty_out(L)
+        store_weight(3, nc.scalar.copy)
+        res[L] = sb("res", [P, D], F32, 4)
+        nc.vector.tensor_tensor(out=res[L][:], in0=outb[L][:], in1=kept[:], op=ADD)
         store_out(L)

@@ -23,8 +23,10 @@ DZ_RUN = 4
 VECTOR_COLUMNS = 320
 WARM_UPS = 3
 UNITS = 8
-SCALAR_UNITS = 5
+SCALAR_UNITS = 4
 ROTATING, SUMS = 5, 3
+PAIRED = range(2, 7)
+KEPT = range(0, 5)
 FLOPS = 2 * (B * S * C * D + B * D * D + D * D * B)
 BYTES = 2 * (B * S * C + B * S * D + B * D + D * D + C * D) + 4 * (B * D) + 4 * (B * D + D * D)
 
@@ -133,7 +135,7 @@ def tile_hetxlhead_pa_v_kernel(
         def empty_turn(i, count=2):
             at = i % count
             if at == 0:
-                t = sb("grp", [P, count, 2, P, 2], F32, 3)
+                t = sb("grp%d" % (i // 2 % 4 if count == 2 else 2 + i), [P, count, 2, P, 2], F32, 1)
                 for k in range(count):
                     grp[i + k] = t
             nc.scalar.copy(out=grp[i][:, at], in_=trb[i][:].rearrange("p h u r -> p h r u"))
@@ -170,13 +172,14 @@ def tile_hetxlhead_pa_v_kernel(
                 outb[0] = summing(0)
             g_pass(outb[0][:], i, h, i == 0 and h == 0, False)
 
-        def direct(a, b):
-            for i in range(a, b):
+        def direct(samples):
+            for i in samples:
                 J = i // S
-                if i % S == 0:
+                opens = J not in outb
+                if opens:
                     outb[J] = summing(J)
                 for h in range(2):
-                    g_pass(outb[J][:], i, h, i % S == 0 and h == 0, False)
+                    g_pass(outb[J][:], i, h, opens and h == 0, False)
 
         def times_noise(i):
             J, s = divmod(i, S)
@@ -188,9 +191,10 @@ def tile_hetxlhead_pa_v_kernel(
                 in1=t[:, at * D : (at + 1) * D], op=MULT,
             )
 
-        def add_pairs(J):
-            part[J] = sb("part", [P, 2 * D], F32, 1)
-            nc.vector.tensor_tensor(out=part[J][:], in0=prod[J][:, 0], in1=prod[J][:, 1], op=ADD)
+        def add_pairs(J, eng=nc.gpsimd):
+            tag = "part" if J not in PAIRED else "wg0" if J == LAST - 1 else "grp%d" % ((2 * J + 3) % 4)
+            part[J] = sb(tag, [P, 2 * D], F32, 1)
+            eng.tensor_tensor(out=part[J][:], in0=prod[J][:, 0], in1=prod[J][:, 1], op=ADD)
 
         def natural(ap, half):
             return ap.rearrange("p (h a u e) -> p h u a e", h=2, u=2, e=DZ_RUN)[:, half]
@@ -247,8 +251,15 @@ def tile_hetxlhead_pa_v_kernel(
             )
 
         def empty_out(J, copy=nc.scalar.copy):
-            res[J] = sb("res", [P, D], F32, 4)
+            res[J] = sb("res", [P, D], F32, 7)
             copy(out=res[J][:], in_=outb[J][:])
+
+        def keep(J):
+            res[J] = sb("res", [P, D], F32, 7)
+            nc.scalar.copy(out=res[J][:], in_=dpb[S * J + 3][:])
+
+        def add_kept(J):
+            nc.vector.tensor_tensor(out=res[J][:], in0=outb[J][:], in1=res[J][:], op=ADD)
 
         def store_out(J):
             nc.sync.dma_start(out=o_view[J // 4, J % 4], in_=res[J][:])
@@ -272,11 +283,11 @@ def tile_hetxlhead_pa_v_kernel(
                 in_=t[:, cols, :].rearrange("p w j -> p (w j)"),
             )
 
-        def grouped_w():
-            return sb("wg", [P, D, 4], BF16, 2)
+        def grouped_w(slot):
+            return sb("wg%d" % slot, [P, D, 4], BF16, 1)
 
         def store_weight(m, copy):
-            r = sb("res1", [P, D], F32, 4)
+            r = sb("res", [P, D], F32, 7)
             copy(out=r[:], in_=acc[m][:])
             nc.sync.dma_start(out=out_1[quarter[m], :], in_=r[:])
 
@@ -332,7 +343,7 @@ def tile_hetxlhead_pa_v_kernel(
         load_n(28, 32)
 
         on_vector, on_scalar = slice(0, VECTOR_COLUMNS), slice(VECTOR_COLUMNS, D)
-        wg = [grouped_w(), grouped_w()]
+        wg = [grouped_w(0), grouped_w(1)]
         prescale(0, 2)
         turn(0)
         unread = rotating("unread", [P, D])
@@ -377,16 +388,17 @@ def tile_hetxlhead_pa_v_kernel(
         turn(6)
         turn(7)
         times_noise(3)
-        quant_g(4, 6)
         empty_turn(6)
         empty_turn(7)
+        keep(0)
         direct_half(1, 0)
         direct_half(1, 1)
-        direct(2, 3)
+        direct([2])
         prescale(16, 18)
         prescale(20, 24)
         sigmoid(0)
-        add_pairs(0)
+        quant_g(4, 6)
+        add_pairs(0, nc.vector)
         quant_g(6, 8)
         add_all(0)
 
@@ -396,159 +408,175 @@ def tile_hetxlhead_pa_v_kernel(
         def side_half(n):
             k, cols = n // 2, (left, right)[n % 2]
             if n % 2 == 0:
-                grouped[k] = grouped_w()
+                grouped[k] = grouped_w(k % 3)
             if beside[k][0] is None:
                 interleave_dz(nc.scalar.copy, grouped[k], dz[0], cols)
             else:
                 interleave(nc.scalar.copy, grouped[k], beside[k][0], cols)
 
-        def side_quant(a, b):
-            k = a // 2
-            quant_w(beside[k][1], grouped[k], beside[k][2], slice((a - 2 * k) * D // 2, (b - 2 * k) * D // 2))
+        def side_quant(k, cols=slice(0, D)):
+            quant_w(beside[k][1], grouped[k], beside[k][2], cols)
 
         for i in range(8, 12):
             turn(i)
             empty_turn(i)
-        done = 0
+        halves = {J: [] for J in range(1, LAST)}
+        halves[PAIRED[0]] = [0]
+        halves[LAST - 1] = [6, 7, 2, 3]
         for J in range(1, LAST):
             first = S * J
             more = J + 2 < TILES
-            count = 0 if J == 1 else 2 - J % 2
-            if J == 3:
-                dz_pass(0)
-                empty_out(0)
+            if J - 1 in PAIRED:
+                add_pairs(J - 1)
+            else:
+                make_dz(J - 1)
+            split = 2 * S * (J + 2) + SCALAR_UNITS - 2 * len(halves[J])
+            if J - 1 in PAIRED:
+                sigmoid(J - 1)
+            for n in halves[J][:2]:
+                side_half(n)
+            if more:
+                scalar_prescale(2 * S * (J + 2), split)
+            if J not in PAIRED:
+                sigmoid(J)
             for i in range(first, first + S):
                 dpre(i)
                 times_noise(i)
-                if i == first:
-                    make_dz(J - 1)
-            if J >= 2:
-                quant_dz(J - 2)
-            for n in range(done, done + count):
+                if i == first and J >= 3:
+                    dz_pass(J - 3)
+                    add_kept(J - 3)
+                    store_out(J - 3)
+            if J in KEPT:
+                keep(J)
+            if not more:
+                turn_dz(J - 2)
+                empty_dz(J - 2)
+            for n in halves[J][2:]:
                 side_half(n)
+            direct(range(first - (J == LAST - 1), first + S - (J < LAST - 1)))
             if more:
-                split = 2 * S * (J + 3) - (SCALAR_UNITS - 2 * count)
-                prescale(2 * S * (J + 2), split)
-                scalar_prescale(split, 2 * S * (J + 3))
-            sigmoid(J)
-            direct(first - (1 if J == 1 else 2), first + S - (2 if more else 1))
-            if J >= 3:
-                dz_pass(J - 2)
-                empty_out(J - 2)
-            quant_g(first + 4, first + 6)
-            if J == 2:
-                side_quant(0, 2)
-            add_pairs(J)
-            quant_g(first + 6, first + 8)
-            add_all(J)
-            if 2 < J < LAST - 1 and (done + count) // 2 > done // 2:
-                side_quant(done // 2 * 2, done // 2 * 2 + 2)
-            done += count
-            turn_dz(J - 1)
-            empty_dz(J - 1)
+                prescale(split, 2 * S * (J + 3))
+            if J - 1 in PAIRED:
+                add_all(J - 1)
+            elif J not in PAIRED:
+                add_pairs(J, nc.vector)
+            else:
+                interleave(nc.vector.tensor_copy, grouped[0], wd_raw, right)
+            if J >= 2 and more:
+                turn_dz(J - 2)
+                empty_dz(J - 2)
             if more:
                 for i in range(first + 8, first + 12):
                     turn(i)
                     empty_turn(i)
-            if J >= 4:
-                store_out(J - 4)
-        store_out(LAST - 4)
-        store_out(LAST - 3)
+            quant_g(first + 4, first + 6)
+            if not more:
+                quant_g(first + 6, first + 8)
+            if J >= 2:
+                quant_dz(J - 2)
+            if more:
+                quant_g(first + 6, first + 8)
+            else:
+                side_quant(3)
+            if J - 1 in PAIRED:
+                make_dz(J - 1, nc.vector)
+            elif J not in PAIRED:
+                add_all(J)
+            else:
+                side_quant(0)
 
         L = LAST
         last = {}
-        prod[L] = sb("prod", [P, 2, 2 * D], F32, 2)
+        prod[L] = sb("prod", [P, 4, S, P], F32, 2)
 
-        def last_dpre(half, pair):
-            last[half, pair] = rotating(("last", half, pair), [P, 2, D // 2])
-            for k in range(2):
+        def last_dpre(m):
+            last[m] = rotating(("last", m), [P, S, P])
+            for s in range(S):
                 for h in range(2):
-                    g_pass(last[half, pair][:, k, :], S * L + 2 * pair + k, h, h == 0, h == 1, (left, right)[half])
+                    g_pass(last[m][:, s, :], S * L + s, h, h == 0, h == 1, quarter[m])
 
-        def last_times_noise(half, pair):
-            cols = (left, right)[half]
+        def last_times_noise(m):
             nc.vector.tensor_tensor(
-                out=prod[L][:, :, pair * D : (pair + 1) * D][:, :, cols], in0=last[half, pair][:],
-                in1=noise[S * L][0][:].rearrange("p (s d) -> p s d", s=S)[:, 2 * pair : 2 * pair + 2, cols], op=MULT,
+                out=prod[L][:, m], in0=last[m][:],
+                in1=noise[S * L][0][:].rearrange("p (s d) -> p s d", s=S)[:, :, quarter[m]], op=MULT,
             )
 
-        def last_add_pairs(half):
-            cols = (left, right)[half]
-            views = [ap.rearrange("p (k d) -> p k d", k=2)[:, :, cols] for ap in (part[L][:], prod[L][:, 0], prod[L][:, 1])]
-            nc.vector.tensor_tensor(out=views[0], in0=views[1], in1=views[2], op=ADD)
+        def last_add_pairs(m):
+            nc.vector.tensor_tensor(out=part[L][:, m], in0=prod[L][:, m, 0:2], in1=prod[L][:, m, 2:4], op=ADD)
 
-        def last_add_all(half):
+        def lines(ap, m):
+            return whole_by_line(ap)[:, :, 16 * m : 16 * (m + 1)]
+
+        def last_add_all(m):
             nc.vector.tensor_tensor(
-                out=by_line(dstd[L][:], half), in0=natural(part[L][:, 0:D], half),
-                in1=natural(part[L][:, D : 2 * D], half), op=ADD,
+                out=lines(dstd[L][:], m), in0=whole_natural(part[L][:, m, 0]), in1=whole_natural(part[L][:, m, 1]), op=ADD
             )
 
-        def last_make_dz(half):
-            nc.vector.tensor_tensor(
-                out=by_line(dz[1][:, 3, :], half), in0=by_line(dstd[L][:], half), in1=by_line(sig[L][:], half), op=MULT
-            )
-
-        def last_make_dz_quarter(m):
-            lines = slice(16 * m, 16 * (m + 1))
-            nc.vector.tensor_tensor(
-                out=whole_by_line(dz[1][:, 3, :])[:, :, lines], in0=whole_by_line(dstd[L][:])[:, :, lines],
-                in1=whole_by_line(sig[L][:])[:, :, lines], op=MULT,
-            )
+        def last_make_dz(m):
+            nc.vector.tensor_tensor(out=lines(dz[1][:, 3, :], m), in0=lines(dstd[L][:], m), in1=lines(sig[L][:], m), op=MULT)
 
         def open_weight(m, bank):
             acc[m] = in_bank(bank, ("weight", m), [P, D])
             weight_pass(m, 0)
 
-        kept = sb("kept", [P, D], F32, 1)
-        part[L] = sb("part", [P, 2 * D], F32, 1)
-        dstd[L] = sb("dstd", [P, D], F32, 2)
+        add_pairs(L - 1)
+        sigmoid(L - 1)
+        side_half(4)
+        last_dpre(0)
+        dz_pass(L - 3)
+        last_times_noise(0)
+        add_kept(L - 3)
+        store_out(L - 3)
+        for m in range(1, 4):
+            last_dpre(m)
+            last_times_noise(m)
+        turn_dz(L - 2)
+        empty_dz(L - 2)
         sigmoid(L)
-        side_quant(6, 7)
-        for half in range(2):
-            for pair in range(2):
-                last_dpre(half, pair)
-        last_times_noise(0, 0)
-        make_dz(L - 1)
-        last_times_noise(0, 1)
-        last_times_noise(1, 0)
+        side_half(5)
+        direct(range(S * L, S * L + S - 1))
+        part[L] = sb("part", [P, 4, 2, P], F32, 1)
+        add_all(L - 1)
+        dstd[L] = sb("dstd", [P, D], F32, 2)
+        t = grouped_w(0)
         quant_dz(L - 2)
-        direct(S * L - 1, S * L)
-        turn_dz(L - 1, bank_of["last", 0, 0])
-        empty_dz(L - 1)
         dz_pass(L - 2)
         empty_out(L - 2)
         store_out(L - 2)
-        direct(S * L, S * L + 3)
         last_add_pairs(0)
-        last_times_noise(1, 1)
-        for half in range(2):
-            nc.scalar.copy(out=kept[:, (left, right)[half]], in_=last[half, 1][:, 1, :])
-        last_add_all(0)
-        quant_dz(L - 1)
-        quant_w(dzq[0], grouped[3], E5M2, quarter[2])
-        dz_pass(L - 1)
-        open_weight(0, bank_of["dz", L - 2])
-        open_weight(1, bank_of["last", 0, 1])
-        open_weight(2, bank_of["last", 1, 0])
-        last_make_dz(0)
-        t = grouped_w()
+        make_dz(L - 1, nc.vector)
+        turn_dz(L - 1, bank_of["dz", L - 2])
+        empty_dz(L - 1)
+        direct([S * L + S - 1])
         last_add_pairs(1)
-        interleave_dz(nc.vector.tensor_copy, t, dz[1], quarter[0])
+        last_add_all(0)
+        side_quant(1)
+        open_weight(0, bank_of["last", 0])
+        open_weight(1, bank_of["last", 1])
+        last_make_dz(0)
+        last_add_all(1)
+        interleave_dz(nc.scalar.copy, t, dz[1], quarter[0])
+        quant_dz(L - 1)
+        dz_pass(L - 1)
+        open_weight(2, bank_of["last", 2])
+        open_weight(3, bank_of["last", 3])
+        last_make_dz(1)
+        last_add_pairs(2)
         interleave_dz(nc.scalar.copy, t, dz[1], quarter[1])
+        side_quant(2)
+        last_add_all(2)
+        quant_w(dzq[1], t, E5M2, quarter[0])
+        weight_pass(0, 1)
         empty_out(L - 1)
         store_out(L - 1)
-        last_add_all(1)
-        quant_w(dzq[1], t, E5M2, quarter[0])
+        last_add_pairs(3)
+        last_make_dz(2)
+        last_add_all(3)
         quant_w(dzq[1], t, E5M2, quarter[1])
-        last_make_dz_quarter(2)
-        last_make_dz_quarter(3)
-        quant_w(dzq[0], grouped[3], E5M2, quarter[3])
-        weight_pass(0, 1)
         weight_pass(1, 1)
+        last_make_dz(3)
+        turn_dz(L, bank_of["dz", L - 1])
         store_weight(0, nc.scalar.copy)
-        turn_dz(L, bank_of["last", 0, 0])
-        store_weight(1, nc.scalar.copy)
-        open_weight(3, bank_of["last", 1, 1])
         interleave_dz(nc.vector.tensor_copy, t, dz[1], quarter[2])
         interleave_dz(nc.vector.tensor_copy, t, dz[1], quarter[3])
         quant_w(dzq[1], t, E5M2, quarter[2])
@@ -558,8 +586,8 @@ def tile_hetxlhead_pa_v_kernel(
         weight_pass(3, 1)
         quant_dz(L)
         dz_pass(L)
-        store_weight(2, nc.scalar.copy)
+        store_weight(1, nc.scalar.copy)
+        store_weight(2, nc.vector.tensor_copy)
         store_weight(3, nc.scalar.copy)
-        res[L] = sb("res", [P, D], F32, 4)
-        nc.vector.tensor_tensor(out=res[L][:], in0=outb[L][:], in1=kept[:], op=ADD)
+        empty_out(L, nc.vector.tensor_copy)
         store_out(L)

@@ -23,10 +23,11 @@ DZ_RUN = 4
 VECTOR_COLUMNS = 320
 WARM_UPS = 3
 UNITS = 8
-SCALAR_UNITS = 4
+SCALAR_UNITS = 5
 ROTATING, SUMS = 5, 3
-PAIRED = range(2, 7)
-KEPT = range(0, 5)
+KEPT = range(0, 3)
+SHORT = 432
+DIRECT = 3
 FLOPS = 2 * (B * S * C * D + B * D * D + D * D * B)
 BYTES = 2 * (B * S * C + B * S * D + B * D + D * D + C * D) + 4 * (B * D) + 4 * (B * D + D * D)
 
@@ -90,7 +91,7 @@ def tile_hetxlhead_pa_v_kernel(
             load_samples(n_view, D, "noise", 4, noise, a, b)
 
         def load_z(J, count):
-            t = sb("z", [P, count, D], F32, 3)
+            t = sb("z", [P, count, D], F32, 2)
             nc.sync.dma_start(out=t[:], in_=z_view[J // 4][:, J % 4 : J % 4 + count])
             for k in range(count):
                 zt[J + k] = t[:, k, :]
@@ -107,8 +108,8 @@ def tile_hetxlhead_pa_v_kernel(
                 nc.sync.dma_start(out=t[:, 2 * u : 2 * u + 2, :].rearrange("p e w -> p (e w)"), in_=rows[u])
             return t
 
-        def scale_views(a, b, tag):
-            t = sb(tag, [P, 2, 2 * P * (b - a) // RUN, RUN], BF16, 3)
+        def scale_views(a, b, tag, bufs):
+            t = sb(tag, [P, 2, 2 * P * (b - a) // RUN, RUN], BF16, bufs)
             for k in range(a, b):
                 gs[k] = (t, k - a, b - a)
             src, at = raw[a // 2]
@@ -116,11 +117,11 @@ def tile_hetxlhead_pa_v_kernel(
             return t[:], src[:, first : first + (b - a) * C // 2].rearrange("p (q u e) -> p u q e", u=2, e=RUN)
 
         def prescale(a, b):
-            dst, src = scale_views(a, b, "gs")
+            dst, src = scale_views(a, b, "gs", 3)
             nc.vector.tensor_scalar(out=dst, in0=src, scalar1=1.0 / TEMPERATURE, scalar2=None, op0=MULT)
 
         def scalar_prescale(a, b):
-            dst, src = scale_views(a, b, "gs_scalar")
+            dst, src = scale_views(a, b, "gs_scalar", 2)
             nc.scalar.activation(dst, src, mybir.ActivationFunctionType.Copy, scale=1.0 / TEMPERATURE)
 
         def turn(i):
@@ -172,8 +173,10 @@ def tile_hetxlhead_pa_v_kernel(
                 outb[0] = summing(0)
             g_pass(outb[0][:], i, h, i == 0 and h == 0, False)
 
-        def direct(samples):
-            for i in samples:
+        waiting = [i for i in range(2, S * TILES) if i % S or i // S not in KEPT and i // S < LAST]
+
+        def direct(count):
+            for i in [waiting.pop(0) for k in range(count)]:
                 J = i // S
                 opens = J not in outb
                 if opens:
@@ -191,10 +194,17 @@ def tile_hetxlhead_pa_v_kernel(
                 in1=t[:, at * D : (at + 1) * D], op=MULT,
             )
 
-        def add_pairs(J, eng=nc.gpsimd):
-            tag = "part" if J not in PAIRED else "wg0" if J == LAST - 1 else "grp%d" % ((2 * J + 3) % 4)
-            part[J] = sb(tag, [P, 2 * D], F32, 1)
-            eng.tensor_tensor(out=part[J][:], in0=prod[J][:, 0], in1=prod[J][:, 1], op=ADD)
+        def add_columns(J, eng, cols):
+            views = [ap.rearrange("p (k d) -> p k d", k=2)[:, :, cols] for ap in (part[J][:], prod[J][:, 0], prod[J][:, 1])]
+            eng.tensor_tensor(out=views[0], in0=views[1], in1=views[2], op=ADD)
+
+        def add_pairs(J):
+            part[J] = sb("wg0" if J == LAST - 1 else "grp%d" % ((2 * J + 3) % 4), [P, 2 * D], F32, 1)
+            add_columns(J, nc.gpsimd, slice(0, D if J - 2 in KEPT else SHORT))
+
+        def add_rest(J):
+            if J - 2 not in KEPT:
+                add_columns(J, nc.vector, slice(SHORT, D))
 
         def natural(ap, half):
             return ap.rearrange("p (h a u e) -> p h u a e", h=2, u=2, e=DZ_RUN)[:, half]
@@ -219,7 +229,7 @@ def tile_hetxlhead_pa_v_kernel(
             sig[J] = sb("sig", [P, D], F32, 3)
             nc.scalar.activation(whole_by_line(sig[J][:]), whole_natural(zt[J]), mybir.ActivationFunctionType.Sigmoid)
 
-        def make_dz(J, eng=nc.gpsimd):
+        def make_dz(J, eng=nc.vector):
             if J % 4 == 0:
                 dz[J // 4] = sb("dz", [P, 4, D], BF16, 2)
             eng.tensor_tensor(out=dz[J // 4][:, J % 4, :], in0=dstd[J][:], in1=sig[J][:], op=MULT)
@@ -256,7 +266,7 @@ def tile_hetxlhead_pa_v_kernel(
 
         def keep(J):
             res[J] = sb("res", [P, D], F32, 7)
-            nc.scalar.copy(out=res[J][:], in_=dpb[S * J + 3][:])
+            nc.scalar.copy(out=res[J][:], in_=dpb[S * J + (0 if J else 1)][:])
 
         def add_kept(J):
             nc.vector.tensor_tensor(out=res[J][:], in0=outb[J][:], in1=res[J][:], op=ADD)
@@ -321,26 +331,26 @@ def tile_hetxlhead_pa_v_kernel(
         load_g(6, 8)
         load_g(8, 10)
         load_g(10, 12)
-        load_z(0, 1)
         load_n(4, 8)
+        load_z(0, 1)
         load_g(12, 16)
         load_n(8, 12)
-        load_z(1, 1)
         wd_raw = load_sorted(w_diag, DZ_RUN)
         load_g(16, 20)
+        load_z(1, 1)
         load_n(12, 16)
-        load_z(2, 2)
-        ft_raw = [load_rows(features[0:512, :])]
         load_g(20, 24)
+        load_z(2, 2)
         load_n(16, 20)
-        ft_raw.append(load_rows(features[512:1024, :]))
         load_g(24, 28)
-        load_z(4, 2)
+        ft_raw = [load_rows(features[0:512, :])]
         load_n(20, 24)
         load_g(28, 32)
+        load_z(4, 2)
         load_n(24, 28)
-        load_z(6, 2)
+        ft_raw.append(load_rows(features[512:1024, :]))
         load_n(28, 32)
+        load_z(6, 2)
 
         on_vector, on_scalar = slice(0, VECTOR_COLUMNS), slice(VECTOR_COLUMNS, D)
         wg = [grouped_w(0), grouped_w(1)]
@@ -384,23 +394,16 @@ def tile_hetxlhead_pa_v_kernel(
         dpre(3)
         prescale(12, 16)
         times_noise(2)
-        scalar_prescale(18, 20)
         turn(6)
         turn(7)
         times_noise(3)
         empty_turn(6)
         empty_turn(7)
-        keep(0)
-        direct_half(1, 0)
-        direct_half(1, 1)
-        direct([2])
-        prescale(16, 18)
-        prescale(20, 24)
-        sigmoid(0)
+        direct(1)
+        prescale(16, 20)
         quant_g(4, 6)
-        add_pairs(0, nc.vector)
         quant_g(6, 8)
-        add_all(0)
+        prescale(20, 24)
 
         grouped = {}
         beside = [(wd_raw, wd, E4M3), (ft_raw[0], ft[0], E4M3), (ft_raw[1], ft[1], E4M3), (None, dzq[0], E5M2)]
@@ -417,73 +420,77 @@ def tile_hetxlhead_pa_v_kernel(
         def side_quant(k, cols=slice(0, D)):
             quant_w(beside[k][1], grouped[k], beside[k][2], cols)
 
-        for i in range(8, 12):
+        for i in range(8, 10):
             turn(i)
             empty_turn(i)
+        keep(0)
+        sigmoid(0)
         halves = {J: [] for J in range(1, LAST)}
-        halves[PAIRED[0]] = [0]
-        halves[LAST - 1] = [6, 7, 2, 3]
+        halves[2], halves[4], halves[5], halves[6] = [0, 1], [2], [3], [6, 7, 4, 5]
         for J in range(1, LAST):
             first = S * J
             more = J + 2 < TILES
-            if J - 1 in PAIRED:
-                add_pairs(J - 1)
-            else:
-                make_dz(J - 1)
-            split = 2 * S * (J + 2) + SCALAR_UNITS - 2 * len(halves[J])
-            if J - 1 in PAIRED:
-                sigmoid(J - 1)
-            for n in halves[J][:2]:
-                side_half(n)
-            if more:
+            add_pairs(J - 1)
+            units = SCALAR_UNITS - 2 * len(halves[J]) - (J in KEPT) - 2 * (J == 1) if more else 0
+            split = 2 * S * (J + 2) + units
+            if units and J >= 3:
                 scalar_prescale(2 * S * (J + 2), split)
-            if J not in PAIRED:
-                sigmoid(J)
             for i in range(first, first + S):
                 dpre(i)
                 times_noise(i)
-                if i == first and J >= 3:
+                if i == first and J in KEPT:
+                    keep(J)
+                if i == first and units and J < 3:
+                    scalar_prescale(2 * S * (J + 2), split)
+                if i == first and J - 3 in KEPT:
                     dz_pass(J - 3)
                     add_kept(J - 3)
                     store_out(J - 3)
-            if J in KEPT:
-                keep(J)
+            if J == 1:
+                for i in range(10, 12):
+                    turn(i)
+                    empty_turn(i)
+            if J > 1:
+                sigmoid(J - 1)
+            for n in halves[J][:2]:
+                side_half(n)
+            if J >= 3 and J - 3 not in KEPT:
+                dz_pass(J - 3)
+                empty_out(J - 3)
+                store_out(J - 3)
             if not more:
                 turn_dz(J - 2)
                 empty_dz(J - 2)
             for n in halves[J][2:]:
                 side_half(n)
-            direct(range(first - (J == LAST - 1), first + S - (J < LAST - 1)))
+            direct(DIRECT - 2 * (J == 1) + (J == 2) + 2 * (not more))
+            add_rest(J - 1)
             if more:
                 prescale(split, 2 * S * (J + 3))
-            if J - 1 in PAIRED:
-                add_all(J - 1)
-            elif J not in PAIRED:
-                add_pairs(J, nc.vector)
             else:
-                interleave(nc.vector.tensor_copy, grouped[0], wd_raw, right)
-            if J >= 2 and more:
-                turn_dz(J - 2)
-                empty_dz(J - 2)
+                quant_g(first + 4, first + 6)
+            add_all(J - 1)
             if more:
+                if J >= 2:
+                    turn_dz(J - 2)
+                    empty_dz(J - 2)
                 for i in range(first + 8, first + 12):
                     turn(i)
                     empty_turn(i)
-            quant_g(first + 4, first + 6)
-            if not more:
+                quant_g(first + 4, first + 6)
+            else:
                 quant_g(first + 6, first + 8)
+            if J == 2:
+                side_quant(0)
+            if not more:
+                side_quant(1)
             if J >= 2:
                 quant_dz(J - 2)
             if more:
                 quant_g(first + 6, first + 8)
             else:
                 side_quant(3)
-            if J - 1 in PAIRED:
-                make_dz(J - 1, nc.vector)
-            elif J not in PAIRED:
-                add_all(J)
-            else:
-                side_quant(0)
+            make_dz(J - 1)
 
         L = LAST
         last = {}
@@ -521,73 +528,77 @@ def tile_hetxlhead_pa_v_kernel(
 
         add_pairs(L - 1)
         sigmoid(L - 1)
-        side_half(4)
+        sigmoid(L)
+        res[L] = sb("kept", [P, D], F32, 1)
         last_dpre(0)
         dz_pass(L - 3)
         last_times_noise(0)
-        add_kept(L - 3)
+        empty_out(L - 3)
         store_out(L - 3)
         for m in range(1, 4):
             last_dpre(m)
             last_times_noise(m)
         turn_dz(L - 2)
-        empty_dz(L - 2)
-        sigmoid(L)
-        side_half(5)
-        direct(range(S * L, S * L + S - 1))
+        for m in range(4):
+            nc.scalar.copy(out=res[L][:, quarter[m]], in_=last[m][:, 0, :])
+            if m == 2:
+                empty_dz(L - 2)
+        direct(3)
         part[L] = sb("part", [P, 4, 2, P], F32, 1)
-        add_all(L - 1)
-        dstd[L] = sb("dstd", [P, D], F32, 2)
-        t = grouped_w(0)
+        add_rest(L - 1)
+        last_add_pairs(0)
         quant_dz(L - 2)
         dz_pass(L - 2)
         empty_out(L - 2)
         store_out(L - 2)
-        last_add_pairs(0)
-        make_dz(L - 1, nc.vector)
-        turn_dz(L - 1, bank_of["dz", L - 2])
-        empty_dz(L - 1)
-        direct([S * L + S - 1])
-        last_add_pairs(1)
-        last_add_all(0)
-        side_quant(1)
+        add_all(L - 1)
+        dstd[L] = sb("dstd", [P, D], F32, 2)
+        t = grouped_w(0)
         open_weight(0, bank_of["last", 0])
-        open_weight(1, bank_of["last", 1])
+        direct(1)
+        last_add_all(0)
+        make_dz(L - 1)
+        turn_dz(L - 1, bank_of["dz", L - 2])
         last_make_dz(0)
-        last_add_all(1)
         interleave_dz(nc.scalar.copy, t, dz[1], quarter[0])
+        empty_dz(L - 1)
+        direct(2)
+        open_weight(1, bank_of["last", 1])
+        last_add_pairs(1)
+        side_quant(2)
+        last_add_all(1)
+        last_add_pairs(2)
+        last_make_dz(1)
+        interleave_dz(nc.scalar.copy, t, dz[1], quarter[1])
         quant_dz(L - 1)
         dz_pass(L - 1)
-        open_weight(2, bank_of["last", 2])
-        open_weight(3, bank_of["last", 3])
-        last_make_dz(1)
-        last_add_pairs(2)
-        interleave_dz(nc.scalar.copy, t, dz[1], quarter[1])
-        side_quant(2)
         last_add_all(2)
         quant_w(dzq[1], t, E5M2, quarter[0])
         weight_pass(0, 1)
+        open_weight(2, bank_of["last", 2])
+        last_make_dz(2)
+        interleave_dz(nc.scalar.copy, t, dz[1], quarter[2])
         empty_out(L - 1)
         store_out(L - 1)
         last_add_pairs(3)
-        last_make_dz(2)
-        last_add_all(3)
         quant_w(dzq[1], t, E5M2, quarter[1])
+        last_add_all(3)
+        open_weight(3, bank_of["last", 3])
         weight_pass(1, 1)
         last_make_dz(3)
         turn_dz(L, bank_of["dz", L - 1])
-        store_weight(0, nc.scalar.copy)
-        interleave_dz(nc.vector.tensor_copy, t, dz[1], quarter[2])
-        interleave_dz(nc.vector.tensor_copy, t, dz[1], quarter[3])
         quant_w(dzq[1], t, E5M2, quarter[2])
         weight_pass(2, 1)
-        empty_dz(L, nc.vector.tensor_copy)
+        direct(len(waiting))
+        interleave_dz(nc.vector.tensor_copy, t, dz[1], quarter[3])
+        store_weight(0, nc.vector.tensor_copy)
+        store_weight(1, nc.scalar.copy)
         quant_w(dzq[1], t, E5M2, quarter[3])
         weight_pass(3, 1)
+        empty_dz(L, nc.vector.tensor_copy)
+        store_weight(2, nc.scalar.copy)
         quant_dz(L)
         dz_pass(L)
-        store_weight(1, nc.scalar.copy)
-        store_weight(2, nc.vector.tensor_copy)
         store_weight(3, nc.scalar.copy)
-        empty_out(L, nc.vector.tensor_copy)
+        add_kept(L)
         store_out(L)

@@ -82,7 +82,7 @@ def tile_hetxlhead_pa_v_kernel(
                 into[i] = (t, i - a)
 
         def load_g(a, b):
-            if b - a == 4:
+            if b - a >= 3:
                 load_samples(g_view, C, "raw", 3, raw, a, b)
             else:
                 load_samples(g_view, C, "raw_part", 5, raw, a, b)
@@ -199,7 +199,7 @@ def tile_hetxlhead_pa_v_kernel(
             eng.tensor_tensor(out=views[0], in0=views[1], in1=views[2], op=ADD)
 
         def add_pairs(J):
-            part[J] = sb("wg0" if J == LAST - 1 else "grp%d" % ((2 * J + 3) % 4), [P, 2 * D], F32, 1)
+            part[J] = sb("sums%d" % (J % 2) if J >= 2 else "grp%d" % ((2 * J + 2) % 4), [P, 2 * D], F32, 1)
             add_columns(J, nc.gpsimd, slice(0, D if J - 2 in KEPT else SHORT))
 
         def add_rest(J):
@@ -244,7 +244,7 @@ def tile_hetxlhead_pa_v_kernel(
                 nc.tensor.transpose(dzt_b[J][:, u, :], words[:, u * P : (u + 1) * P], ident[:])
 
         def empty_dz(J, copy=nc.scalar.copy):
-            dzt[J] = sb("dzt", [P, P, 2], F32, 2)
+            dzt[J] = sb("sums%d" % (J % 2), [P, P, 2], F32, 1)
             copy(out=dzt[J][:], in_=dzt_b[J][:].rearrange("p u r -> p r u"))
 
         def quant_dz(J):
@@ -261,11 +261,11 @@ def tile_hetxlhead_pa_v_kernel(
             )
 
         def empty_out(J, copy=nc.scalar.copy):
-            res[J] = sb("res", [P, D], F32, 7)
+            res[J] = sb("res", [P, D], F32, 6)
             copy(out=res[J][:], in_=outb[J][:])
 
         def keep(J):
-            res[J] = sb("res", [P, D], F32, 7)
+            res[J] = sb("res", [P, D], F32, 6)
             nc.scalar.copy(out=res[J][:], in_=dpb[S * J + (0 if J else 1)][:])
 
         def add_kept(J):
@@ -297,7 +297,7 @@ def tile_hetxlhead_pa_v_kernel(
             return sb("wg%d" % slot, [P, D, 4], BF16, 1)
 
         def store_weight(m, copy):
-            r = sb("res", [P, D], F32, 7)
+            r = sb("res", [P, D], F32, 6)
             copy(out=r[:], in_=acc[m][:])
             nc.sync.dma_start(out=out_1[quarter[m], :], in_=r[:])
 
@@ -325,15 +325,16 @@ def tile_hetxlhead_pa_v_kernel(
         load_g(1, 2)
         wc_raw.append(load_sorted(w_cls[512:1024, :], RUN))
         load_g(2, 4)
-        load_n(0, 2)
         load_g(4, 6)
+        load_n(0, 2)
         load_n(2, 4)
         load_g(6, 8)
         load_g(8, 10)
         load_g(10, 12)
         load_n(4, 8)
         load_z(0, 1)
-        load_g(12, 16)
+        load_g(12, 13)
+        load_g(13, 16)
         load_n(8, 12)
         wd_raw = load_sorted(w_diag, DZ_RUN)
         load_g(16, 20)
@@ -402,8 +403,8 @@ def tile_hetxlhead_pa_v_kernel(
         direct(1)
         prescale(16, 20)
         quant_g(4, 6)
-        quant_g(6, 8)
         prescale(20, 24)
+        quant_g(6, 8)
 
         grouped = {}
         beside = [(wd_raw, wd, E4M3), (ft_raw[0], ft[0], E4M3), (ft_raw[1], ft[1], E4M3), (None, dzq[0], E5M2)]
@@ -450,10 +451,10 @@ def tile_hetxlhead_pa_v_kernel(
                 for i in range(10, 12):
                     turn(i)
                     empty_turn(i)
-            if J > 1:
-                sigmoid(J - 1)
             for n in halves[J][:2]:
                 side_half(n)
+            if J > 1:
+                sigmoid(J - 1)
             if J >= 3 and J - 3 not in KEPT:
                 dz_pass(J - 3)
                 empty_out(J - 3)
@@ -483,13 +484,13 @@ def tile_hetxlhead_pa_v_kernel(
             if J == 2:
                 side_quant(0)
             if not more:
-                side_quant(1)
+                side_quant(3)
             if J >= 2:
                 quant_dz(J - 2)
             if more:
                 quant_g(first + 6, first + 8)
             else:
-                side_quant(3)
+                side_quant(1)
             make_dz(J - 1)
 
         L = LAST
@@ -544,7 +545,7 @@ def tile_hetxlhead_pa_v_kernel(
             if m == 2:
                 empty_dz(L - 2)
         direct(3)
-        part[L] = sb("part", [P, 4, 2, P], F32, 1)
+        part[L] = sb("grp0", [P, 4, 2, P], F32, 1)
         add_rest(L - 1)
         last_add_pairs(0)
         quant_dz(L - 2)

@@ -23,7 +23,7 @@ DZ_RUN = 4
 VECTOR_COLUMNS = 320
 WARM_UPS = 3
 UNITS = 8
-SCALAR_UNITS = 5
+SCALAR_UNITS = 4
 ROTATING, SUMS = 5, 3
 KEPT = range(0, 3)
 SHORT = 432
@@ -427,12 +427,12 @@ def tile_hetxlhead_pa_v_kernel(
         keep(0)
         sigmoid(0)
         halves = {J: [] for J in range(1, LAST)}
-        halves[2], halves[4], halves[5], halves[6] = [0, 1], [2], [3], [6, 7, 4, 5]
+        halves[2], halves[4], halves[5], halves[6] = [0, 1], [2], [3], [6, 7, 4]
         for J in range(1, LAST):
             first = S * J
             more = J + 2 < TILES
             add_pairs(J - 1)
-            units = SCALAR_UNITS - 2 * len(halves[J]) - (J in KEPT) - 2 * (J == 1) if more else 0
+            units = SCALAR_UNITS - 2 * len(halves[J]) - 2 * (J == 1) if more else 0
             split = 2 * S * (J + 2) + units
             if units and J >= 3:
                 scalar_prescale(2 * S * (J + 2), split)
@@ -455,13 +455,12 @@ def tile_hetxlhead_pa_v_kernel(
                 side_half(n)
             if J > 1:
                 sigmoid(J - 1)
-            if J >= 3 and J - 3 not in KEPT:
-                dz_pass(J - 3)
-                empty_out(J - 3)
-                store_out(J - 3)
             if not more:
+                dz_pass(J - 3)
                 turn_dz(J - 2)
                 empty_dz(J - 2)
+                empty_out(J - 3)
+                store_out(J - 3)
             for n in halves[J][2:]:
                 side_half(n)
             direct(DIRECT - 2 * (J == 1) + (J == 2) + 2 * (not more))
@@ -497,16 +496,19 @@ def tile_hetxlhead_pa_v_kernel(
         last = {}
         prod[L] = sb("prod", [P, 4, S, P], F32, 2)
 
-        def last_dpre(m):
-            last[m] = rotating(("last", m), [P, S, P])
-            for s in range(S):
+        def last_dpre(n):
+            last[n] = rotating(("last", n), [P, 2, D // 2])
+            for k in range(2):
                 for h in range(2):
-                    g_pass(last[m][:, s, :], S * L + s, h, h == 0, h == 1, quarter[m])
+                    g_pass(last[n][:, k, :], S * L + 2 * (n % 2) + k, h, h == 0, h == 1, (left, right)[n // 2])
 
-        def last_times_noise(m):
+        def last_times_noise(n):
+            half, samples = n // 2, slice(2 * (n % 2), 2 * (n % 2) + 2)
             nc.vector.tensor_tensor(
-                out=prod[L][:, m], in0=last[m][:],
-                in1=noise[S * L][0][:].rearrange("p (s d) -> p s d", s=S)[:, :, quarter[m]], op=MULT,
+                out=prod[L][:, 2 * half : 2 * half + 2, samples].rearrange("p m s c -> p s m c"),
+                in0=last[n][:].rearrange("p s (m c) -> p s m c", m=2),
+                in1=noise[S * L][0][:].rearrange("p (s m c) -> p s m c", s=S, c=P)[:, samples, 2 * half : 2 * half + 2],
+                op=MULT,
             )
 
         def last_add_pairs(m):
@@ -529,21 +531,21 @@ def tile_hetxlhead_pa_v_kernel(
 
         add_pairs(L - 1)
         sigmoid(L - 1)
-        sigmoid(L)
-        res[L] = sb("kept", [P, D], F32, 1)
+        side_half(5)
         last_dpre(0)
         dz_pass(L - 3)
         last_times_noise(0)
-        empty_out(L - 3)
-        store_out(L - 3)
         for m in range(1, 4):
             last_dpre(m)
             last_times_noise(m)
+        res[L] = sb("kept", [P, D], F32, 1)
+        for half in range(2):
+            nc.scalar.copy(out=res[L][:, (left, right)[half]], in_=last[2 * half][:, 0, :])
         turn_dz(L - 2)
-        for m in range(4):
-            nc.scalar.copy(out=res[L][:, quarter[m]], in_=last[m][:, 0, :])
-            if m == 2:
-                empty_dz(L - 2)
+        empty_dz(L - 2)
+        sigmoid(L)
+        empty_out(L - 3)
+        store_out(L - 3)
         direct(3)
         part[L] = sb("grp0", [P, 4, 2, P], F32, 1)
         add_rest(L - 1)
@@ -577,27 +579,27 @@ def tile_hetxlhead_pa_v_kernel(
         quant_w(dzq[1], t, E5M2, quarter[0])
         weight_pass(0, 1)
         open_weight(2, bank_of["last", 2])
-        last_make_dz(2)
-        interleave_dz(nc.scalar.copy, t, dz[1], quarter[2])
         empty_out(L - 1)
         store_out(L - 1)
+        store_weight(0, nc.scalar.copy)
+        last_make_dz(2)
         last_add_pairs(3)
         quant_w(dzq[1], t, E5M2, quarter[1])
         last_add_all(3)
         open_weight(3, bank_of["last", 3])
         weight_pass(1, 1)
+        store_weight(1, nc.scalar.copy)
+        interleave_dz(nc.vector.tensor_copy, t, dz[1], quarter[2])
         last_make_dz(3)
         turn_dz(L, bank_of["dz", L - 1])
         quant_w(dzq[1], t, E5M2, quarter[2])
         weight_pass(2, 1)
         direct(len(waiting))
         interleave_dz(nc.vector.tensor_copy, t, dz[1], quarter[3])
-        store_weight(0, nc.vector.tensor_copy)
-        store_weight(1, nc.scalar.copy)
+        store_weight(2, nc.scalar.copy)
         quant_w(dzq[1], t, E5M2, quarter[3])
         weight_pass(3, 1)
         empty_dz(L, nc.vector.tensor_copy)
-        store_weight(2, nc.scalar.copy)
         quant_dz(L)
         dz_pass(L)
         store_weight(3, nc.scalar.copy)

@@ -23,10 +23,10 @@ DZ_RUN = 4
 VECTOR_COLUMNS = 320
 WARM_UPS = 3
 UNITS = 8
-SCALAR_UNITS = 4
+SCALAR_UNITS = 5
 ROTATING, SUMS = 5, 3
 KEPT = range(0, 3)
-SHORT = 432
+SHORT = 400
 DIRECT = 3
 FLOPS = 2 * (B * S * C * D + B * D * D + D * D * B)
 BYTES = 2 * (B * S * C + B * S * D + B * D + D * D + C * D) + 4 * (B * D) + 4 * (B * D + D * D)
@@ -432,7 +432,7 @@ def tile_hetxlhead_pa_v_kernel(
             first = S * J
             more = J + 2 < TILES
             add_pairs(J - 1)
-            units = SCALAR_UNITS - 2 * len(halves[J]) - 2 * (J == 1) if more else 0
+            units = SCALAR_UNITS - 2 * len(halves[J]) - (J in KEPT) - 2 * (J == 1) if more else 0
             split = 2 * S * (J + 2) + units
             if units and J >= 3:
                 scalar_prescale(2 * S * (J + 2), split)
@@ -494,7 +494,7 @@ def tile_hetxlhead_pa_v_kernel(
 
         L = LAST
         last = {}
-        prod[L] = sb("prod", [P, 4, S, P], F32, 2)
+        prod[L] = sb("prod", [P, 2, 2 * D], F32, 2)
 
         def last_dpre(n):
             last[n] = rotating(("last", n), [P, 2, D // 2])
@@ -503,27 +503,22 @@ def tile_hetxlhead_pa_v_kernel(
                     g_pass(last[n][:, k, :], S * L + 2 * (n % 2) + k, h, h == 0, h == 1, (left, right)[n // 2])
 
         def last_times_noise(n):
-            half, samples = n // 2, slice(2 * (n % 2), 2 * (n % 2) + 2)
+            pair, cols = n % 2, (left, right)[n // 2]
             nc.vector.tensor_tensor(
-                out=prod[L][:, 2 * half : 2 * half + 2, samples].rearrange("p m s c -> p s m c"),
-                in0=last[n][:].rearrange("p s (m c) -> p s m c", m=2),
-                in1=noise[S * L][0][:].rearrange("p (s m c) -> p s m c", s=S, c=P)[:, samples, 2 * half : 2 * half + 2],
-                op=MULT,
+                out=prod[L][:, :, pair * D : (pair + 1) * D][:, :, cols], in0=last[n][:],
+                in1=noise[S * L][0][:].rearrange("p (s d) -> p s d", s=S)[:, 2 * pair : 2 * pair + 2, cols], op=MULT,
             )
 
-        def last_add_pairs(m):
-            nc.vector.tensor_tensor(out=part[L][:, m], in0=prod[L][:, m, 0:2], in1=prod[L][:, m, 2:4], op=ADD)
-
-        def lines(ap, m):
-            return whole_by_line(ap)[:, :, 16 * m : 16 * (m + 1)]
-
-        def last_add_all(m):
+        def last_add_all(half):
             nc.vector.tensor_tensor(
-                out=lines(dstd[L][:], m), in0=whole_natural(part[L][:, m, 0]), in1=whole_natural(part[L][:, m, 1]), op=ADD
+                out=by_line(dstd[L][:], half), in0=natural(part[L][:, 0:D], half),
+                in1=natural(part[L][:, D : 2 * D], half), op=ADD,
             )
 
-        def last_make_dz(m):
-            nc.vector.tensor_tensor(out=lines(dz[1][:, 3, :], m), in0=lines(dstd[L][:], m), in1=lines(sig[L][:], m), op=MULT)
+        def last_make_dz(half):
+            nc.vector.tensor_tensor(
+                out=by_line(dz[1][:, 3, :], half), in0=by_line(dstd[L][:], half), in1=by_line(sig[L][:], half), op=MULT
+            )
 
         def open_weight(m, bank):
             acc[m] = in_bank(bank, ("weight", m), [P, D])
@@ -535,9 +530,9 @@ def tile_hetxlhead_pa_v_kernel(
         last_dpre(0)
         dz_pass(L - 3)
         last_times_noise(0)
-        for m in range(1, 4):
-            last_dpre(m)
-            last_times_noise(m)
+        for n in range(1, 4):
+            last_dpre(n)
+            last_times_noise(n)
         res[L] = sb("kept", [P, D], F32, 1)
         for half in range(2):
             nc.scalar.copy(out=res[L][:, (left, right)[half]], in_=last[2 * half][:, 0, :])
@@ -547,9 +542,10 @@ def tile_hetxlhead_pa_v_kernel(
         empty_out(L - 3)
         store_out(L - 3)
         direct(3)
-        part[L] = sb("grp0", [P, 4, 2, P], F32, 1)
+        open_weight(2, bank_of["last", 1])
+        part[L] = sb("grp0", [P, 2 * D], F32, 1)
         add_rest(L - 1)
-        last_add_pairs(0)
+        add_columns(L, nc.vector, left)
         quant_dz(L - 2)
         dz_pass(L - 2)
         empty_out(L - 2)
@@ -559,49 +555,42 @@ def tile_hetxlhead_pa_v_kernel(
         t = grouped_w(0)
         open_weight(0, bank_of["last", 0])
         direct(1)
+        open_weight(3, bank_of["last", 3])
         last_add_all(0)
         make_dz(L - 1)
         turn_dz(L - 1, bank_of["dz", L - 2])
         last_make_dz(0)
         interleave_dz(nc.scalar.copy, t, dz[1], quarter[0])
         empty_dz(L - 1)
-        direct(2)
-        open_weight(1, bank_of["last", 1])
-        last_add_pairs(1)
-        side_quant(2)
-        last_add_all(1)
-        last_add_pairs(2)
-        last_make_dz(1)
         interleave_dz(nc.scalar.copy, t, dz[1], quarter[1])
-        quant_dz(L - 1)
-        dz_pass(L - 1)
-        last_add_all(2)
+        direct(2)
+        open_weight(1, bank_of["last", 2])
+        add_columns(L, nc.vector, right)
+        side_quant(2)
         quant_w(dzq[1], t, E5M2, quarter[0])
         weight_pass(0, 1)
-        open_weight(2, bank_of["last", 2])
+        store_weight(0, nc.scalar.copy)
+        last_add_all(1)
+        quant_dz(L - 1)
+        dz_pass(L - 1)
         empty_out(L - 1)
         store_out(L - 1)
-        store_weight(0, nc.scalar.copy)
-        last_make_dz(2)
-        last_add_pairs(3)
+        last_make_dz(1)
         quant_w(dzq[1], t, E5M2, quarter[1])
-        last_add_all(3)
-        open_weight(3, bank_of["last", 3])
+        turn_dz(L, bank_of["dz", L - 1])
         weight_pass(1, 1)
         store_weight(1, nc.scalar.copy)
         interleave_dz(nc.vector.tensor_copy, t, dz[1], quarter[2])
-        last_make_dz(3)
-        turn_dz(L, bank_of["dz", L - 1])
+        interleave_dz(nc.vector.tensor_copy, t, dz[1], quarter[3])
         quant_w(dzq[1], t, E5M2, quarter[2])
         weight_pass(2, 1)
         direct(len(waiting))
-        interleave_dz(nc.vector.tensor_copy, t, dz[1], quarter[3])
-        store_weight(2, nc.scalar.copy)
+        empty_dz(L, nc.vector.tensor_copy)
         quant_w(dzq[1], t, E5M2, quarter[3])
         weight_pass(3, 1)
-        empty_dz(L, nc.vector.tensor_copy)
         quant_dz(L)
         dz_pass(L)
+        store_weight(2, nc.vector.tensor_copy)
         store_weight(3, nc.scalar.copy)
         add_kept(L)
         store_out(L)

@@ -26,8 +26,8 @@ UNITS = 8
 SCALAR_UNITS = 5
 ROTATING, SUMS = 5, 3
 KEPT = range(0, 3)
-SHORT = 400
-DIRECT = 3
+SHORT = 416
+DIRECT = 6
 FLOPS = 2 * (B * S * C * D + B * D * D + D * D * B)
 BYTES = 2 * (B * S * C + B * S * D + B * D + D * D + C * D) + 4 * (B * D) + 4 * (B * D + D * D)
 
@@ -136,7 +136,7 @@ def tile_hetxlhead_pa_v_kernel(
         def empty_turn(i, count=2):
             at = i % count
             if at == 0:
-                t = sb("grp%d" % (i // 2 % 4 if count == 2 else 2 + i), [P, count, 2, P, 2], F32, 1)
+                t = sb("grp%d" % (i // 2 % 4 if count == 2 else (2 + i) % 4), [P, count, 2, P, 2], F32, 1)
                 for k in range(count):
                     grp[i + k] = t
             nc.scalar.copy(out=grp[i][:, at], in_=trb[i][:].rearrange("p h u r -> p h r u"))
@@ -173,16 +173,14 @@ def tile_hetxlhead_pa_v_kernel(
                 outb[0] = summing(0)
             g_pass(outb[0][:], i, h, i == 0 and h == 0, False)
 
-        waiting = [i for i in range(2, S * TILES) if i % S or i // S not in KEPT and i // S < LAST]
+        waiting = [(i, h) for i in range(2, S * TILES) if i % S or i // S not in KEPT and i // S < LAST for h in range(2)]
 
         def direct(count):
-            for i in [waiting.pop(0) for k in range(count)]:
-                J = i // S
-                opens = J not in outb
+            for i, h in [waiting.pop(0) for k in range(count)]:
+                opens = i // S not in outb
                 if opens:
-                    outb[J] = summing(J)
-                for h in range(2):
-                    g_pass(outb[J][:], i, h, opens and h == 0, False)
+                    outb[i // S] = summing(i // S)
+                g_pass(outb[i // S][:], i, h, opens, False)
 
         def times_noise(i):
             J, s = divmod(i, S)
@@ -324,7 +322,8 @@ def tile_hetxlhead_pa_v_kernel(
         wc_raw = [load_sorted(w_cls[0:512, :], RUN)]
         load_g(1, 2)
         wc_raw.append(load_sorted(w_cls[512:1024, :], RUN))
-        load_g(2, 4)
+        load_g(2, 3)
+        load_g(3, 4)
         load_g(4, 6)
         load_n(0, 2)
         load_n(2, 4)
@@ -332,9 +331,9 @@ def tile_hetxlhead_pa_v_kernel(
         load_g(8, 10)
         load_g(10, 12)
         load_n(4, 8)
-        load_z(0, 1)
         load_g(12, 13)
         load_g(13, 16)
+        load_z(0, 1)
         load_n(8, 12)
         wd_raw = load_sorted(w_diag, DZ_RUN)
         load_g(16, 20)
@@ -372,27 +371,29 @@ def tile_hetxlhead_pa_v_kernel(
         interleave(nc.vector.tensor_copy, wg[1], wc_raw[1], on_vector)
         interleave(nc.scalar.copy, wg[1], wc_raw[1], on_scalar)
         empty_turn(1, 1)
-        prescale(4, 8)
-        quant_w(wc[1], wg[1], E4M3)
-        quant_g(1, 2)
+        prescale(4, 6)
         turn(2)
-        turn(3)
+        empty_turn(2, 1)
+        quant_w(wc[1], wg[1], E4M3)
+        prescale(6, 8)
+        quant_g(1, 2)
         dpre_half(0, 1)
+        turn(3)
+        empty_turn(3, 1)
         dpre_half(1, 0)
         dpre_half(1, 1)
-        direct_half(0, 1)
-        empty_turn(2)
-        empty_turn(3)
         prescale(8, 12)
+        quant_g(2, 3)
         times_noise(0)
-        quant_g(2, 4)
+        dpre(2)
+        quant_g(3, 4)
         times_noise(1)
         turn(4)
         turn(5)
         empty_turn(4)
         empty_turn(5)
-        dpre(2)
         dpre(3)
+        direct_half(0, 1)
         prescale(12, 16)
         times_noise(2)
         turn(6)
@@ -400,7 +401,7 @@ def tile_hetxlhead_pa_v_kernel(
         times_noise(3)
         empty_turn(6)
         empty_turn(7)
-        direct(1)
+        direct(2)
         prescale(16, 20)
         quant_g(4, 6)
         prescale(20, 24)
@@ -425,7 +426,6 @@ def tile_hetxlhead_pa_v_kernel(
             turn(i)
             empty_turn(i)
         keep(0)
-        sigmoid(0)
         halves = {J: [] for J in range(1, LAST)}
         halves[2], halves[4], halves[5], halves[6] = [0, 1], [2], [3], [6, 7, 4]
         for J in range(1, LAST):
@@ -453,8 +453,7 @@ def tile_hetxlhead_pa_v_kernel(
                     empty_turn(i)
             for n in halves[J][:2]:
                 side_half(n)
-            if J > 1:
-                sigmoid(J - 1)
+            sigmoid(J - 1)
             if not more:
                 dz_pass(J - 3)
                 turn_dz(J - 2)
@@ -463,7 +462,7 @@ def tile_hetxlhead_pa_v_kernel(
                 store_out(J - 3)
             for n in halves[J][2:]:
                 side_half(n)
-            direct(DIRECT - 2 * (J == 1) + (J == 2) + 2 * (not more))
+            direct(DIRECT - 3 * (J == 1) + (J == 2) + 4 * (not more))
             add_rest(J - 1)
             if more:
                 prescale(split, 2 * S * (J + 3))
@@ -541,7 +540,7 @@ def tile_hetxlhead_pa_v_kernel(
         sigmoid(L)
         empty_out(L - 3)
         store_out(L - 3)
-        direct(3)
+        direct(6)
         open_weight(2, bank_of["last", 1])
         part[L] = sb("grp0", [P, 2 * D], F32, 1)
         add_rest(L - 1)
@@ -554,7 +553,7 @@ def tile_hetxlhead_pa_v_kernel(
         dstd[L] = sb("dstd", [P, D], F32, 2)
         t = grouped_w(0)
         open_weight(0, bank_of["last", 0])
-        direct(1)
+        direct(2)
         open_weight(3, bank_of["last", 3])
         last_add_all(0)
         make_dz(L - 1)
@@ -563,7 +562,7 @@ def tile_hetxlhead_pa_v_kernel(
         interleave_dz(nc.scalar.copy, t, dz[1], quarter[0])
         empty_dz(L - 1)
         interleave_dz(nc.scalar.copy, t, dz[1], quarter[1])
-        direct(2)
+        direct(4)
         open_weight(1, bank_of["last", 2])
         add_columns(L, nc.vector, right)
         side_quant(2)

@@ -26,7 +26,6 @@ UNITS = 8
 SCALAR_UNITS = 5
 ROTATING, SUMS = 5, 3
 KEPT = range(0, 3)
-SHORT = 416
 DIRECT = 6
 FLOPS = 2 * (B * S * C * D + B * D * D + D * D * B)
 BYTES = 2 * (B * S * C + B * S * D + B * D + D * D + C * D) + 4 * (B * D) + 4 * (B * D + D * D)
@@ -198,11 +197,7 @@ def tile_hetxlhead_pa_v_kernel(
 
         def add_pairs(J):
             part[J] = sb("sums%d" % (J % 2) if J >= 2 else "grp%d" % ((2 * J + 2) % 4), [P, 2 * D], F32, 1)
-            add_columns(J, nc.gpsimd, slice(0, D if J - 2 in KEPT else SHORT))
-
-        def add_rest(J):
-            if J - 2 not in KEPT:
-                add_columns(J, nc.vector, slice(SHORT, D))
+            add_columns(J, nc.gpsimd, slice(0, D))
 
         def natural(ap, half):
             return ap.rearrange("p (h a u e) -> p h u a e", h=2, u=2, e=DZ_RUN)[:, half]
@@ -463,7 +458,6 @@ def tile_hetxlhead_pa_v_kernel(
             for n in halves[J][2:]:
                 side_half(n)
             direct(DIRECT - 3 * (J == 1) + (J == 2) + 4 * (not more))
-            add_rest(J - 1)
             if more:
                 prescale(split, 2 * S * (J + 3))
             else:
@@ -543,7 +537,6 @@ def tile_hetxlhead_pa_v_kernel(
         direct(6)
         open_weight(2, bank_of["last", 1])
         part[L] = sb("grp0", [P, 2 * D], F32, 1)
-        add_rest(L - 1)
         add_columns(L, nc.vector, left)
         quant_dz(L - 2)
         dz_pass(L - 2)

@@ -26,7 +26,7 @@ UNITS = 8
 SCALAR_UNITS = 5
 ROTATING, SUMS = 5, 3
 KEPT = range(0, 3)
-DIRECT = 6
+DIRECT = 3
 FLOPS = 2 * (B * S * C * D + B * D * D + D * D * B)
 BYTES = 2 * (B * S * C + B * S * D + B * D + D * D + C * D) + 4 * (B * D) + 4 * (B * D + D * D)
 
@@ -172,14 +172,15 @@ def tile_hetxlhead_pa_v_kernel(
                 outb[0] = summing(0)
             g_pass(outb[0][:], i, h, i == 0 and h == 0, False)
 
-        waiting = [(i, h) for i in range(2, S * TILES) if i % S or i // S not in KEPT and i // S < LAST for h in range(2)]
+        waiting = [i for i in range(2, S * TILES) if i % S or i // S not in KEPT and i // S < LAST]
 
         def direct(count):
-            for i, h in [waiting.pop(0) for k in range(count)]:
+            for i in [waiting.pop(0) for k in range(count)]:
                 opens = i // S not in outb
                 if opens:
                     outb[i // S] = summing(i // S)
-                g_pass(outb[i // S][:], i, h, opens, False)
+                for h in range(2):
+                    g_pass(outb[i // S][:], i, h, opens and h == 0, False)
 
         def times_noise(i):
             J, s = divmod(i, S)
@@ -396,7 +397,7 @@ def tile_hetxlhead_pa_v_kernel(
         times_noise(3)
         empty_turn(6)
         empty_turn(7)
-        direct(2)
+        direct(1)
         prescale(16, 20)
         quant_g(4, 6)
         prescale(20, 24)
@@ -457,7 +458,7 @@ def tile_hetxlhead_pa_v_kernel(
                 store_out(J - 3)
             for n in halves[J][2:]:
                 side_half(n)
-            direct(DIRECT - 3 * (J == 1) + (J == 2) + 4 * (not more))
+            direct(DIRECT - 2 * (J == 1) + (J == 2) + 2 * (not more))
             if more:
                 prescale(split, 2 * S * (J + 3))
             else:
@@ -534,7 +535,7 @@ def tile_hetxlhead_pa_v_kernel(
         sigmoid(L)
         empty_out(L - 3)
         store_out(L - 3)
-        direct(6)
+        direct(3)
         open_weight(2, bank_of["last", 1])
         part[L] = sb("grp0", [P, 2 * D], F32, 1)
         add_columns(L, nc.vector, left)
@@ -546,7 +547,7 @@ def tile_hetxlhead_pa_v_kernel(
         dstd[L] = sb("dstd", [P, D], F32, 2)
         t = grouped_w(0)
         open_weight(0, bank_of["last", 0])
-        direct(2)
+        direct(1)
         open_weight(3, bank_of["last", 3])
         last_add_all(0)
         make_dz(L - 1)
@@ -555,8 +556,7 @@ def tile_hetxlhead_pa_v_kernel(
         interleave_dz(nc.scalar.copy, t, dz[1], quarter[0])
         empty_dz(L - 1)
         interleave_dz(nc.scalar.copy, t, dz[1], quarter[1])
-        direct(4)
-        open_weight(1, bank_of["last", 2])
+        direct(2)
         add_columns(L, nc.vector, right)
         side_quant(2)
         quant_w(dzq[1], t, E5M2, quarter[0])
@@ -565,6 +565,7 @@ def tile_hetxlhead_pa_v_kernel(
         last_add_all(1)
         quant_dz(L - 1)
         dz_pass(L - 1)
+        open_weight(1, bank_of["last", 2])
         empty_out(L - 1)
         store_out(L - 1)
         last_make_dz(1)

@@ -21,7 +21,6 @@ PAIRS = 2 * TILES
 RUN = 8
 DZ_RUN = 4
 VECTOR_COLUMNS = 320
-WARM_UPS = 3
 UNITS = 8
 SCALAR_UNITS = 5
 ROTATING, SUMS = 5, 3
@@ -352,9 +351,7 @@ def tile_hetxlhead_pa_v_kernel(
         wg = [grouped_w(0), grouped_w(1)]
         prescale(0, 2)
         turn(0)
-        unread = rotating("unread", [P, D])
-        for k in range(WARM_UPS):
-            nc.tensor.matmul(unread[:], lhsT=raw[0][0][:, 0:P], rhs=raw[0][0][:, 0:D], start=True, stop=True)
+        turns.append("skipped")
         interleave(nc.vector.tensor_copy, wg[0], wc_raw[0], on_vector)
         interleave(nc.scalar.copy, wg[0], wc_raw[0], on_scalar)
         empty_turn(0, 1)

from contextlib import ExitStack

import concourse.mybir as mybir
from concourse.masks import make_identity

F32 = mybir.dt.float32
BF16 = mybir.dt.bfloat16
U32 = mybir.dt.uint32
U8 = mybir.dt.uint8
E4M3 = mybir.dt.float8_e4m3fn_x4
E5M2 = mybir.dt.float8_e5m2_x4
MULT = mybir.AluOpType.mult
ADD = mybir.AluOpType.add

P = 128
B, S, D, C = 1024, 4, 512, 1024
TEMPERATURE = 1.5
TILES = B // P
LAST = TILES - 1
PAIRS = 2 * TILES
RUN = 8
DZ_RUN = 4
VECTOR_COLUMNS = 320
UNITS = 8
SCALAR_UNITS = 5
ROTATING, SUMS = 5, 3
KEPT = range(0, 3)
DIRECT = 3
FLOPS = 2 * (B * S * C * D + B * D * D + D * D * B)
BYTES = 2 * (B * S * C + B * S * D + B * D + D * D + C * D) + 4 * (B * D) + 4 * (B * D + D * D)


def tile_hetxlhead_pa_v_kernel(
    tc, features, w_diag, b_diag, w_cls, b_cls, noise_diag, lr_samples, z, grad_out, out_0, out_1
):
    nc = tc.nc
    g_view = grad_out.rearrange("(g p j) s c -> g p (j s c)", p=P, j=4)
    n_view = noise_diag.rearrange("(g p j) s d -> g p (j s d)", p=P, j=4)
    z_view = z.rearrange("(g p j) d -> g p j d", p=P, j=4)
    o_view = out_0.rearrange("(g p j) d -> g j p d", p=P, j=4)

    with ExitStack() as ctx:
        pool = ctx.enter_context(tc.tile_pool(name="sbuf", bufs=1))
        psum = ctx.enter_context(tc.psum_pool(name="psum", bufs=1))

        def sb(tag, shape, dtype, bufs, align=64):
            return pool.tile(shape, dtype, name=tag, tag=tag, bufs=bufs, align_bytes=align)

        turns, bank_of = [], {}

        def in_bank(k, key, shape):
            bank_of[key] = k
            return psum.tile(shape, F32, name="bank%d" % k, tag="bank%d" % k, bufs=1)

        def rotating(key, shape):
            turns.append(key)
            return in_bank((len(turns) - 1) % ROTATING, key, shape)

        def summing(J):
            return in_bank(ROTATING + J % SUMS, ("sum", J), [P, D])

        ident = sb("ident", [P, P], F32, 1)
        make_identity(nc, ident[:])

        raw, noise, zt, gs, trb, grp, cod, dpb = {}, {}, {}, {}, {}, {}, {}, {}
        prod, part, dstd, sig, dz, dzt_b, dzt, dzc, outb, res, acc = {}, {}, {}, {}, {}, {}, {}, {}, {}, {}, {}

        def quantised(tag, cols, bufs):
            return sb(tag + "_c", [P, cols], U32, bufs, 256), sb(tag + "_s", [P, cols], U8, bufs, 256)

        def load_samples(view, width, tag, bufs, into, a, b):
            t = sb(tag, [P, (b - a) * width], BF16, bufs)
            cuts = [a] + [i for i in range(a + 1, b) if i % 16 == 0] + [b]
            for lo, hi in zip(cuts, cuts[1:]):
                nc.sync.dma_start(
                    out=t[:, (lo - a) * width : (hi - a) * width],
                    in_=view[lo // 16][:, (lo % 16) * width : ((hi - 1) % 16 + 1) * width],
                )
            for i in range(a, b):
                into[i] = (t, i - a)

        def load_g(a, b):
            if b - a >= 3:
                load_samples(g_view, C, "raw", 3, raw, a, b)
            else:
                load_samples(g_view, C, "raw_part", 5, raw, a, b)

        def load_n(a, b):
            load_samples(n_view, D, "noise", 4, noise, a, b)

        def load_z(J, count):
            t = sb("z", [P, count, D], F32, 2)
            nc.sync.dma_start(out=t[:], in_=z_view[J // 4][:, J % 4 : J % 4 + count])
            for k in range(count):
                zt[J + k] = t[:, k, :]

        def load_rows(src):
            t = sb("wraw", [P, 4, D], BF16, 3)
            nc.sync.dma_start(out=t[:], in_=src.rearrange("(p j) w -> p j w", j=4))
            return t

        def load_sorted(src, run):
            t = sb("wraw", [P, 4, D], BF16, 3)
            rows = src.rearrange("(a u b e) w -> u a b (e w)", u=2, b=run // 2, e=2)
            for u in range(2):
                nc.sync.dma_start(out=t[:, 2 * u : 2 * u + 2, :].rearrange("p e w -> p (e w)"), in_=rows[u])
            return t

        def scale_views(a, b, tag, bufs):
            t = sb(tag, [P, 2, 2 * P * (b - a) // RUN, RUN], BF16, bufs)
            for k in range(a, b):
                gs[k] = (t, k - a, b - a)
            src, at = raw[a // 2]
            first = C * at + (a % 2) * C // 2
            return t[:], src[:, first : first + (b - a) * C // 2].rearrange("p (q u e) -> p u q e", u=2, e=RUN)

        def prescale(a, b):
            dst, src = scale_views(a, b, "gs", 3)
            nc.vector.tensor_scalar(out=dst, in0=src, scalar1=1.0 / TEMPERATURE, scalar2=None, op0=MULT)

        def scalar_prescale(a, b):
            dst, src = scale_views(a, b, "gs_scalar", 2)
            nc.scalar.activation(dst, src, mybir.ActivationFunctionType.Copy, scale=1.0 / TEMPERATURE)

        def turn(i):
            trb[i] = rotating(("turn", i), [P, 2, 2, P])
            for h in range(2):
                t, at, count = gs[2 * i + h]
                words = t[:].rearrange("p u q e -> p (u q e)").bitcast(F32)
                for u in range(2):
                    a = (u * count + at) * P
                    nc.tensor.transpose(trb[i][:, h, u, :], words[:, a : a + P], ident[:])

        def empty_turn(i, count=2):
            at = i % count
            if at == 0:
                t = sb("grp%d" % (i // 2 % 4 if count == 2 else (2 + i) % 4), [P, count, 2, P, 2], F32, 1)
                for k in range(count):
                    grp[i + k] = t
            nc.scalar.copy(out=grp[i][:, at], in_=trb[i][:].rearrange("p h u r -> p h r u"))

        def quant_g(a, b):
            codes, scales = quantised("g", 256 * (b - a), 6)
            nc.vector.quantize_mx(
                out=codes[:].bitcast(E5M2), scales=scales[:],
                in_=grp[a][:].rearrange("p s h r u -> p (s h r u)").bitcast(BF16),
            )
            for i in range(a, b):
                cod[i] = (codes, scales, i - a)

        def g_pass(out, i, h, start, stop, moving=slice(0, D)):
            codes, scales, at = cod[i]
            cols = slice((at * 2 + h) * P, (at * 2 + h + 1) * P)
            nc.tensor.matmul_mx(
                out=out, lhsT=codes[:, cols].bitcast(E5M2), lhsT_scale=scales[:, cols],
                rhs=wc[h][0][:, moving].bitcast(E4M3), rhs_scale=wc[h][1][:, moving], start=start, stop=stop,
            )

        def dpre(i):
            dpb[i] = rotating(("dpre", i), [P, D])
            for h in range(2):
                g_pass(dpb[i][:], i, h, h == 0, h == 1)

        def dpre_half(i, h):
            if h == 0:
                dpb[i] = in_bank(ROTATING + 1 + i, ("dpre", i), [P, D])
            g_pass(dpb[i][:], i, h, h == 0, h == 1)

        def direct_half(i, h):
            if i == 0 and h == 0:
                outb[0] = summing(0)
            g_pass(outb[0][:], i, h, i == 0 and h == 0, False)

        waiting = [i for i in range(2, S * TILES) if i % S or i // S not in KEPT and i // S < LAST]

        def direct(count):
            for i in [waiting.pop(0) for k in range(count)]:
                opens = i // S not in outb
                if opens:
                    outb[i // S] = summing(i // S)
                for h in range(2):
                    g_pass(outb[i // S][:], i, h, opens and h == 0, False)

        def times_noise(i):
            J, s = divmod(i, S)
            if s == 0:
                prod[J] = sb("prod", [P, 2, 2 * D], F32, 2)
            t, at = noise[i]
            nc.vector.tensor_tensor(
                out=prod[J][:, s % 2, (s // 2) * D : (s // 2 + 1) * D], in0=dpb[i][:],
                in1=t[:, at * D : (at + 1) * D], op=MULT,
            )

        def add_columns(J, eng, cols):
            views = [ap.rearrange("p (k d) -> p k d", k=2)[:, :, cols] for ap in (part[J][:], prod[J][:, 0], prod[J][:, 1])]
            eng.tensor_tensor(out=views[0], in0=views[1], in1=views[2], op=ADD)

        def add_pairs(J):
            part[J] = sb("sums%d" % (J % 2) if J >= 2 else "grp%d" % ((2 * J + 2) % 4), [P, 2 * D], F32, 1)
            add_columns(J, nc.gpsimd, slice(0, D))

        def natural(ap, half):
            return ap.rearrange("p (h a u e) -> p h u a e", h=2, u=2, e=DZ_RUN)[:, half]

        def by_line(ap, half):
            return ap.rearrange("p (u h a e) -> p h u a e", h=2, u=2, e=DZ_RUN)[:, half]

        def whole_natural(ap):
            return ap.rearrange("p (a u e) -> p u a e", u=2, e=DZ_RUN)

        def whole_by_line(ap):
            return ap.rearrange("p (u a e) -> p u a e", u=2, e=DZ_RUN)

        def add_all(J):
            dstd[J] = sb("dstd", [P, D], F32, 2)
            nc.vector.tensor_tensor(
                out=whole_by_line(dstd[J][:]), in0=whole_natural(part[J][:, 0:D]),
                in1=whole_natural(part[J][:, D : 2 * D]), op=ADD,
            )

        def sigmoid(J):
            sig[J] = sb("sig", [P, D], F32, 3)
            nc.scalar.activation(whole_by_line(sig[J][:]), whole_natural(zt[J]), mybir.ActivationFunctionType.Sigmoid)

        def make_dz(J, eng=nc.vector):
            if J % 4 == 0:
                dz[J // 4] = sb("dz", [P, 4, D], BF16, 2)
            eng.tensor_tensor(out=dz[J // 4][:, J % 4, :], in0=dstd[J][:], in1=sig[J][:], op=MULT)

        def turn_dz(J, bank=None):
            if bank is None:
                dzt_b[J] = rotating(("dz", J), [P, 2, P])
            else:
                dzt_b[J] = in_bank(bank, ("dz", J), [P, 2, P])
            words = dz[J // 4][:, J % 4, :].bitcast(F32)
            for u in range(2):
                nc.tensor.transpose(dzt_b[J][:, u, :], words[:, u * P : (u + 1) * P], ident[:])

        def empty_dz(J, copy=nc.scalar.copy):
            dzt[J] = sb("sums%d" % (J % 2), [P, P, 2], F32, 1)
            copy(out=dzt[J][:], in_=dzt_b[J][:].rearrange("p u r -> p r u"))

        def quant_dz(J):
            dzc[J] = quantised("dzt", P, 2)
            nc.vector.quantize_mx(
                out=dzc[J][0][:].bitcast(E5M2), scales=dzc[J][1][:],
                in_=dzt[J][:].rearrange("p r u -> p (r u)").bitcast(BF16),
            )

        def dz_pass(J):
            nc.tensor.matmul_mx(
                out=outb[J][:], lhsT=dzc[J][0][:].bitcast(E5M2), lhsT_scale=dzc[J][1][:],
                rhs=wd[0][:].bitcast(E4M3), rhs_scale=wd[1][:], start=False, stop=True,
            )

        def empty_out(J, copy=nc.scalar.copy):
            res[J] = sb("res", [P, D], F32, 6)
            copy(out=res[J][:], in_=outb[J][:])

        def keep(J):
            res[J] = sb("res", [P, D], F32, 6)
            nc.scalar.copy(out=res[J][:], in_=dpb[S * J + (0 if J else 1)][:])

        def add_kept(J):
            nc.vector.tensor_tensor(out=res[J][:], in0=outb[J][:], in1=res[J][:], op=ADD)

        def store_out(J):
            nc.sync.dma_start(out=o_view[J // 4, J % 4], in_=res[J][:])

        def interleave(copy, dst, src, cols):
            copy(
                out=dst[:, cols, :].rearrange("p (c i) j -> p c j i", i=4),
                in_=src[:, :, cols].rearrange("p j (c i) -> p c j i", i=4),
            )

        def interleave_dz(copy, dst, src, cols):
            lines = slice(cols.start // (2 * DZ_RUN), cols.stop // (2 * DZ_RUN))
            copy(
                out=dst[:].rearrange("p (a u e) j -> p u a j e", u=2, e=DZ_RUN)[:, :, lines],
                in_=src[:].rearrange("p j (u a e) -> p u a j e", u=2, e=DZ_RUN)[:, :, lines],
            )

        def quant_w(pair, t, fmt, cols=slice(0, D)):
            nc.vector.quantize_mx(
                out=pair[0][:, cols].bitcast(fmt), scales=pair[1][:, cols],
                in_=t[:, cols, :].rearrange("p w j -> p (w j)"),
            )

        def grouped_w(slot):
            return sb("wg%d" % slot, [P, D, 4], BF16, 1)

        def store_weight(m, copy):
            r = sb("res", [P, D], F32, 6)
            copy(out=r[:], in_=acc[m][:])
            nc.sync.dma_start(out=out_1[quarter[m], :], in_=r[:])

        def weight_pass(m, g):
            cols = quarter[m]
            nc.tensor.matmul_mx(
                out=acc[m][:], lhsT=dzq[g][0][:, cols].bitcast(E5M2), lhsT_scale=dzq[g][1][:, cols],
                rhs=ft[g][0][:].bitcast(E4M3), rhs_scale=ft[g][1][:], start=g == 0, stop=g == 1,
            )

        wc = [quantised("wc0", D, 1), quantised("wc1", D, 1)]
        wd = quantised("wd", D, 1)
        ft = [quantised("ft0", D, 1), quantised("ft1", D, 1)]
        dzq = [quantised("dz0", D, 1), quantised("dz1", D, 1)]
        left, right = slice(0, D // 2), slice(D // 2, D)
        quarter = [slice(m * P, (m + 1) * P) for m in range(4)]
        ctx.enter_context(tc.manual_schedule())

        dummy = sb("dummy", [P, 1], F32, 1)
        nc.vector.memset(dummy[:], 0.0)
        nc.scalar.activation(dummy[:], dummy[:], mybir.ActivationFunctionType.Sigmoid)

        load_g(0, 1)
        wc_raw = [load_sorted(w_cls[0:512, :], RUN)]
        load_g(1, 2)
        wc_raw.append(load_sorted(w_cls[512:1024, :], RUN))
        load_g(2, 3)
        load_g(3, 4)
        load_g(4, 6)
        load_n(0, 2)
        load_n(2, 4)
        load_g(6, 8)
        load_g(8, 10)
        load_g(10, 12)
        load_n(4, 8)
        load_g(12, 13)
        load_g(13, 16)
        load_z(0, 1)
        load_n(8, 12)
        wd_raw = load_sorted(w_diag, DZ_RUN)
        load_g(16, 20)
        load_z(1, 1)
        load_n(12, 16)
        load_g(20, 24)
        load_z(2, 2)
        load_n(16, 20)
        load_g(24, 28)
        ft_raw = [load_rows(features[0:512, :])]
        load_n(20, 24)
        load_g(28, 32)
        load_z(4, 2)
        load_n(24, 28)
        ft_raw.append(load_rows(features[512:1024, :]))
        load_n(28, 32)
        load_z(6, 2)

        on_vector, on_scalar = slice(0, VECTOR_COLUMNS), slice(VECTOR_COLUMNS, D)
        wg = [grouped_w(0), grouped_w(1)]
        prescale(0, 2)
        turn(0)
        turns.append("skipped")
        interleave(nc.vector.tensor_copy, wg[0], wc_raw[0], on_vector)
        interleave(nc.scalar.copy, wg[0], wc_raw[0], on_scalar)
        empty_turn(0, 1)
        prescale(2, 4)
        turn(1)
        quant_w(wc[0], wg[0], E4M3)
        quant_g(0, 1)
        dpre_half(0, 0)
        direct_half(0, 0)
        interleave(nc.vector.tensor_copy, wg[1], wc_raw[1], on_vector)
        interleave(nc.scalar.copy, wg[1], wc_raw[1], on_scalar)
        empty_turn(1, 1)
        prescale(4, 6)
        turn(2)
        empty_turn(2, 1)
        quant_w(wc[1], wg[1], E4M3)
        prescale(6, 8)
        quant_g(1, 2)
        dpre_half(0, 1)
        turn(3)
        empty_turn(3, 1)
        dpre_half(1, 0)
        dpre_half(1, 1)
        prescale(8, 12)
        quant_g(2, 3)
        times_noise(0)
        dpre(2)
        quant_g(3, 4)
        times_noise(1)
        turn(4)
        turn(5)
        empty_turn(4)
        empty_turn(5)
        dpre(3)
        direct_half(0, 1)
        prescale(12, 16)
        times_noise(2)
        turn(6)
        turn(7)
        times_noise(3)
        empty_turn(6)
        empty_turn(7)
        direct(1)
        prescale(16, 20)
        quant_g(4, 6)
        prescale(20, 24)
        quant_g(6, 8)

        grouped = {}
        beside = [(wd_raw, wd, E4M3), (ft_raw[0], ft[0], E4M3), (ft_raw[1], ft[1], E4M3), (None, dzq[0], E5M2)]

        def side_half(n):
            k, cols = n // 2, (left, right)[n % 2]
            if n % 2 == 0:
                grouped[k] = grouped_w(k % 3)
            if beside[k][0] is None:
                interleave_dz(nc.scalar.copy, grouped[k], dz[0], cols)
            else:
                interleave(nc.scalar.copy, grouped[k], beside[k][0], cols)

        def side_quant(k, cols=slice(0, D)):
            quant_w(beside[k][1], grouped[k], beside[k][2], cols)

        for i in range(8, 10):
            turn(i)
            empty_turn(i)
        keep(0)
        halves = {J: [] for J in range(1, LAST)}
        halves[2], halves[4], halves[5], halves[6] = [0, 1], [2], [3], [6, 7, 4]
        for J in range(1, LAST):
            first = S * J
            more = J + 2 < TILES
            add_pairs(J - 1)
            units = SCALAR_UNITS - 2 * len(halves[J]) - (J in KEPT) - 2 * (J == 1) if more else 0
            split = 2 * S * (J + 2) + units
            if units and J >= 3:
                scalar_prescale(2 * S * (J + 2), split)
            for i in range(first, first + S):
                dpre(i)
                times_noise(i)
                if i == first and J in KEPT:
                    keep(J)
                if i == first and units and J < 3:
                    scalar_prescale(2 * S * (J + 2), split)
                if i == first and J - 3 in KEPT:
                    dz_pass(J - 3)
                    add_kept(J - 3)
                    store_out(J - 3)
            if J == 1:
                for i in range(10, 12):
                    turn(i)
                    empty_turn(i)
            for n in halves[J][:2]:
                side_half(n)
            sigmoid(J - 1)
            if not more:
                dz_pass(J - 3)
                turn_dz(J - 2)
                empty_dz(J - 2)
                empty_out(J - 3)
                store_out(J - 3)
            for n in halves[J][2:]:
                side_half(n)
            direct(DIRECT - 2 * (J == 1) + (J == 2) + 2 * (not more))
            if more:
                prescale(split, 2 * S * (J + 3))
            else:
                quant_g(first + 4, first + 6)
            add_all(J - 1)
            if more:
                if J >= 2:
                    turn_dz(J - 2)
                    empty_dz(J - 2)
                for i in range(first + 8, first + 12):
                    turn(i)
                    empty_turn(i)
                quant_g(first + 4, first + 6)
            else:
                quant_g(first + 6, first + 8)
            if J == 2:
                side_quant(0)
            if not more:
                side_quant(3)
            if J >= 2:
                quant_dz(J - 2)
            if more:
                quant_g(first + 6, first + 8)
            else:
                side_quant(1)
            make_dz(J - 1)

        L = LAST
        last = {}
        prod[L] = sb("prod", [P, 2, 2 * D], F32, 2)

        def last_dpre(n):
            last[n] = rotating(("last", n), [P, 2, D // 2])
            for k in range(2):
                for h in range(2):
                    g_pass(last[n][:, k, :], S * L + 2 * (n % 2) + k, h, h == 0, h == 1, (left, right)[n // 2])

        def last_times_noise(n):
            pair, cols = n % 2, (left, right)[n // 2]
            nc.vector.tensor_tensor(
                out=prod[L][:, :, pair * D : (pair + 1) * D][:, :, cols], in0=last[n][:],
                in1=noise[S * L][0][:].rearrange("p (s d) -> p s d", s=S)[:, 2 * pair : 2 * pair + 2, cols], op=MULT,
            )

        def last_add_all(half):
            nc.vector.tensor_tensor(
                out=by_line(dstd[L][:], half), in0=natural(part[L][:, 0:D], half),
                in1=natural(part[L][:, D : 2 * D], half), op=ADD,
            )

        def last_make_dz(half):
            nc.vector.tensor_tensor(
                out=by_line(dz[1][:, 3, :], half), in0=by_line(dstd[L][:], half), in1=by_line(sig[L][:], half), op=MULT
            )

        def open_weight(m, bank):
            acc[m] = in_bank(bank, ("weight", m), [P, D])
            weight_pass(m, 0)

        add_pairs(L - 1)
        sigmoid(L - 1)
        side_half(5)
        last_dpre(0)
        dz_pass(L - 3)
        last_times_noise(0)
        for n in range(1, 4):
            last_dpre(n)
            last_times_noise(n)
        res[L] = sb("kept", [P, D], F32, 1)
        for half in range(2):
            nc.scalar.copy(out=res[L][:, (left, right)[half]], in_=last[2 * half][:, 0, :])
        turn_dz(L - 2)
        empty_dz(L - 2)
        sigmoid(L)
        empty_out(L - 3)
        store_out(L - 3)
        direct(3)
        open_weight(2, bank_of["last", 1])
        part[L] = sb("grp0", [P, 2 * D], F32, 1)
        add_columns(L, nc.vector, left)
        quant_dz(L - 2)
        dz_pass(L - 2)
        empty_out(L - 2)
        store_out(L - 2)
        add_all(L - 1)
        dstd[L] = sb("dstd", [P, D], F32, 2)
        t = grouped_w(0)
        open_weight(0, bank_of["last", 0])
        direct(1)
        open_weight(3, bank_of["last", 3])
        last_add_all(0)
        make_dz(L - 1)
        turn_dz(L - 1, bank_of["dz", L - 2])
        last_make_dz(0)
        interleave_dz(nc.scalar.copy, t, dz[1], quarter[0])
        empty_dz(L - 1)
        interleave_dz(nc.scalar.copy, t, dz[1], quarter[1])
        direct(2)
        add_columns(L, nc.vector, right)
        side_quant(2)
        quant_w(dzq[1], t, E5M2, quarter[0])
        weight_pass(0, 1)
        store_weight(0, nc.scalar.copy)
        last_add_all(1)
        quant_dz(L - 1)
        dz_pass(L - 1)
        open_weight(1, bank_of["last", 2])
        empty_out(L - 1)
        store_out(L - 1)
        last_make_dz(1)
        quant_w(dzq[1], t, E5M2, quarter[1])
        turn_dz(L, bank_of["dz", L - 1])
        weight_pass(1, 1)
        store_weight(1, nc.scalar.copy)
        interleave_dz(nc.vector.tensor_copy, t, dz[1], quarter[2])
        interleave_dz(nc.vector.tensor_copy, t, dz[1], quarter[3])
        quant_w(dzq[1], t, E5M2, quarter[2])
        weight_pass(2, 1)
        direct(len(waiting))
        empty_dz(L, nc.vector.tensor_copy)
        quant_w(dzq[1], t, E5M2, quarter[3])
        weight_pass(3, 1)
        quant_dz(L)
        dz_pass(L)
        store_weight(2, nc.vector.tensor_copy)
        store_weight(3, nc.scalar.copy)
        add_kept(L)
        store_out(L)
